import numpy as np
import ml_dtypes


def mxq(x, axis, fmt="e4m3"):
    dtype, down = {"e4m3": (ml_dtypes.float8_e4m3fn, 7), "e5m2": (ml_dtypes.float8_e5m2, 14)}[fmt]
    v = np.moveaxis(np.asarray(x, np.float32).astype(ml_dtypes.bfloat16).astype(np.float64), axis, -1)
    blocks = v.reshape(v.shape[:-1] + (-1, 32))
    amax = np.abs(blocks).max(-1, keepdims=True)
    byte = np.maximum(np.where(amax > 0, np.frexp(amax)[1] - 1 + 127, 0) - down, 1)
    scale = np.exp2(byte - 127.0)
    codes = (blocks / scale).astype(np.float32).astype(dtype).astype(np.float64)
    return np.moveaxis((codes * scale).reshape(v.shape), -1, axis)


WIDE = False


def mx_kscale(k):
    if not WIDE:
        return np.ones(k)
    levels = np.array([10, -10, 5, -5, 0])
    if k % 512:
        return np.exp2(np.random.permutation(np.resize(levels, k // 32))).repeat(32)
    a = np.empty((k // 512, 16))
    for p in range(k // 512):
        a[p, :8] = np.random.permutation(np.resize(levels, 8))
        for g in range(8):
            far = levels[np.abs(levels - a[p, g]) >= 10]
            a[p, g + 8] = far[np.random.randint(len(far))]
    return np.exp2(a.ravel()).repeat(32)


BF16 = ml_dtypes.bfloat16


def bf(x):
    return np.asarray(x, np.float32).astype(BF16)


def f64(x):
    return np.asarray(x).astype(np.float64)


B, S, D, DV, NS, SD = 4, 1024, 1024, 512, 2, 128
R = B * S


def silu(v):
    return v / (1.0 + np.exp(-v))


def draw0():
    s, r, t = mx_kscale(D), mx_kscale(D), mx_kscale(DV)
    return {"x": bf(np.random.standard_normal((B, S, D)) * r),
            "h": bf(np.random.standard_normal((B, S, D)) * s),
            "Wv": bf(np.random.standard_normal((NS, DV, D)) / np.sqrt(D) * t[:, None] / s),
            "W1": bf(np.random.standard_normal((NS, SD, D + DV)) / np.sqrt(D + DV) / np.concatenate([r, t]))}


def core(x, h, Wv, W1):
    xf = f64(x).reshape(R, D)
    hf = f64(h).reshape(R, D)
    w1 = f64(W1)
    views = mxq(hf, 1, "e4m3") @ mxq(f64(Wv).transpose(0, 2, 1), 1, "e4m3")
    a = mxq(xf, 1, "e4m3") @ mxq(w1[:, :, :D].transpose(0, 2, 1), 1, "e4m3")
    b = mxq(views, 2, "e4m3") @ mxq(w1[:, :, D:].transpose(0, 2, 1), 1, "e4m3")
    return silu(a + b).reshape(NS, B, S, SD)


def e4m3fn_bytes(y):
    return np.clip(np.asarray(y, np.float64), -448.0, 448.0).astype(np.float32).astype(ml_dtypes.float8_e4m3fn).view(np.uint8)


def e4m3fn_values(b):
    return np.asarray(b, np.uint8).view(ml_dtypes.float8_e4m3fn).astype(np.float64)


def setup_inputs():
    d = draw0()
    x0 = np.asarray(d['x']).astype(np.float64)
    s = (np.max(np.abs(x0), axis=(0, 1), keepdims=True) / 448.0).astype(np.float32)
    out = {}
    for k, v in d.items():
        if k == 'x':
            out['x_bytes'] = e4m3fn_bytes(x0 / s.astype(np.float64))
            out['x_scale'] = s
        else:
            out[k] = v
    return out


def reference(x_bytes, x_scale, h, Wv, W1):
    return core(e4m3fn_values(x_bytes) * x_scale.astype(np.float64), h, Wv, W1)

@@ -1,0 +1,462 @@
+from contextlib import ExitStack
+
+import concourse.mybir as mybir
+from concourse.masks import make_identity
+
+FLOPS = 2 * 4096 * 1024 * 1024 + 2 * 4096 * 256 * 1536
+
+F32 = mybir.dt.float32
+BF16 = mybir.dt.bfloat16
+U32 = mybir.dt.uint32
+U8 = mybir.dt.uint8
+F8 = mybir.dt.float8_e4m3fn
+X4 = mybir.dt.float8_e4m3fn_x4
+MULT = mybir.AluOpType.mult
+ACT = mybir.ActivationFunctionType
+
+P = 128
+D = 1024
+NS = 2
+STEPS = 16
+APART = ()
+SORT_V = ()
+SORT_S = ()
+
+
+def tile_distributedb_pa_t_kernel(tc, x_bytes, x_scale, h, Wv, W1, out):
+    nc = tc.nc
+    x_rows = x_bytes.rearrange("b r k -> (b r) k")
+    h_rows = h.rearrange("b r k -> (b r) k")
+    out_rows = out.rearrange("s b r f -> s (b r) f")
+
+    with ExitStack() as ctx:
+        keep = ctx.enter_context(tc.tile_pool(name="keep", bufs=1))
+        raw = ctx.enter_context(tc.tile_pool(name="raw", bufs=5))
+        wpool = ctx.enter_context(tc.tile_pool(name="wpool", bufs=2))
+        stage = ctx.enter_context(tc.tile_pool(name="stage", bufs=3))
+        psum = ctx.enter_context(tc.psum_pool(name="psum", bufs=2))
+
+        ident = keep.tile([P, P], F32, name="ident", align_bytes=64)
+        make_identity(nc, ident[:])
+        ones = keep.tile([P, 1], F32, name="ones")
+        nc.vector.memset(ones[:], 1.0)
+        warm = keep.tile([P, 1], F32, name="warm")
+        nc.scalar.activation(out=warm[:], in_=ones[:], func=ACT.Silu)
+        scale = keep.tile([P, 8], F32, name="scale")
+        nc.scalar.dma_start(
+            out=scale[:].rearrange("p (g t) -> p g t", g=2),
+            in_=x_scale.rearrange("o b (g p t) -> p (o b g) t", g=2, p=P, t=4),
+        )
+
+        wv_codes = keep.tile([P, 4 * 512], U32, name="wv_codes", align_bytes=256)
+        wv_sc = keep.tile([P, 4 * 512], U8, name="wv_sc", align_bytes=256)
+        w1_codes = keep.tile([P, 6 * P], U32, name="w1_codes", align_bytes=256)
+        w1_sc = keep.tile([P, 6 * P], U8, name="w1_sc", align_bytes=256)
+        w1_stage = keep.tile([P, 6 * P * 4], BF16, name="w1_stage", align_bytes=256)
+
+        wv_raw, w1_raw, h_raw, x_raw = {}, {}, {}, {}
+        wv_stage, h_sorted, x_wide, hx_stage, v_stage = {}, {}, {}, {}, {}
+        hxq, vq, banks = {}, {}, {}
+        scale_rows = keep.tile([P, D], F32, name="scale_rows")
+
+        def load_wv(s, t):
+            w = wpool.tile([P, D], BF16, name="wv_raw", bufs=8)
+            nc.sync.dma_start(out=w[:], in_=Wv[s].rearrange("(m t) k -> m t k", t=4)[:, t, :])
+            wv_raw[s, t] = w
+
+        def load_w1(s):
+            w = wpool.tile([P, 1536], BF16, name="w1_raw")
+            nc.sync.dma_start(out=w[:], in_=W1[s])
+            w1_raw[s] = w
+
+        def load_h(i, n=1):
+            q = i // 2
+            if q not in h_raw:
+                h_raw[q] = raw.tile([P, 4 * D], BF16, name="h_raw")
+            src = h_rows[512 * q : 512 * (q + 1), :].rearrange("(p c) k -> p (c k)", c=4)
+            lo, hi = i % 2 * 2 * D, (i % 2 + n) * 2 * D
+            nc.sync.dma_start(out=h_raw[q][:, lo:hi], in_=src[:, lo:hi])
+
+        def load_x(i, n=1):
+            q = i // 2
+            if q not in x_raw:
+                x_raw[q] = raw.tile([P, 4 * D], U8, name="x_raw")
+            src = x_rows[512 * q : 512 * (q + 1), :].rearrange("(p c) k -> p (c k)", c=4)
+            lo, hi = i % 2 * 2 * D, (i % 2 + n) * 2 * D
+            nc.sync.dma_start(out=x_raw[q][:, lo:hi], in_=src[:, lo:hi])
+
+        def prefetch(i):
+            if i % 2 == 0 and i + 6 < STEPS:
+                load_h(i + 6, 2)
+                load_x(i + 6, 2)
+
+        def copy_words(on_vector, dst, src):
+            if on_vector:
+                nc.vector.tensor_copy(out=dst, in_=src)
+            else:
+                nc.scalar.copy(out=dst, in_=src)
+
+        def turn_weights(parts):
+            bank = psum.tile([P, 512], F32, name="bank_v", bufs=3)
+            for j, (words, base) in enumerate(parts):
+                for u in range(2):
+                    c = 2 * j + u
+                    nc.tensor.transpose(bank[:, c * P : (c + 1) * P], words[:, base + u : base + 256 : 2], ident[:])
+            return bank
+
+        def turn_wv(s, t):
+            words = wv_raw[s, t][:].bitcast(F32)
+            banks["w", s, t] = turn_weights(((words, 0), (words, 256)))
+
+        def copy_wv(s, t, on_vector=False):
+            if t % 2 == 0:
+                wv_stage[s, t // 2] = wpool.tile([P, 2 * D], BF16, name="wv_stage", align_bytes=256, bufs=3)
+            dst = wv_stage[s, t // 2][:, t % 2 * D : (t % 2 + 1) * D].bitcast(F32)
+            copy_words(
+                on_vector,
+                dst.rearrange("p (g m u) -> p g m u", g=2, u=2),
+                banks["w", s, t][:].rearrange("p (g u m) -> p g m u", g=2, u=2),
+            )
+
+        def quant_wv(s, half):
+            c = (2 * s + half) * 512
+            nc.vector.quantize_mx(
+                out=wv_codes[:, c : c + 512].bitcast(X4), scales=wv_sc[:, c : c + 512], in_=wv_stage[s, half][:]
+            )
+
+        def turn_w1(j):
+            banks["1", j] = turn_weights([(w1_raw[s][:].bitcast(F32), 256 * j) for s in range(NS)])
+
+        def copy_w1(j, on_vector=False):
+            dst = w1_stage[:, j * D : (j + 1) * D].bitcast(F32)
+            copy_words(
+                on_vector,
+                dst.rearrange("p (s f u) -> p s f u", s=2, u=2),
+                banks["1", j][:].rearrange("p (s u f) -> p s f u", s=2, u=2),
+            )
+
+        def quant_w1(lo, hi):
+            nc.vector.quantize_mx(
+                out=w1_codes[:, lo * 256 : hi * 256].bitcast(X4),
+                scales=w1_sc[:, lo * 256 : hi * 256],
+                in_=w1_stage[:, lo * D : hi * D],
+            )
+
+        def load_scale_rows():
+            nc.sync.dma_start(out=scale_rows[:], in_=x_scale.rearrange("o b k -> (o b k)").partition_broadcast(P))
+
+        def widen_x(i):
+            w = stage.tile([P, 2 * D], BF16, name="x_wide", align_bytes=256)
+            x_wide[i] = w
+            if i in APART:
+                for a in range(2):
+                    c = (2 * (i % 2) + a) * D
+                    nc.vector.tensor_tensor(
+                        out=w[:, a * D : (a + 1) * D],
+                        in0=x_raw[i // 2][:, c : c + D].bitcast(F8),
+                        in1=scale_rows[:],
+                        op=MULT,
+                    )
+                return
+            src = x_raw[i // 2][:, i % 2 * 2 * D : (i % 2 + 1) * 2 * D].bitcast(F8)
+            nc.vector.tensor_scalar(
+                out=w[:].rearrange("p (u n e) -> p n u e", u=2, e=2),
+                in0=src.rearrange("p (n u e) -> p n u e", u=2, e=2),
+                scalar1=ones[:, 0:1],
+                scalar2=None,
+                op0=MULT,
+            )
+
+        def turn_x(i, g):
+            words = x_wide[i][:].bitcast(F32)
+            bank = psum.tile([P, 512], F32, name="bank_x", bufs=2)
+            for u in range(2):
+                for a in range(2):
+                    if i in APART:
+                        c = a * 512 + g * 256
+                        w = words[:, c + u : c + 256 : 2]
+                    else:
+                        c = u * 512 + a * 256 + g * P
+                        w = words[:, c : c + P]
+                    k = 2 * u + a
+                    nc.tensor.transpose(bank[:, k * P : (k + 1) * P], w, ident[:])
+            banks["x", i, g] = bank
+
+        def stage_of(kind, i):
+            j = i - 1 if kind == "h" else i
+            if j not in hx_stage:
+                hx_stage[j] = stage.tile([P, 4 * D], BF16, name="hx_stage", align_bytes=256)
+            return hx_stage[j]
+
+        def unload(i, kind, g, on_vector):
+            c = (g if kind == "h" else 2 + g) * D
+            copy_words(
+                on_vector,
+                stage_of(kind, i)[:, c : c + D].bitcast(F32).rearrange("p (n u) -> p n u", u=2),
+                banks[kind, i, g][:].rearrange("p (u n) -> p n u", u=2),
+            )
+
+        def scale_x(i, g, on_vector=False):
+            if i in APART:
+                unload(i, "x", g, on_vector)
+                return
+            sc = scale[:, 4 * g : 4 * g + 4].rearrange("p (u e) -> p u e", u=2)
+            nc.vector.tensor_tensor(
+                out=stage_of("x", i)[:, (2 + g) * D : (3 + g) * D].rearrange("p (n u e) -> p n u e", u=2, e=2),
+                in0=banks["x", i, g][:].bitcast(BF16).rearrange("p (u n e) -> p n u e", u=2, e=2),
+                in1=sc.unsqueeze(1).to_broadcast([P, 256, 2, 2]),
+                op=MULT,
+            )
+
+        def sort_h(i):
+            on_vector = i in SORT_V
+            if not on_vector and i not in SORT_S:
+                return
+            w = stage.tile([P, 2 * D], BF16, name="h_sorted", align_bytes=256, bufs=2)
+            src = h_raw[i // 2][:, i % 2 * 2 * D : (i % 2 + 1) * 2 * D].bitcast(F32)
+            copy_words(
+                on_vector,
+                w[:].bitcast(F32).rearrange("p (u n) -> p u n", u=2),
+                src.rearrange("p (n u) -> p u n", u=2),
+            )
+            h_sorted[i] = w
+
+        def turn_h(i, g):
+            bank = psum.tile([P, 512], F32, name="bank_h", bufs=2)
+            for u in range(2):
+                for a in range(2):
+                    if i in h_sorted:
+                        c = u * 512 + a * 256 + g * P
+                        w = h_sorted[i][:].bitcast(F32)[:, c : c + P]
+                    else:
+                        c = (2 * (i % 2) + a) * 512 + g * 256
+                        w = h_raw[i // 2][:].bitcast(F32)[:, c + u : c + 256 : 2]
+                    k = 2 * u + a
+                    nc.tensor.transpose(bank[:, k * P : (k + 1) * P], w, ident[:])
+            banks["h", i, g] = bank
+
+        def copy_h(i, g, on_vector=False):
+            unload(i, "h", g, on_vector)
+
+        def quantise(name, src, pieces=1):
+            n = src.shape[1] // 4
+            codes = stage.tile([P, n], U32, name=name + "_codes", align_bytes=256)
+            scales = stage.tile([P, n], U8, name=name + "_scales", align_bytes=256)
+            n = n // pieces
+            for k in range(pieces):
+                nc.vector.quantize_mx(
+                    out=codes[:, k * n : (k + 1) * n].bitcast(X4),
+                    scales=scales[:, k * n : (k + 1) * n],
+                    in_=src[:, 4 * k * n : 4 * (k + 1) * n],
+                )
+            return codes, scales
+
+        def quant_hx(i, kinds="hx"):
+            if i == STEPS - 1:
+                kinds = "x"
+            if i not in hxq:
+                hxq[i] = (
+                    stage.tile([P, 1024], U32, name="hx_codes", align_bytes=256),
+                    stage.tile([P, 1024], U8, name="hx_scales", align_bytes=256),
+                )
+            codes, scales = hxq[i]
+            lo, hi = (0 if "h" in kinds else 512), (1024 if "x" in kinds else 512)
+            nc.vector.quantize_mx(
+                out=codes[:, lo:hi].bitcast(X4), scales=scales[:, lo:hi], in_=hx_stage[i][:, 4 * lo : 4 * hi]
+            )
+
+        def quant_v(i, pieces=1):
+            vq[i] = quantise("v", v_stage[i], pieces)
+
+        def views(i, s):
+            codes, scales = hxq[i - 1]
+            if i not in v_stage:
+                v_stage[i] = stage.tile([P, 2 * D], BF16, name="v_stage", align_bytes=256)
+            for a in range(2):
+                bank = psum.tile([P, 512], F32, name="bank_v", bufs=3)
+                for t in range(4):
+                    for g in range(2):
+                        w = ((4 * s + t) * 2 + g) * P
+                        c = g * 256 + a * P
+                        nc.tensor.matmul_mx(
+                            out=bank[:, t * P : (t + 1) * P],
+                            lhsT=wv_codes[:, w : w + P].bitcast(X4),
+                            lhsT_scale=wv_sc[:, w : w + P],
+                            rhs=codes[:, c : c + P].bitcast(X4),
+                            rhs_scale=scales[:, c : c + P],
+                            start=(g == 0),
+                            stop=(g == 1),
+                        )
+                k = 2 * s + a
+                nc.scalar.copy(
+                    out=v_stage[i][:, k * 512 : (k + 1) * 512].rearrange("p (r t) -> p r t", t=4),
+                    in_=bank[:].rearrange("p (t r) -> p r t", t=4),
+                )
+
+        def finish(i):
+            xc, xs = hxq[i]
+            vc, vs = vq[i]
+            bank = psum.tile([P, 512], F32, name="bank_o", bufs=1)
+            for a in range(2):
+                for j in range(2):
+                    c = 512 + j * 256 + a * P
+                    nc.tensor.matmul_mx(
+                        out=bank[:, a * 256 : (a + 1) * 256],
+                        lhsT=xc[:, c : c + P].bitcast(X4),
+                        lhsT_scale=xs[:, c : c + P],
+                        rhs=w1_codes[:, j * 256 : (j + 1) * 256].bitcast(X4),
+                        rhs_scale=w1_sc[:, j * 256 : (j + 1) * 256],
+                        start=(j == 0),
+                        stop=False,
+                    )
+                for s in range(NS):
+                    c = (2 * s + a) * P
+                    w = (4 + s) * P
+                    k = 2 * a + s
+                    nc.tensor.matmul_mx(
+                        out=bank[:, k * P : (k + 1) * P],
+                        lhsT=vc[:, c : c + P].bitcast(X4),
+                        lhsT_scale=vs[:, c : c + P],
+                        rhs=w1_codes[:, w : w + P].bitcast(X4),
+                        rhs_scale=w1_sc[:, w : w + P],
+                        start=False,
+                        stop=(s == 1),
+                    )
+            res = stage.tile([P, 512], F32, name="res", bufs=4)
+            nc.scalar.activation(
+                out=res[:].rearrange("p (s a f) -> p s a f", s=2, a=2),
+                in_=bank[:].rearrange("p (a s f) -> p s a f", s=2, a=2),
+                func=ACT.Silu,
+            )
+            dst = out_rows[:, 512 * (i // 2) : 512 * (i // 2 + 1), :].rearrange("s (p c) f -> p s c f", c=4)
+            c = i % 2 * 2
+            for s in range(NS):
+                nc.sync.dma_start(
+                    out=dst[:, s, c : c + 2, :],
+                    in_=res[:, s * 256 : (s + 1) * 256].rearrange("p (a f) -> p a f", a=2),
+                )
+
+        def x_part_apart(i):
+            xc, xs = hxq[i]
+            for k in range(4):
+                s, a = divmod(k, 2)
+                bank = psum.tile([P, 512], F32, name="bank_x" if k < 2 else "bank_h", bufs=2)
+                for j in range(2):
+                    c = 512 + j * 256 + a * P
+                    w = (2 * j + s) * P
+                    nc.tensor.matmul_mx(
+                        out=bank[:, 0:P],
+                        lhsT=xc[:, c : c + P].bitcast(X4),
+                        lhsT_scale=xs[:, c : c + P],
+                        rhs=w1_codes[:, w : w + P].bitcast(X4),
+                        rhs_scale=w1_sc[:, w : w + P],
+                        start=(j == 0),
+                        stop=False,
+                    )
+                banks["o", k] = bank
+
+        def finish_apart(i, pieces=1):
+            vc, vs = vq[i]
+            dst = out_rows[:, 512 * (i // 2) : 512 * (i // 2 + 1), :].rearrange("s (p c) f -> p s c f", c=4)
+            for k in range(4):
+                s, a = divmod(k, 2)
+                w = (4 + s) * P
+                nc.tensor.matmul_mx(
+                    out=banks["o", k][:, 0:P],
+                    lhsT=vc[:, k * P : (k + 1) * P].bitcast(X4),
+                    lhsT_scale=vs[:, k * P : (k + 1) * P],
+                    rhs=w1_codes[:, w : w + P].bitcast(X4),
+                    rhs_scale=w1_sc[:, w : w + P],
+                    start=False,
+                    stop=True,
+                )
+                res = stage.tile([P, P], F32, name="res_apart", bufs=4)
+                nc.scalar.activation(out=res[:], in_=banks["o", k][:, 0:P], func=ACT.Silu)
+                nc.sync.dma_start(out=dst[:, s, i % 2 * 2 + a, :], in_=res[:])
+
+        with tc.manual_schedule():
+            load_h(0)
+            load_x(0)
+            load_wv(0, 1)
+            load_wv(0, 2)
+            load_wv(0, 0)
+            load_wv(1, 0)
+            load_wv(0, 3)
+            load_wv(1, 2)
+            load_wv(1, 1)
+            turn_h(0, 1)
+            load_h(1)
+            widen_x(0)
+            load_x(1)
+            load_wv(1, 3)
+            turn_h(0, 0)
+            turn_wv(0, 1)
+            load_w1(0)
+            load_x(2, 2)
+            load_w1(1)
+            copy_h(0, 1)
+            copy_h(0, 0, True)
+            turn_x(0, 0)
+            turn_wv(0, 0)
+            copy_wv(0, 0)
+            turn_wv(0, 2)
+            copy_wv(0, 2)
+            copy_wv(0, 1, True)
+            turn_wv(0, 3)
+            turn_wv(1, 0)
+            turn_wv(1, 1)
+            load_h(2, 2)
+            scale_x(0, 0)
+            quant_wv(0, 0)
+            copy_wv(0, 3)
+            quant_wv(0, 1)
+            quant_hx(-1, "h")
+            turn_x(0, 1)
+            copy_wv(1, 0)
+            turn_wv(1, 2)
+            load_x(6, 2)
+            copy_wv(1, 2, True)
+            turn_h(1, 0)
+            turn_wv(1, 3)
+            load_x(4, 2)
+            copy_wv(1, 1)
+            turn_h(1, 1)
+            copy_h(1, 0)
+            scale_x(0, 1)
+            load_h(4, 2)
+            copy_wv(1, 3)
+            quant_wv(1, 1)
+            copy_h(1, 1)
+            views(0, 0)
+            widen_x(1)
+            turn_w1(0)
+            copy_w1(0)
+            load_h(6, 2)
+            turn_w1(1)
+            quant_wv(1, 0)
+            quant_hx(0)
+            copy_w1(1)
+            quant_w1(0, 2)
+            turn_w1(2)
+            copy_w1(2)
+            quant_w1(2, 3)
+            views(0, 1)
+            for i in range(1, STEPS):
+                prefetch(i)
+                turn_x(i, 1)
+                quant_v(i - 1)
+                turn_x(i, 0)
+                if i + 1 < STEPS: turn_h(i + 1, 0)
+                if i + 1 < STEPS: copy_h(i + 1, 0)
+                if i + 1 < STEPS: turn_h(i + 1, 1)
+                scale_x(i, 0)
+                scale_x(i, 1)
+                if i + 1 < STEPS: copy_h(i + 1, 1)
+                if i + 1 < STEPS: widen_x(i + 1)
+                views(i, 0)
+                views(i, 1)
+                quant_hx(i)
+                finish(i - 1)
+            x_part_apart(STEPS - 1)
+            quant_v(STEPS - 1, 4)
+            finish_apart(STEPS - 1)

@@ -18,9 +18,7 @@ P = 128
 D = 1024
 NS = 2
 STEPS = 16
-APART = ()
-SORT_V = ()
-SORT_S = ()
+V_BLOCKS = 3
 
 
 def tile_distributedb_pa_t_kernel(tc, x_bytes, x_scale, h, Wv, W1, out):
@@ -36,17 +34,18 @@ def tile_distributedb_pa_t_kernel(tc, x_bytes, x_scale, h, Wv, W1, out):
         stage = ctx.enter_context(tc.tile_pool(name="stage", bufs=3))
         psum = ctx.enter_context(tc.psum_pool(name="psum", bufs=2))
 
+        scale = keep.tile([P, 8], F32, name="scale")
+        nc.scalar.dma_start(
+            out=scale[:].rearrange("p (g t) -> p g t", g=2),
+            in_=x_scale.rearrange("o b (g p t) -> p (o b g) t", g=2, p=P, t=4),
+        )
+
         ident = keep.tile([P, P], F32, name="ident", align_bytes=64)
         make_identity(nc, ident[:])
         ones = keep.tile([P, 1], F32, name="ones")
         nc.vector.memset(ones[:], 1.0)
         warm = keep.tile([P, 1], F32, name="warm")
         nc.scalar.activation(out=warm[:], in_=ones[:], func=ACT.Silu)
-        scale = keep.tile([P, 8], F32, name="scale")
-        nc.scalar.dma_start(
-            out=scale[:].rearrange("p (g t) -> p g t", g=2),
-            in_=x_scale.rearrange("o b (g p t) -> p (o b g) t", g=2, p=P, t=4),
-        )
 
         wv_codes = keep.tile([P, 4 * 512], U32, name="wv_codes", align_bytes=256)
         wv_sc = keep.tile([P, 4 * 512], U8, name="wv_sc", align_bytes=256)
@@ -55,9 +54,9 @@ def tile_distributedb_pa_t_kernel(tc, x_bytes, x_scale, h, Wv, W1, out):
         w1_stage = keep.tile([P, 6 * P * 4], BF16, name="w1_stage", align_bytes=256)
 
         wv_raw, w1_raw, h_raw, x_raw = {}, {}, {}, {}
-        wv_stage, h_sorted, x_wide, hx_stage, v_stage = {}, {}, {}, {}, {}
+        wv_stage, h_sorted, x_wide, x_plain, hx_stage, v_stage = {}, {}, {}, {}, {}, {}
         hxq, vq, banks = {}, {}, {}
-        scale_rows = keep.tile([P, D], F32, name="scale_rows")
+        shared = [keep.tile([P, 2 * D], BF16, name="shared%d" % n, align_bytes=256) for n in range(2)]
 
         def load_wv(s, t):
             w = wpool.tile([P, D], BF16, name="wv_raw", bufs=8)
@@ -142,44 +141,39 @@ def tile_distributedb_pa_t_kernel(tc, x_bytes, x_scale, h, Wv, W1, out):
                 in_=w1_stage[:, lo * D : hi * D],
             )
 
-        def load_scale_rows():
-            nc.sync.dma_start(out=scale_rows[:], in_=x_scale.rearrange("o b k -> (o b k)").partition_broadcast(P))
-
-        def widen_x(i):
+        def widen_x(i, blocks=V_BLOCKS):
             w = stage.tile([P, 2 * D], BF16, name="x_wide", align_bytes=256)
-            x_wide[i] = w
-            if i in APART:
-                for a in range(2):
-                    c = (2 * (i % 2) + a) * D
-                    nc.vector.tensor_tensor(
-                        out=w[:, a * D : (a + 1) * D],
-                        in0=x_raw[i // 2][:, c : c + D].bitcast(F8),
-                        in1=scale_rows[:],
-                        op=MULT,
-                    )
-                return
-            src = x_raw[i // 2][:, i % 2 * 2 * D : (i % 2 + 1) * 2 * D].bitcast(F8)
+            x_wide[i] = w, blocks
+            c = i % 2 * 2 * D
+            src = x_raw[i // 2][:, c : c + blocks * 512].bitcast(F8)
             nc.vector.tensor_scalar(
-                out=w[:].rearrange("p (u n e) -> p n u e", u=2, e=2),
+                out=w[:, : blocks * 512].rearrange("p (u n e) -> p n u e", u=2, e=2),
                 in0=src.rearrange("p (n u e) -> p n u e", u=2, e=2),
                 scalar1=ones[:, 0:1],
                 scalar2=None,
                 op0=MULT,
             )
 
+        def widen_x_rest(i):
+            w = stage.tile([P, (4 - V_BLOCKS) * 512], BF16, name="x_plain", align_bytes=256)
+            x_plain[i] = w
+            c = i % 2 * 2 * D
+            nc.scalar.copy(out=w[:], in_=x_raw[i // 2][:, c + V_BLOCKS * 512 : c + 2 * D].bitcast(F8))
+
         def turn_x(i, g):
-            words = x_wide[i][:].bitcast(F32)
+            w, blocks = x_wide[i]
             bank = psum.tile([P, 512], F32, name="bank_x", bufs=2)
             for u in range(2):
                 for a in range(2):
-                    if i in APART:
-                        c = a * 512 + g * 256
-                        w = words[:, c + u : c + 256 : 2]
+                    b = 2 * a + g
+                    if b < blocks:
+                        c = (u * blocks + b) * P
+                        words = w[:].bitcast(F32)[:, c : c + P]
                     else:
-                        c = u * 512 + a * 256 + g * P
-                        w = words[:, c : c + P]
+                        c = (b - blocks) * 256
+                        words = x_plain[i][:].bitcast(F32)[:, c + u : c + 256 : 2]
                     k = 2 * u + a
-                    nc.tensor.transpose(bank[:, k * P : (k + 1) * P], w, ident[:])
+                    nc.tensor.transpose(bank[:, k * P : (k + 1) * P], words, ident[:])
             banks["x", i, g] = bank
 
         def stage_of(kind, i):
@@ -196,10 +190,7 @@ def tile_distributedb_pa_t_kernel(tc, x_bytes, x_scale, h, Wv, W1, out):
                 banks[kind, i, g][:].rearrange("p (u n) -> p n u", u=2),
             )
 
-        def scale_x(i, g, on_vector=False):
-            if i in APART:
-                unload(i, "x", g, on_vector)
-                return
+        def scale_x(i, g):
             sc = scale[:, 4 * g : 4 * g + 4].rearrange("p (u e) -> p u e", u=2)
             nc.vector.tensor_tensor(
                 out=stage_of("x", i)[:, (2 + g) * D : (3 + g) * D].rearrange("p (n u e) -> p n u e", u=2, e=2),
@@ -209,15 +200,11 @@ def tile_distributedb_pa_t_kernel(tc, x_bytes, x_scale, h, Wv, W1, out):
             )
 
         def sort_h(i):
-            on_vector = i in SORT_V
-            if not on_vector and i not in SORT_S:
-                return
-            w = stage.tile([P, 2 * D], BF16, name="h_sorted", align_bytes=256, bufs=2)
+            w = shared[i % 2]
             src = h_raw[i // 2][:, i % 2 * 2 * D : (i % 2 + 1) * 2 * D].bitcast(F32)
-            copy_words(
-                on_vector,
-                w[:].bitcast(F32).rearrange("p (u n) -> p u n", u=2),
-                src.rearrange("p (n u) -> p u n", u=2),
+            nc.gpsimd.tensor_copy(
+                out=w[:].bitcast(F32).rearrange("p (u n) -> p u n", u=2),
+                in_=src.rearrange("p (n u) -> p u n", u=2),
             )
             h_sorted[i] = w
 
@@ -271,7 +258,7 @@ def tile_distributedb_pa_t_kernel(tc, x_bytes, x_scale, h, Wv, W1, out):
         def views(i, s):
             codes, scales = hxq[i - 1]
             if i not in v_stage:
-                v_stage[i] = stage.tile([P, 2 * D], BF16, name="v_stage", align_bytes=256)
+                v_stage[i] = shared[(i + 1) % 2]
             for a in range(2):
                 bank = psum.tile([P, 512], F32, name="bank_v", bufs=3)
                 for t in range(4):
@@ -375,88 +362,74 @@ def tile_distributedb_pa_t_kernel(tc, x_bytes, x_scale, h, Wv, W1, out):
                 nc.sync.dma_start(out=dst[:, s, i % 2 * 2 + a, :], in_=res[:])
 
         with tc.manual_schedule():
-            load_h(0)
-            load_x(0)
-            load_wv(0, 1)
-            load_wv(0, 2)
             load_wv(0, 0)
-            load_wv(1, 0)
-            load_wv(0, 3)
-            load_wv(1, 2)
-            load_wv(1, 1)
-            turn_h(0, 1)
+            load_x(0)
+            for t in range(1, 4):
+                load_wv(0, t)
+            load_h(0)
+            for t in range(4):
+                load_wv(1, t)
             load_h(1)
-            widen_x(0)
             load_x(1)
-            load_wv(1, 3)
-            turn_h(0, 0)
-            turn_wv(0, 1)
-            load_w1(0)
-            load_x(2, 2)
-            load_w1(1)
-            copy_h(0, 1)
-            copy_h(0, 0, True)
-            turn_x(0, 0)
-            turn_wv(0, 0)
-            copy_wv(0, 0)
-            turn_wv(0, 2)
-            copy_wv(0, 2)
-            copy_wv(0, 1, True)
-            turn_wv(0, 3)
-            turn_wv(1, 0)
-            turn_wv(1, 1)
-            load_h(2, 2)
-            scale_x(0, 0)
-            quant_wv(0, 0)
-            copy_wv(0, 3)
-            quant_wv(0, 1)
+            for s in range(NS):
+                load_w1(s)
+            for i in (2, 4, 6):
+                load_h(i, 2)
+                load_x(i, 2)
+            widen_x(0, 4)
+            for t in range(4):
+                turn_wv(0, t)
+                copy_wv(0, t)
+                if t == 1:
+                    turn_x(0, 0)
+                    scale_x(0, 0)
+                if t % 2 == 1:
+                    quant_wv(0, t // 2)
+            for g in range(2):
+                turn_h(0, g)
+                copy_h(0, g, g == 1)
             quant_hx(-1, "h")
             turn_x(0, 1)
-            copy_wv(1, 0)
-            turn_wv(1, 2)
-            load_x(6, 2)
-            copy_wv(1, 2, True)
-            turn_h(1, 0)
-            turn_wv(1, 3)
-            load_x(4, 2)
-            copy_wv(1, 1)
-            turn_h(1, 1)
-            copy_h(1, 0)
             scale_x(0, 1)
-            load_h(4, 2)
-            copy_wv(1, 3)
-            quant_wv(1, 1)
-            copy_h(1, 1)
+            for t in range(4):
+                turn_wv(1, t)
+                copy_wv(1, t)
+                if t % 2 == 1:
+                    quant_wv(1, t // 2)
             views(0, 0)
-            widen_x(1)
-            turn_w1(0)
-            copy_w1(0)
-            load_h(6, 2)
-            turn_w1(1)
-            quant_wv(1, 0)
+            for g in range(2):
+                turn_h(1, g)
+                copy_h(1, g)
+            widen_x(1, 4)
             quant_hx(0)
-            copy_w1(1)
-            quant_w1(0, 2)
-            turn_w1(2)
-            copy_w1(2)
-            quant_w1(2, 3)
             views(0, 1)
+            for j in range(3):
+                turn_w1(j)
+                copy_w1(j)
+            quant_w1(0, 2)
+            quant_w1(2, 3)
+            widen_x_rest(2)
             for i in range(1, STEPS):
+                more = i + 1 < STEPS
                 prefetch(i)
-                turn_x(i, 1)
                 quant_v(i - 1)
-                turn_x(i, 0)
-                if i + 1 < STEPS: turn_h(i + 1, 0)
-                if i + 1 < STEPS: copy_h(i + 1, 0)
-                if i + 1 < STEPS: turn_h(i + 1, 1)
-                scale_x(i, 0)
-                scale_x(i, 1)
-                if i + 1 < STEPS: copy_h(i + 1, 1)
-                if i + 1 < STEPS: widen_x(i + 1)
-                views(i, 0)
-                views(i, 1)
+                if i + 2 < STEPS:
+                    sort_h(i + 2)
+                for g in range(2):
+                    turn_x(i, g)
+                for g in range(2):
+                    if more:
+                        turn_h(i + 1, g)
+                        copy_h(i + 1, g)
+                    scale_x(i, g)
+                if more:
+                    widen_x(i + 1)
+                for s in range(NS):
+                    views(i, s)
                 quant_hx(i)
                 finish(i - 1)
+                if i + 2 < STEPS:
+                    widen_x_rest(i + 2)
             x_part_apart(STEPS - 1)
             quant_v(STEPS - 1, 4)
             finish_apart(STEPS - 1)

@@ -17,8 +17,9 @@ ACT = mybir.ActivationFunctionType
 P = 128
 D = 1024
 NS = 2
-STEPS = 16
-V_BLOCKS = 3
+PAIRS = (1,) * 16
+STEPS = len(PAIRS)
+S_BLOCKS = {1: 1}
 
 
 def tile_distributedb_pa_t_kernel(tc, x_bytes, x_scale, h, Wv, W1, out):
@@ -26,20 +27,26 @@ def tile_distributedb_pa_t_kernel(tc, x_bytes, x_scale, h, Wv, W1, out):
     x_rows = x_bytes.rearrange("b r k -> (b r) k")
     h_rows = h.rearrange("b r k -> (b r) k")
     out_rows = out.rearrange("s b r f -> s (b r) f")
+    row0 = [256 * sum(PAIRS[:i]) for i in range(STEPS + 1)]
+
+    def plain_blocks(i):
+        return S_BLOCKS[PAIRS[i]] if 2 <= i < STEPS else 0
+
+    def h_blocks(i):
+        return 4 * PAIRS[i] if i < STEPS else 0
 
     with ExitStack() as ctx:
         keep = ctx.enter_context(tc.tile_pool(name="keep", bufs=1))
-        raw = ctx.enter_context(tc.tile_pool(name="raw", bufs=5))
+        raw = ctx.enter_context(tc.tile_pool(name="raw", bufs=4))
         wpool = ctx.enter_context(tc.tile_pool(name="wpool", bufs=2))
-        stage = ctx.enter_context(tc.tile_pool(name="stage", bufs=3))
-        psum = ctx.enter_context(tc.psum_pool(name="psum", bufs=2))
+        stage = ctx.enter_context(tc.tile_pool(name="stage", bufs=2))
+        psum = ctx.enter_context(tc.psum_pool(name="psum", bufs=8))
 
         scale = keep.tile([P, 8], F32, name="scale")
         nc.scalar.dma_start(
             out=scale[:].rearrange("p (g t) -> p g t", g=2),
             in_=x_scale.rearrange("o b (g p t) -> p (o b g) t", g=2, p=P, t=4),
         )
-
         ident = keep.tile([P, P], F32, name="ident", align_bytes=64)
         make_identity(nc, ident[:])
         ones = keep.tile([P, 1], F32, name="ones")
@@ -52,11 +59,15 @@ def tile_distributedb_pa_t_kernel(tc, x_bytes, x_scale, h, Wv, W1, out):
         w1_codes = keep.tile([P, 6 * P], U32, name="w1_codes", align_bytes=256)
         w1_sc = keep.tile([P, 6 * P], U8, name="w1_sc", align_bytes=256)
         w1_stage = keep.tile([P, 6 * P * 4], BF16, name="w1_stage", align_bytes=256)
+        wide = max(h_blocks(i + 1) + plain_blocks(i) for i in range(STEPS)) * 512
+        shared = [keep.tile([P, wide], BF16, name="shared%d" % n, align_bytes=256) for n in range(2)]
 
         wv_raw, w1_raw, h_raw, x_raw = {}, {}, {}, {}
-        wv_stage, h_sorted, x_wide, x_plain, hx_stage, v_stage = {}, {}, {}, {}, {}, {}
-        hxq, vq, banks = {}, {}, {}
-        shared = [keep.tile([P, 2 * D], BF16, name="shared%d" % n, align_bytes=256) for n in range(2)]
+        in_order = {}
+        wv_stage, x_wide, stages, quant, banks = {}, {}, {}, {}, {}
+
+        def new_bank():
+            return psum.tile([P, 512], F32, name="bank")
 
         def load_wv(s, t):
             w = wpool.tile([P, D], BF16, name="wv_raw", bufs=8)
@@ -68,26 +79,20 @@ def tile_distributedb_pa_t_kernel(tc, x_bytes, x_scale, h, Wv, W1, out):
             nc.sync.dma_start(out=w[:], in_=W1[s])
             w1_raw[s] = w
 
-        def load_h(i, n=1):
-            q = i // 2
-            if q not in h_raw:
-                h_raw[q] = raw.tile([P, 4 * D], BF16, name="h_raw")
-            src = h_rows[512 * q : 512 * (q + 1), :].rearrange("(p c) k -> p (c k)", c=4)
-            lo, hi = i % 2 * 2 * D, (i % 2 + n) * 2 * D
-            nc.sync.dma_start(out=h_raw[q][:, lo:hi], in_=src[:, lo:hi])
+        def load_h(i):
+            h_raw[i] = raw.tile([P, wide], BF16, name="h_raw", align_bytes=256)
+            src = h_rows[row0[i] : row0[i + 1], :].rearrange("(p r) k -> p r k", p=P)
+            if i > 0:
+                nc.sync.dma_start(out=h_raw[i][:, : h_blocks(i) * 512], in_=src.rearrange("p r k -> p (r k)"))
+                return
+            for g in range(2):
+                dst = h_raw[i][:, g * D : (g + 1) * D].rearrange("p (r k) -> p r k", k=512)
+                nc.sync.dma_start(out=dst, in_=src[:, :, g * 512 : (g + 1) * 512])
 
-        def load_x(i, n=1):
-            q = i // 2
-            if q not in x_raw:
-                x_raw[q] = raw.tile([P, 4 * D], U8, name="x_raw")
-            src = x_rows[512 * q : 512 * (q + 1), :].rearrange("(p c) k -> p (c k)", c=4)
-            lo, hi = i % 2 * 2 * D, (i % 2 + n) * 2 * D
-            nc.sync.dma_start(out=x_raw[q][:, lo:hi], in_=src[:, lo:hi])
-
-        def prefetch(i):
-            if i % 2 == 0 and i + 6 < STEPS:
-                load_h(i + 6, 2)
-                load_x(i + 6, 2)
+        def load_x(i):
+            x_raw[i] = raw.tile([P, 4 * D], U8, name="x_raw")
+            src = x_rows[row0[i] : row0[i + 1], :].rearrange("(p r) k -> p (r k)", p=P)
+            nc.sync.dma_start(out=x_raw[i][:, : PAIRS[i] * 2 * D], in_=src)
 
         def copy_words(on_vector, dst, src):
             if on_vector:
@@ -95,17 +100,21 @@ def tile_distributedb_pa_t_kernel(tc, x_bytes, x_scale, h, Wv, W1, out):
             else:
                 nc.scalar.copy(out=dst, in_=src)
 
-        def turn_weights(parts):
-            bank = psum.tile([P, 512], F32, name="bank_v", bufs=3)
-            for j, (words, base) in enumerate(parts):
-                for u in range(2):
-                    c = 2 * j + u
-                    nc.tensor.transpose(bank[:, c * P : (c + 1) * P], words[:, base + u : base + 256 : 2], ident[:])
-            return bank
+        def every_second(tile, block, u):
+            return tile[:].bitcast(F32)[:, 256 * block + u : 256 * (block + 1) : 2]
+
+        def in_a_row(tile, blocks, block, u):
+            c = (u * blocks + block) * P
+            return tile[:].bitcast(F32)[:, c : c + P]
+
+        def turn(key, parts):
+            bank = new_bank()
+            for c, words in enumerate(parts):
+                nc.tensor.transpose(bank[:, c * P : (c + 1) * P], words, ident[:])
+            banks[key] = bank
 
         def turn_wv(s, t):
-            words = wv_raw[s, t][:].bitcast(F32)
-            banks["w", s, t] = turn_weights(((words, 0), (words, 256)))
+            turn(("w", s, t), [every_second(wv_raw[s, t], g, u) for g in range(2) for u in range(2)])
 
         def copy_wv(s, t, on_vector=False):
             if t % 2 == 0:
@@ -124,7 +133,7 @@ def tile_distributedb_pa_t_kernel(tc, x_bytes, x_scale, h, Wv, W1, out):
             )
 
         def turn_w1(j):
-            banks["1", j] = turn_weights([(w1_raw[s][:].bitcast(F32), 256 * j) for s in range(NS)])
+            turn(("1", j), [every_second(w1_raw[s], j, u) for s in range(NS) for u in range(2)])
 
         def copy_w1(j, on_vector=False):
             dst = w1_stage[:, j * D : (j + 1) * D].bitcast(F32)
@@ -141,130 +150,110 @@ def tile_distributedb_pa_t_kernel(tc, x_bytes, x_scale, h, Wv, W1, out):
                 in_=w1_stage[:, lo * D : hi * D],
             )
 
-        def widen_x(i, blocks=V_BLOCKS):
-            w = stage.tile([P, 2 * D], BF16, name="x_wide", align_bytes=256)
-            x_wide[i] = w, blocks
-            c = i % 2 * 2 * D
-            src = x_raw[i // 2][:, c : c + blocks * 512].bitcast(F8)
+        def widen_x(i):
+            n = (4 * PAIRS[i] - plain_blocks(i)) * 512
+            x_wide[i] = stage.tile([P, 4 * D], BF16, name="x_wide", align_bytes=256)
             nc.vector.tensor_scalar(
-                out=w[:, : blocks * 512].rearrange("p (u n e) -> p n u e", u=2, e=2),
-                in0=src.rearrange("p (n u e) -> p n u e", u=2, e=2),
+                out=x_wide[i][:, :n].rearrange("p (u n e) -> p n u e", u=2, e=2),
+                in0=x_raw[i][:, :n].bitcast(F8).rearrange("p (n u e) -> p n u e", u=2, e=2),
                 scalar1=ones[:, 0:1],
                 scalar2=None,
                 op0=MULT,
             )
 
-        def widen_x_rest(i):
-            w = stage.tile([P, (4 - V_BLOCKS) * 512], BF16, name="x_plain", align_bytes=256)
-            x_plain[i] = w
-            c = i % 2 * 2 * D
-            nc.scalar.copy(out=w[:], in_=x_raw[i // 2][:, c + V_BLOCKS * 512 : c + 2 * D].bitcast(F8))
+        def widen_x_plain(i):
+            n = plain_blocks(i) * 512
+            if i + 1 == STEPS:
+                h_raw[i + 1] = raw.tile([P, wide], BF16, name="h_raw", align_bytes=256)
+            end, c = PAIRS[i] * 2 * D, h_blocks(i + 1) * 512
+            nc.scalar.copy(out=h_raw[i + 1][:, c : c + n], in_=x_raw[i][:, end - n : end].bitcast(F8))
 
-        def turn_x(i, g):
-            w, blocks = x_wide[i]
-            bank = psum.tile([P, 512], F32, name="bank_x", bufs=2)
-            for u in range(2):
-                for a in range(2):
-                    b = 2 * a + g
-                    if b < blocks:
-                        c = (u * blocks + b) * P
-                        words = w[:].bitcast(F32)[:, c : c + P]
-                    else:
-                        c = (b - blocks) * 256
-                        words = x_plain[i][:].bitcast(F32)[:, c + u : c + 256 : 2]
-                    k = 2 * u + a
-                    nc.tensor.transpose(bank[:, k * P : (k + 1) * P], words, ident[:])
-            banks["x", i, g] = bank
-
-        def stage_of(kind, i):
-            j = i - 1 if kind == "h" else i
-            if j not in hx_stage:
-                hx_stage[j] = stage.tile([P, 4 * D], BF16, name="hx_stage", align_bytes=256)
-            return hx_stage[j]
-
-        def unload(i, kind, g, on_vector):
-            c = (g if kind == "h" else 2 + g) * D
-            copy_words(
-                on_vector,
-                stage_of(kind, i)[:, c : c + D].bitcast(F32).rearrange("p (n u) -> p n u", u=2),
-                banks[kind, i, g][:].rearrange("p (u n) -> p n u", u=2),
+        def sort_words(engine, dst, src, blocks):
+            engine.tensor_copy(
+                out=dst[:, : blocks * 512].bitcast(F32).rearrange("p (u n) -> p u n", u=2),
+                in_=src[:, : blocks * 512].bitcast(F32).rearrange("p (n u) -> p u n", u=2),
             )
 
-        def scale_x(i, g):
+        def sort_h(i, engine=nc.gpsimd, dst=None):
+            in_order[i] = dst if dst is not None else shared[i % 2], h_blocks(i) + plain_blocks(i - 1)
+            sort_words(engine, in_order[i][0], h_raw[i], in_order[i][1])
+
+        def sort_w1(s, engine):
+            in_order["1", s] = wpool.tile([P, 1536], BF16, name="w1_sorted")
+            sort_words(engine, in_order["1", s], w1_raw[s], 3)
+
+        def words_of(kind, i, block, u):
+            if kind == "h":
+                if i == 0:
+                    return every_second(h_raw[i], block % 2 * 2 + block // 2, u)
+                if i not in in_order:
+                    return every_second(h_raw[i], block, u)
+                return in_a_row(*in_order[i], block, u)
+            first_plain = 4 * PAIRS[i] - plain_blocks(i)
+            if block < first_plain:
+                return in_a_row(x_wide[i], first_plain, block, u)
+            return in_a_row(*in_order[i + 1], h_blocks(i + 1) + block - first_plain, u)
+
+        def turn_rows(kind, i, q, g):
+            turn((kind, i, q, g), [words_of(kind, i, 2 * (2 * q + a) + g, u) for u in range(2) for a in range(2)])
+
+        def stage_part(kind, i, q, g):
+            j = i - 1 if kind == "h" else i
+            if j not in stages:
+                stages[j] = stage.tile([P, 4 * D], BF16, name="hx_stage", align_bytes=256, bufs=3)
+            c = (g if kind == "h" else 2 + g) * D
+            return stages[j][:, c : c + D]
+
+        def copy_h(i, q, g, on_vector=False):
+            copy_words(
+                on_vector,
+                stage_part("h", i, q, g).bitcast(F32).rearrange("p (n u) -> p n u", u=2),
+                banks["h", i, q, g][:].rearrange("p (u n) -> p n u", u=2),
+            )
+
+        def scale_x(i, q, g):
             sc = scale[:, 4 * g : 4 * g + 4].rearrange("p (u e) -> p u e", u=2)
             nc.vector.tensor_tensor(
-                out=stage_of("x", i)[:, (2 + g) * D : (3 + g) * D].rearrange("p (n u e) -> p n u e", u=2, e=2),
-                in0=banks["x", i, g][:].bitcast(BF16).rearrange("p (u n e) -> p n u e", u=2, e=2),
+                out=stage_part("x", i, q, g).rearrange("p (n u e) -> p n u e", u=2, e=2),
+                in0=banks["x", i, q, g][:].bitcast(BF16).rearrange("p (u n e) -> p n u e", u=2, e=2),
                 in1=sc.unsqueeze(1).to_broadcast([P, 256, 2, 2]),
                 op=MULT,
             )
 
-        def sort_h(i):
-            w = shared[i % 2]
-            src = h_raw[i // 2][:, i % 2 * 2 * D : (i % 2 + 1) * 2 * D].bitcast(F32)
-            nc.gpsimd.tensor_copy(
-                out=w[:].bitcast(F32).rearrange("p (u n) -> p u n", u=2),
-                in_=src.rearrange("p (n u) -> p u n", u=2),
-            )
-            h_sorted[i] = w
-
-        def turn_h(i, g):
-            bank = psum.tile([P, 512], F32, name="bank_h", bufs=2)
-            for u in range(2):
-                for a in range(2):
-                    if i in h_sorted:
-                        c = u * 512 + a * 256 + g * P
-                        w = h_sorted[i][:].bitcast(F32)[:, c : c + P]
-                    else:
-                        c = (2 * (i % 2) + a) * 512 + g * 256
-                        w = h_raw[i // 2][:].bitcast(F32)[:, c + u : c + 256 : 2]
-                    k = 2 * u + a
-                    nc.tensor.transpose(bank[:, k * P : (k + 1) * P], w, ident[:])
-            banks["h", i, g] = bank
-
-        def copy_h(i, g, on_vector=False):
-            unload(i, "h", g, on_vector)
-
-        def quantise(name, src, pieces=1):
-            n = src.shape[1] // 4
-            codes = stage.tile([P, n], U32, name=name + "_codes", align_bytes=256)
-            scales = stage.tile([P, n], U8, name=name + "_scales", align_bytes=256)
-            n = n // pieces
+        def quantise(kind, i, pieces=1):
+            codes = stage.tile([P, D], U32, name=kind + "_codes", align_bytes=256, bufs=2)
+            scales = stage.tile([P, D], U8, name=kind + "_scales", align_bytes=256, bufs=2)
+            n = PAIRS[i] * 512 // pieces
             for k in range(pieces):
                 nc.vector.quantize_mx(
                     out=codes[:, k * n : (k + 1) * n].bitcast(X4),
                     scales=scales[:, k * n : (k + 1) * n],
-                    in_=src[:, 4 * k * n : 4 * (k + 1) * n],
+                    in_=stages[kind, i][:, 4 * k * n : 4 * (k + 1) * n],
                 )
-            return codes, scales
+            quant[kind, i] = codes, scales
 
-        def quant_hx(i, kinds="hx"):
-            if i == STEPS - 1:
-                kinds = "x"
-            if i not in hxq:
-                hxq[i] = (
-                    stage.tile([P, 1024], U32, name="hx_codes", align_bytes=256),
-                    stage.tile([P, 1024], U8, name="hx_scales", align_bytes=256),
-                )
-            codes, scales = hxq[i]
-            lo, hi = (0 if "h" in kinds else 512), (1024 if "x" in kinds else 512)
+        def quantise_hx(j, with_h=True, with_x=True):
+            if j not in quant:
+                codes = stage.tile([P, D], U32, name="hx_codes", align_bytes=256, bufs=3)
+                scales = stage.tile([P, D], U8, name="hx_scales", align_bytes=256, bufs=3)
+                quant[j] = codes, scales
+                quant["h", j + 1] = codes[:, :512], scales[:, :512]
+                quant["x", j] = codes[:, 512:], scales[:, 512:]
+            codes, scales = quant[j]
+            lo, hi = (0 if with_h else 512), (D if with_x else 512)
             nc.vector.quantize_mx(
-                out=codes[:, lo:hi].bitcast(X4), scales=scales[:, lo:hi], in_=hx_stage[i][:, 4 * lo : 4 * hi]
+                out=codes[:, lo:hi].bitcast(X4), scales=scales[:, lo:hi], in_=stages[j][:, 4 * lo : 4 * hi]
             )
 
-        def quant_v(i, pieces=1):
-            vq[i] = quantise("v", v_stage[i], pieces)
-
-        def views(i, s):
-            codes, scales = hxq[i - 1]
-            if i not in v_stage:
-                v_stage[i] = shared[(i + 1) % 2]
+        def views(i, q, s):
+            codes, scales = quant["h", i]
+            stages["v", i] = shared[(i + 1) % 2]
             for a in range(2):
-                bank = psum.tile([P, 512], F32, name="bank_v", bufs=3)
+                bank = new_bank()
                 for t in range(4):
                     for g in range(2):
                         w = ((4 * s + t) * 2 + g) * P
-                        c = g * 256 + a * P
+                        c = ((2 * q + g) * 2 + a) * P
                         nc.tensor.matmul_mx(
                             out=bank[:, t * P : (t + 1) * P],
                             lhsT=wv_codes[:, w : w + P].bitcast(X4),
@@ -274,162 +263,133 @@ def tile_distributedb_pa_t_kernel(tc, x_bytes, x_scale, h, Wv, W1, out):
                             start=(g == 0),
                             stop=(g == 1),
                         )
-                k = 2 * s + a
+                k = (2 * q + s) * 2 + a
                 nc.scalar.copy(
-                    out=v_stage[i][:, k * 512 : (k + 1) * 512].rearrange("p (r t) -> p r t", t=4),
+                    out=stages["v", i][:, k * 512 : (k + 1) * 512].rearrange("p (r t) -> p r t", t=4),
                     in_=bank[:].rearrange("p (t r) -> p r t", t=4),
                 )
 
-        def finish(i):
-            xc, xs = hxq[i]
-            vc, vs = vq[i]
-            bank = psum.tile([P, 512], F32, name="bank_o", bufs=1)
+        def second(dst, kind, i, c, w, n, start, stop):
+            codes, scales = quant[kind, i]
+            nc.tensor.matmul_mx(
+                out=dst,
+                lhsT=codes[:, c : c + P].bitcast(X4),
+                lhsT_scale=scales[:, c : c + P],
+                rhs=w1_codes[:, w : w + n].bitcast(X4),
+                rhs_scale=w1_sc[:, w : w + n],
+                start=start,
+                stop=stop,
+            )
+
+        def out_view(i):
+            return out_rows[:, row0[i] : row0[i + 1], :].rearrange("s (p r) f -> p s r f", p=P)
+
+        def finish(i, q):
+            bank = new_bank()
             for a in range(2):
-                for j in range(2):
-                    c = 512 + j * 256 + a * P
-                    nc.tensor.matmul_mx(
-                        out=bank[:, a * 256 : (a + 1) * 256],
-                        lhsT=xc[:, c : c + P].bitcast(X4),
-                        lhsT_scale=xs[:, c : c + P],
-                        rhs=w1_codes[:, j * 256 : (j + 1) * 256].bitcast(X4),
-                        rhs_scale=w1_sc[:, j * 256 : (j + 1) * 256],
-                        start=(j == 0),
-                        stop=False,
-                    )
+                for g in range(2):
+                    second(bank[:, a * 256 : (a + 1) * 256], "x", i, ((2 * q + g) * 2 + a) * P, g * 256, 256, g == 0, False)
                 for s in range(NS):
-                    c = (2 * s + a) * P
-                    w = (4 + s) * P
                     k = 2 * a + s
-                    nc.tensor.matmul_mx(
-                        out=bank[:, k * P : (k + 1) * P],
-                        lhsT=vc[:, c : c + P].bitcast(X4),
-                        lhsT_scale=vs[:, c : c + P],
-                        rhs=w1_codes[:, w : w + P].bitcast(X4),
-                        rhs_scale=w1_sc[:, w : w + P],
-                        start=False,
-                        stop=(s == 1),
-                    )
+                    second(bank[:, k * P : (k + 1) * P], "v", i, ((2 * q + s) * 2 + a) * P, (4 + s) * P, P, False, s == 1)
             res = stage.tile([P, 512], F32, name="res", bufs=4)
             nc.scalar.activation(
                 out=res[:].rearrange("p (s a f) -> p s a f", s=2, a=2),
                 in_=bank[:].rearrange("p (a s f) -> p s a f", s=2, a=2),
                 func=ACT.Silu,
             )
-            dst = out_rows[:, 512 * (i // 2) : 512 * (i // 2 + 1), :].rearrange("s (p c) f -> p s c f", c=4)
-            c = i % 2 * 2
             for s in range(NS):
                 nc.sync.dma_start(
-                    out=dst[:, s, c : c + 2, :],
+                    out=out_view(i)[:, s, 2 * q : 2 * q + 2, :],
                     in_=res[:, s * 256 : (s + 1) * 256].rearrange("p (a f) -> p a f", a=2),
                 )
 
-        def x_part_apart(i):
-            xc, xs = hxq[i]
+        def finish_apart(i):
             for k in range(4):
                 s, a = divmod(k, 2)
-                bank = psum.tile([P, 512], F32, name="bank_x" if k < 2 else "bank_h", bufs=2)
-                for j in range(2):
-                    c = 512 + j * 256 + a * P
-                    w = (2 * j + s) * P
-                    nc.tensor.matmul_mx(
-                        out=bank[:, 0:P],
-                        lhsT=xc[:, c : c + P].bitcast(X4),
-                        lhsT_scale=xs[:, c : c + P],
-                        rhs=w1_codes[:, w : w + P].bitcast(X4),
-                        rhs_scale=w1_sc[:, w : w + P],
-                        start=(j == 0),
-                        stop=False,
-                    )
-                banks["o", k] = bank
-
-        def finish_apart(i, pieces=1):
-            vc, vs = vq[i]
-            dst = out_rows[:, 512 * (i // 2) : 512 * (i // 2 + 1), :].rearrange("s (p c) f -> p s c f", c=4)
-            for k in range(4):
-                s, a = divmod(k, 2)
-                w = (4 + s) * P
-                nc.tensor.matmul_mx(
-                    out=banks["o", k][:, 0:P],
-                    lhsT=vc[:, k * P : (k + 1) * P].bitcast(X4),
-                    lhsT_scale=vs[:, k * P : (k + 1) * P],
-                    rhs=w1_codes[:, w : w + P].bitcast(X4),
-                    rhs_scale=w1_sc[:, w : w + P],
-                    start=False,
-                    stop=True,
-                )
+                bank = new_bank()
+                for g in range(2):
+                    second(bank[:, 0:P], "x", i, (2 * g + a) * P, (2 * g + s) * P, P, g == 0, False)
+                second(bank[:, 0:P], "v", i, k * P, (4 + s) * P, P, False, True)
                 res = stage.tile([P, P], F32, name="res_apart", bufs=4)
-                nc.scalar.activation(out=res[:], in_=banks["o", k][:, 0:P], func=ACT.Silu)
-                nc.sync.dma_start(out=dst[:, s, i % 2 * 2 + a, :], in_=res[:])
+                nc.scalar.activation(out=res[:], in_=bank[:, 0:P], func=ACT.Silu)
+                nc.sync.dma_start(out=out_view(i)[:, s, a, :], in_=res[:])
+
+        def halves(i):
+            return [(q, g) for q in range(PAIRS[i]) for g in range(2)]
 
         with tc.manual_schedule():
-            load_wv(0, 0)
             load_x(0)
-            for t in range(1, 4):
+            for t in range(4):
                 load_wv(0, t)
             load_h(0)
             for t in range(4):
                 load_wv(1, t)
             load_h(1)
-            load_x(1)
             for s in range(NS):
                 load_w1(s)
-            for i in (2, 4, 6):
-                load_h(i, 2)
-                load_x(i, 2)
-            widen_x(0, 4)
+            load_x(1)
+            load_h(2)
+            load_x(2)
+            load_h(3)
+            load_x(3)
+            widen_x(0)
             for t in range(4):
                 turn_wv(0, t)
                 copy_wv(0, t)
                 if t == 1:
-                    turn_x(0, 0)
-                    scale_x(0, 0)
-                if t % 2 == 1:
-                    quant_wv(0, t // 2)
+                    for g in range(2):
+                        turn_rows("x", 0, 0, g)
+                        scale_x(0, 0, g)
             for g in range(2):
-                turn_h(0, g)
-                copy_h(0, g, g == 1)
-            quant_hx(-1, "h")
-            turn_x(0, 1)
-            scale_x(0, 1)
+                quant_wv(0, g)
+                turn_rows("h", 0, 0, g)
+                copy_h(0, 0, g)
+            quantise_hx(-1, with_x=False)
             for t in range(4):
                 turn_wv(1, t)
                 copy_wv(1, t)
-                if t % 2 == 1:
-                    quant_wv(1, t // 2)
-            views(0, 0)
+            sort_h(1, nc.vector, stage.tile([P, 2 * D], BF16, name="h1_sorted", bufs=1, align_bytes=256))
             for g in range(2):
-                turn_h(1, g)
-                copy_h(1, g)
-            widen_x(1, 4)
-            quant_hx(0)
-            views(0, 1)
+                quant_wv(1, g)
+            views(0, 0, 0)
+            widen_x(1)
+            for g in range(2):
+                turn_rows("h", 1, 0, g)
+                copy_h(1, 0, g)
             for j in range(3):
                 turn_w1(j)
                 copy_w1(j)
+            sort_h(2, nc.vector)
+            quantise_hx(0)
+            views(0, 0, 1)
             quant_w1(0, 2)
             quant_w1(2, 3)
-            widen_x_rest(2)
+            widen_x_plain(2)
             for i in range(1, STEPS):
                 more = i + 1 < STEPS
-                prefetch(i)
-                quant_v(i - 1)
-                if i + 2 < STEPS:
+                if i + 3 < STEPS:
+                    load_h(i + 3)
+                    load_x(i + 3)
+                quantise("v", i - 1)
+                if more:
                     sort_h(i + 2)
-                for g in range(2):
-                    turn_x(i, g)
-                for g in range(2):
-                    if more:
-                        turn_h(i + 1, g)
-                        copy_h(i + 1, g)
-                    scale_x(i, g)
+                for q, g in halves(i):
+                    turn_rows("x", i, q, g)
+                    scale_x(i, q, g)
+                if more:
+                    for q, g in halves(i + 1):
+                        turn_rows("h", i + 1, q, g)
+                        copy_h(i + 1, q, g)
                 if more:
                     widen_x(i + 1)
-                for s in range(NS):
-                    views(i, s)
-                quant_hx(i)
-                finish(i - 1)
+                for q in range(PAIRS[i]):
+                    for s in range(NS):
+                        views(i, q, s)
+                quantise_hx(i, with_h=more)
+                for q in range(PAIRS[i - 1]):
+                    finish(i - 1, q)
                 if i + 2 < STEPS:
-                    widen_x_rest(i + 2)
-            x_part_apart(STEPS - 1)
-            quant_v(STEPS - 1, 4)
+                    widen_x_plain(i + 2)
+            quantise("v", STEPS - 1, 4)
             finish_apart(STEPS - 1)

@@ -17,9 +17,10 @@ ACT = mybir.ActivationFunctionType
 P = 128
 D = 1024
 NS = 2
-PAIRS = (1,) * 16
+PAIRS = (1, 1, 1, 2, 2, 2, 2, 2, 2, 1)
 STEPS = len(PAIRS)
-S_BLOCKS = {1: 1}
+S_BLOCKS = {1: 1, 2: 3}
+G_BLOCKS = {1: 5, 2: 11}
 
 
 def tile_distributedb_pa_t_kernel(tc, x_bytes, x_scale, h, Wv, W1, out):
@@ -63,8 +64,7 @@ def tile_distributedb_pa_t_kernel(tc, x_bytes, x_scale, h, Wv, W1, out):
         shared = [keep.tile([P, wide], BF16, name="shared%d" % n, align_bytes=256) for n in range(2)]
 
         wv_raw, w1_raw, h_raw, x_raw = {}, {}, {}, {}
-        in_order = {}
-        wv_stage, x_wide, stages, quant, banks = {}, {}, {}, {}, {}
+        wv_stage, place, stages, quant, banks = {}, {}, {}, {}, {}
 
         def new_bank():
             return psum.tile([P, 512], F32, name="bank")
@@ -80,14 +80,20 @@ def tile_distributedb_pa_t_kernel(tc, x_bytes, x_scale, h, Wv, W1, out):
             w1_raw[s] = w
 
         def load_h(i):
-            h_raw[i] = raw.tile([P, wide], BF16, name="h_raw", align_bytes=256)
+            h_raw[i] = raw.tile([P, wide], BF16, name="h_raw", align_bytes=256, bufs=4)
+            if i == STEPS:
+                return
             src = h_rows[row0[i] : row0[i + 1], :].rearrange("(p r) k -> p r k", p=P)
             if i > 0:
                 nc.sync.dma_start(out=h_raw[i][:, : h_blocks(i) * 512], in_=src.rearrange("p r k -> p (r k)"))
+                for b in range(h_blocks(i)):
+                    place["h", i, b] = h_raw[i], None, b
                 return
             for g in range(2):
                 dst = h_raw[i][:, g * D : (g + 1) * D].rearrange("p (r k) -> p r k", k=512)
                 nc.sync.dma_start(out=dst, in_=src[:, :, g * 512 : (g + 1) * 512])
+                for a in range(2):
+                    place["h", i, 2 * a + g] = h_raw[i], None, 2 * g + a
 
         def load_x(i):
             x_raw[i] = raw.tile([P, 4 * D], U8, name="x_raw")
@@ -151,58 +157,48 @@ def tile_distributedb_pa_t_kernel(tc, x_bytes, x_scale, h, Wv, W1, out):
             )
 
         def widen_x(i):
-            n = (4 * PAIRS[i] - plain_blocks(i)) * 512
-            x_wide[i] = stage.tile([P, 4 * D], BF16, name="x_wide", align_bytes=256)
+            blocks = 4 * PAIRS[i] - plain_blocks(i)
+            w = stage.tile([P, blocks * 512], BF16, name="x_wide", align_bytes=256)
             nc.vector.tensor_scalar(
-                out=x_wide[i][:, :n].rearrange("p (u n e) -> p n u e", u=2, e=2),
-                in0=x_raw[i][:, :n].bitcast(F8).rearrange("p (n u e) -> p n u e", u=2, e=2),
+                out=w[:].rearrange("p (u n e) -> p n u e", u=2, e=2),
+                in0=x_raw[i][:, : blocks * 512].bitcast(F8).rearrange("p (n u e) -> p n u e", u=2, e=2),
                 scalar1=ones[:, 0:1],
                 scalar2=None,
                 op0=MULT,
             )
+            for b in range(blocks):
+                place["x", i, b] = w, blocks, b
 
         def widen_x_plain(i):
-            n = plain_blocks(i) * 512
-            if i + 1 == STEPS:
-                h_raw[i + 1] = raw.tile([P, wide], BF16, name="h_raw", align_bytes=256)
-            end, c = PAIRS[i] * 2 * D, h_blocks(i + 1) * 512
-            nc.scalar.copy(out=h_raw[i + 1][:, c : c + n], in_=x_raw[i][:, end - n : end].bitcast(F8))
-
-        def sort_words(engine, dst, src, blocks):
-            engine.tensor_copy(
-                out=dst[:, : blocks * 512].bitcast(F32).rearrange("p (u n) -> p u n", u=2),
-                in_=src[:, : blocks * 512].bitcast(F32).rearrange("p (n u) -> p u n", u=2),
+            first, c = 4 * PAIRS[i] - plain_blocks(i), h_blocks(i + 1)
+            nc.scalar.copy(
+                out=h_raw[i + 1][:, c * 512 : (c + plain_blocks(i)) * 512],
+                in_=x_raw[i][:, first * 512 : 4 * PAIRS[i] * 512].bitcast(F8),
             )
+            for b in range(plain_blocks(i)):
+                place["x", i, first + b] = h_raw[i + 1], None, c + b
 
-        def sort_h(i, engine=nc.gpsimd, dst=None):
-            in_order[i] = dst if dst is not None else shared[i % 2], h_blocks(i) + plain_blocks(i - 1)
-            sort_words(engine, in_order[i][0], h_raw[i], in_order[i][1])
-
-        def sort_w1(s, engine):
-            in_order["1", s] = wpool.tile([P, 1536], BF16, name="w1_sorted")
-            sort_words(engine, in_order["1", s], w1_raw[s], 3)
+        def sort_words(i, engine, dst, blocks):
+            keys = [key for key, (tile, order, n) in place.items() if tile is h_raw[i]][:blocks]
+            engine.tensor_copy(
+                out=dst[:, : len(keys) * 512].bitcast(F32).rearrange("p (u n) -> p u n", u=2),
+                in_=h_raw[i][:, : len(keys) * 512].bitcast(F32).rearrange("p (n u) -> p u n", u=2),
+            )
+            for n, key in enumerate(keys):
+                place[key] = dst, len(keys), n
 
         def words_of(kind, i, block, u):
-            if kind == "h":
-                if i == 0:
-                    return every_second(h_raw[i], block % 2 * 2 + block // 2, u)
-                if i not in in_order:
-                    return every_second(h_raw[i], block, u)
-                return in_a_row(*in_order[i], block, u)
-            first_plain = 4 * PAIRS[i] - plain_blocks(i)
-            if block < first_plain:
-                return in_a_row(x_wide[i], first_plain, block, u)
-            return in_a_row(*in_order[i + 1], h_blocks(i + 1) + block - first_plain, u)
+            tile, blocks, n = place[kind, i, block]
+            return every_second(tile, n, u) if blocks is None else in_a_row(tile, blocks, n, u)
 
         def turn_rows(kind, i, q, g):
             turn((kind, i, q, g), [words_of(kind, i, 2 * (2 * q + a) + g, u) for u in range(2) for a in range(2)])
 
         def stage_part(kind, i, q, g):
-            j = i - 1 if kind == "h" else i
-            if j not in stages:
-                stages[j] = stage.tile([P, 4 * D], BF16, name="hx_stage", align_bytes=256, bufs=3)
-            c = (g if kind == "h" else 2 + g) * D
-            return stages[j][:, c : c + D]
+            if (kind, i) not in stages:
+                stages[kind, i] = stage.tile([P, 4 * D], BF16, name=kind + "_stage", align_bytes=256)
+            c = (2 * q + g) * D
+            return stages[kind, i][:, c : c + D]
 
         def copy_h(i, q, g, on_vector=False):
             copy_words(
@@ -220,30 +216,19 @@ def tile_distributedb_pa_t_kernel(tc, x_bytes, x_scale, h, Wv, W1, out):
                 op=MULT,
             )
 
-        def quantise(kind, i, pieces=1):
-            codes = stage.tile([P, D], U32, name=kind + "_codes", align_bytes=256, bufs=2)
-            scales = stage.tile([P, D], U8, name=kind + "_scales", align_bytes=256, bufs=2)
+        def quantise(kind, i, pieces=1, only=None):
+            if (kind, i) not in quant:
+                codes = stage.tile([P, D], U32, name=kind + "_codes", align_bytes=256)
+                scales = stage.tile([P, D], U8, name=kind + "_scales", align_bytes=256)
+                quant[kind, i] = codes, scales
+            codes, scales = quant[kind, i]
             n = PAIRS[i] * 512 // pieces
-            for k in range(pieces):
+            for k in only or range(pieces):
                 nc.vector.quantize_mx(
                     out=codes[:, k * n : (k + 1) * n].bitcast(X4),
                     scales=scales[:, k * n : (k + 1) * n],
                     in_=stages[kind, i][:, 4 * k * n : 4 * (k + 1) * n],
                 )
-            quant[kind, i] = codes, scales
-
-        def quantise_hx(j, with_h=True, with_x=True):
-            if j not in quant:
-                codes = stage.tile([P, D], U32, name="hx_codes", align_bytes=256, bufs=3)
-                scales = stage.tile([P, D], U8, name="hx_scales", align_bytes=256, bufs=3)
-                quant[j] = codes, scales
-                quant["h", j + 1] = codes[:, :512], scales[:, :512]
-                quant["x", j] = codes[:, 512:], scales[:, 512:]
-            codes, scales = quant[j]
-            lo, hi = (0 if with_h else 512), (D if with_x else 512)
-            nc.vector.quantize_mx(
-                out=codes[:, lo:hi].bitcast(X4), scales=scales[:, lo:hi], in_=stages[j][:, 4 * lo : 4 * hi]
-            )
 
         def views(i, q, s):
             codes, scales = quant["h", i]
@@ -298,22 +283,21 @@ def tile_distributedb_pa_t_kernel(tc, x_bytes, x_scale, h, Wv, W1, out):
                 in_=bank[:].rearrange("p (a s f) -> p s a f", s=2, a=2),
                 func=ACT.Silu,
             )
-            for s in range(NS):
-                nc.sync.dma_start(
-                    out=out_view(i)[:, s, 2 * q : 2 * q + 2, :],
-                    in_=res[:, s * 256 : (s + 1) * 256].rearrange("p (a f) -> p a f", a=2),
-                )
+            nc.sync.dma_start(
+                out=out_view(i)[:, :, 2 * q : 2 * q + 2, :].rearrange("p s a f -> p s (a f)"),
+                in_=res[:].rearrange("p (s c) -> p s c", s=2),
+            )
 
-        def finish_apart(i):
+        def finish_apart(i, q):
             for k in range(4):
                 s, a = divmod(k, 2)
                 bank = new_bank()
                 for g in range(2):
-                    second(bank[:, 0:P], "x", i, (2 * g + a) * P, (2 * g + s) * P, P, g == 0, False)
-                second(bank[:, 0:P], "v", i, k * P, (4 + s) * P, P, False, True)
+                    second(bank[:, 0:P], "x", i, ((2 * q + g) * 2 + a) * P, (2 * g + s) * P, P, g == 0, False)
+                second(bank[:, 0:P], "v", i, (4 * q + k) * P, (4 + s) * P, P, False, True)
                 res = stage.tile([P, P], F32, name="res_apart", bufs=4)
                 nc.scalar.activation(out=res[:], in_=bank[:, 0:P], func=ACT.Silu)
-                nc.sync.dma_start(out=out_view(i)[:, s, a, :], in_=res[:])
+                nc.sync.dma_start(out=out_view(i)[:, s, 2 * q + a, :], in_=res[:])
 
         def halves(i):
             return [(q, g) for q in range(PAIRS[i]) for g in range(2)]
@@ -345,11 +329,11 @@ def tile_distributedb_pa_t_kernel(tc, x_bytes, x_scale, h, Wv, W1, out):
                 quant_wv(0, g)
                 turn_rows("h", 0, 0, g)
                 copy_h(0, 0, g)
-            quantise_hx(-1, with_x=False)
+            quantise("h", 0)
             for t in range(4):
                 turn_wv(1, t)
                 copy_wv(1, t)
-            sort_h(1, nc.vector, stage.tile([P, 2 * D], BF16, name="h1_sorted", bufs=1, align_bytes=256))
+            sort_words(1, nc.vector, shared[0], 4)
             for g in range(2):
                 quant_wv(1, g)
             views(0, 0, 0)
@@ -359,37 +343,45 @@ def tile_distributedb_pa_t_kernel(tc, x_bytes, x_scale, h, Wv, W1, out):
                 copy_h(1, 0, g)
             for j in range(3):
                 turn_w1(j)
-                copy_w1(j)
-            sort_h(2, nc.vector)
-            quantise_hx(0)
+                if j == 0:
+                    sort_words(2, nc.vector, shared[0], 4)
+                copy_w1(j, j == 0)
+            quantise("h", 1)
             views(0, 0, 1)
+            quantise("x", 0)
             quant_w1(0, 2)
             quant_w1(2, 3)
             widen_x_plain(2)
             for i in range(1, STEPS):
                 more = i + 1 < STEPS
-                if i + 3 < STEPS:
+                if i + 3 <= STEPS:
                     load_h(i + 3)
+                if i + 3 < STEPS:
                     load_x(i + 3)
                 quantise("v", i - 1)
                 if more:
-                    sort_h(i + 2)
-                for q, g in halves(i):
-                    turn_rows("x", i, q, g)
-                    scale_x(i, q, g)
-                if more:
+                    sort_words(i + 2, nc.gpsimd, shared[i % 2], G_BLOCKS[PAIRS[i]])
                     for q, g in halves(i + 1):
                         turn_rows("h", i + 1, q, g)
                         copy_h(i + 1, q, g)
+                if i + 2 < STEPS:
+                    widen_x_plain(i + 2)
+                for q, g in halves(i):
+                    turn_rows("x", i, q, g)
+                    scale_x(i, q, g)
                 if more:
                     widen_x(i + 1)
                 for q in range(PAIRS[i]):
                     for s in range(NS):
                         views(i, q, s)
-                quantise_hx(i, with_h=more)
+                if more:
+                    quantise("h", i + 1)
+                quantise("x", i)
                 for q in range(PAIRS[i - 1]):
                     finish(i - 1, q)
-                if i + 2 < STEPS:
-                    widen_x_plain(i + 2)
-            quantise("v", STEPS - 1, 4)
-            finish_apart(STEPS - 1)
+            last = STEPS - 1
+            for q in range(PAIRS[last] - 1):
+                quantise("v", last, PAIRS[last], (q,))
+                finish(last, q)
+            quantise("v", last, 4 * PAIRS[last], range(4 * PAIRS[last] - 4, 4 * PAIRS[last]))
+            finish_apart(last, PAIRS[last] - 1)

@@ -55,6 +55,9 @@ def tile_distributedb_pa_t_kernel(tc, x_bytes, x_scale, h, Wv, W1, out):
         warm = keep.tile([P, 1], F32, name="warm")
         nc.scalar.activation(out=warm[:], in_=ones[:], func=ACT.Silu)
 
+        zeros = keep.tile([P, 512], BF16, name="zeros", align_bytes=64)
+        nc.vector.memset(zeros[:], 0.0)
+
         wv_codes = keep.tile([P, 4 * 512], U32, name="wv_codes", align_bytes=256)
         wv_sc = keep.tile([P, 4 * 512], U8, name="wv_sc", align_bytes=256)
         w1_codes = keep.tile([P, 6 * P], U32, name="w1_codes", align_bytes=256)
@@ -69,10 +72,11 @@ def tile_distributedb_pa_t_kernel(tc, x_bytes, x_scale, h, Wv, W1, out):
         def new_bank():
             return psum.tile([P, 512], F32, name="bank")
 
-        def load_wv(s, t):
-            w = wpool.tile([P, D], BF16, name="wv_raw", bufs=8)
-            nc.sync.dma_start(out=w[:], in_=Wv[s].rearrange("(m t) k -> m t k", t=4)[:, t, :])
-            wv_raw[s, t] = w
+        def load_wv(s, t, n):
+            w = keep.tile([P, n * D], BF16, name="wv_raw%d%d" % (s, t))
+            nc.sync.dma_start(out=w[:], in_=Wv[s].rearrange("(m t) k -> m (t k)", t=4)[:, t * D : (t + n) * D])
+            for j in range(n):
+                wv_raw[s, t + j] = w, j
 
         def load_w1(s):
             w = wpool.tile([P, 1536], BF16, name="w1_raw")
@@ -120,7 +124,8 @@ def tile_distributedb_pa_t_kernel(tc, x_bytes, x_scale, h, Wv, W1, out):
             banks[key] = bank
 
         def turn_wv(s, t):
-            turn(("w", s, t), [every_second(wv_raw[s, t], g, u) for g in range(2) for u in range(2)])
+            w, j = wv_raw[s, t]
+            turn(("w", s, t), [every_second(w, 2 * j + g, u) for g in range(2) for u in range(2)])
 
         def copy_wv(s, t, on_vector=False):
             if t % 2 == 0:
@@ -304,11 +309,11 @@ def tile_distributedb_pa_t_kernel(tc, x_bytes, x_scale, h, Wv, W1, out):
 
         with tc.manual_schedule():
             load_x(0)
-            for t in range(4):
-                load_wv(0, t)
+            for t, n in ((0, 1), (1, 1), (2, 2)):
+                load_wv(0, t, n)
             load_h(0)
-            for t in range(4):
-                load_wv(1, t)
+            for t in (0, 2):
+                load_wv(1, t, 2)
             load_h(1)
             for s in range(NS):
                 load_w1(s)
@@ -317,6 +322,9 @@ def tile_distributedb_pa_t_kernel(tc, x_bytes, x_scale, h, Wv, W1, out):
             load_x(2)
             load_h(3)
             load_x(3)
+            idle = new_bank()
+            for n in range(5):
+                nc.tensor.matmul(idle[:], lhsT=zeros[:, :P], rhs=zeros[:], start=True, stop=True)
             widen_x(0)
             for t in range(4):
                 turn_wv(0, t)

@@ -55,9 +55,6 @@ def tile_distributedb_pa_t_kernel(tc, x_bytes, x_scale, h, Wv, W1, out):
         warm = keep.tile([P, 1], F32, name="warm")
         nc.scalar.activation(out=warm[:], in_=ones[:], func=ACT.Silu)
 
-        zeros = keep.tile([P, 512], BF16, name="zeros", align_bytes=64)
-        nc.vector.memset(zeros[:], 0.0)
-
         wv_codes = keep.tile([P, 4 * 512], U32, name="wv_codes", align_bytes=256)
         wv_sc = keep.tile([P, 4 * 512], U8, name="wv_sc", align_bytes=256)
         w1_codes = keep.tile([P, 6 * P], U32, name="w1_codes", align_bytes=256)
@@ -322,9 +319,6 @@ def tile_distributedb_pa_t_kernel(tc, x_bytes, x_scale, h, Wv, W1, out):
             load_x(2)
             load_h(3)
             load_x(3)
-            idle = new_bank()
-            for n in range(5):
-                nc.tensor.matmul(idle[:], lhsT=zeros[:, :P], rhs=zeros[:], start=True, stop=True)
             widen_x(0)
             for t in range(4):
                 turn_wv(0, t)

@@ -18,9 +18,12 @@ P = 128
 D = 1024
 NS = 2
 PAIRS = (1, 1, 1, 2, 2, 2, 2, 2, 2, 1)
+X_PAIRS = (0, 1, 1, 1, 2, 2, 2, 2, 2, 2, 1)
+WIDE = (0,0,0,0,0,0,0,0,2,1)
+V_BLOCKS = (0,)*10
 STEPS = len(PAIRS)
-S_BLOCKS = {1: 1, 2: 3}
-G_BLOCKS = {1: 5, 2: 11}
+S_BLOCKS = (0,0,0,1,3,3,3,3,3,4,2)
+G_BLOCKS = (0,5,5,11,11,11,11,11,11)
 
 
 def tile_distributedb_pa_t_kernel(tc, x_bytes, x_scale, h, Wv, W1, out):
@@ -28,10 +31,12 @@ def tile_distributedb_pa_t_kernel(tc, x_bytes, x_scale, h, Wv, W1, out):
     x_rows = x_bytes.rearrange("b r k -> (b r) k")
     h_rows = h.rearrange("b r k -> (b r) k")
     out_rows = out.rearrange("s b r f -> s (b r) f")
-    row0 = [256 * sum(PAIRS[:i]) for i in range(STEPS + 1)]
+    pairs = {"h": PAIRS, "v": PAIRS, "x": X_PAIRS}
+    first = {kind: [sum(n[:i]) for i in range(len(n) + 1)] for kind, n in pairs.items()}
+    x_place = [(i, q) for i in range(STEPS + 1) for q in range(X_PAIRS[i])]
 
     def plain_blocks(i):
-        return S_BLOCKS[PAIRS[i]] if 2 <= i < STEPS else 0
+        return S_BLOCKS[i]
 
     def h_blocks(i):
         return 4 * PAIRS[i] if i < STEPS else 0
@@ -44,10 +49,6 @@ def tile_distributedb_pa_t_kernel(tc, x_bytes, x_scale, h, Wv, W1, out):
         psum = ctx.enter_context(tc.psum_pool(name="psum", bufs=8))
 
         scale = keep.tile([P, 8], F32, name="scale")
-        nc.scalar.dma_start(
-            out=scale[:].rearrange("p (g t) -> p g t", g=2),
-            in_=x_scale.rearrange("o b (g p t) -> p (o b g) t", g=2, p=P, t=4),
-        )
         ident = keep.tile([P, P], F32, name="ident", align_bytes=64)
         make_identity(nc, ident[:])
         ones = keep.tile([P, 1], F32, name="ones")
@@ -60,8 +61,9 @@ def tile_distributedb_pa_t_kernel(tc, x_bytes, x_scale, h, Wv, W1, out):
         w1_codes = keep.tile([P, 6 * P], U32, name="w1_codes", align_bytes=256)
         w1_sc = keep.tile([P, 6 * P], U8, name="w1_sc", align_bytes=256)
         w1_stage = keep.tile([P, 6 * P * 4], BF16, name="w1_stage", align_bytes=256)
-        wide = max(h_blocks(i + 1) + plain_blocks(i) for i in range(STEPS)) * 512
+        wide = max(h_blocks(i) + plain_blocks(i) for i in range(STEPS + 1)) * 512
         shared = [keep.tile([P, wide], BF16, name="shared%d" % n, align_bytes=256) for n in range(2)]
+
 
         wv_raw, w1_raw, h_raw, x_raw = {}, {}, {}, {}
         wv_stage, place, stages, quant, banks = {}, {}, {}, {}, {}
@@ -72,34 +74,38 @@ def tile_distributedb_pa_t_kernel(tc, x_bytes, x_scale, h, Wv, W1, out):
         def load_wv(s, t, n):
             w = keep.tile([P, n * D], BF16, name="wv_raw%d%d" % (s, t))
             nc.sync.dma_start(out=w[:], in_=Wv[s].rearrange("(m t) k -> m (t k)", t=4)[:, t * D : (t + n) * D])
-            for j in range(n):
-                wv_raw[s, t + j] = w, j
+            for b in range(2 * n):
+                place["wv", s, 2 * t + b] = w, None, b
+            wv_raw[s, t] = w
+
+        def load_scale(engine):
+            engine.dma_start(
+                out=scale[:].rearrange("p (g t) -> p g t", g=2),
+                in_=x_scale.rearrange("o b (g p t) -> p (o b g) t", g=2, p=P, t=4),
+            )
 
         def load_w1(s):
             w = wpool.tile([P, 1536], BF16, name="w1_raw")
             nc.sync.dma_start(out=w[:], in_=W1[s])
+            for j in range(3):
+                place["w1", s, j] = w, None, j
             w1_raw[s] = w
 
         def load_h(i):
             h_raw[i] = raw.tile([P, wide], BF16, name="h_raw", align_bytes=256, bufs=4)
             if i == STEPS:
                 return
-            src = h_rows[row0[i] : row0[i + 1], :].rearrange("(p r) k -> p r k", p=P)
-            if i > 0:
-                nc.sync.dma_start(out=h_raw[i][:, : h_blocks(i) * 512], in_=src.rearrange("p r k -> p (r k)"))
-                for b in range(h_blocks(i)):
-                    place["h", i, b] = h_raw[i], None, b
-                return
-            for g in range(2):
-                dst = h_raw[i][:, g * D : (g + 1) * D].rearrange("p (r k) -> p r k", k=512)
-                nc.sync.dma_start(out=dst, in_=src[:, :, g * 512 : (g + 1) * 512])
-                for a in range(2):
-                    place["h", i, 2 * a + g] = h_raw[i], None, 2 * g + a
+            rows = h_rows[256 * first["h"][i] : 256 * first["h"][i + 1], :]
+            dst = h_raw[i][:, : h_blocks(i) * 512].rearrange("p (q c) -> p q c", c=2 * D)
+            nc.sync.dma_start(out=dst, in_=rows.rearrange("(q p r) k -> p q (r k)", p=P, r=2))
+            for b in range(h_blocks(i)):
+                place["h", i, b] = h_raw[i], None, b
 
         def load_x(i):
-            x_raw[i] = raw.tile([P, 4 * D], U8, name="x_raw")
-            src = x_rows[row0[i] : row0[i + 1], :].rearrange("(p r) k -> p (r k)", p=P)
-            nc.sync.dma_start(out=x_raw[i][:, : PAIRS[i] * 2 * D], in_=src)
+            x_raw[i] = raw.tile([P, 4 * D], U8, name="x_raw", bufs=4)
+            rows = x_rows[256 * first["x"][i] : 256 * first["x"][i + 1], :]
+            dst = x_raw[i][:, : X_PAIRS[i] * 2 * D].rearrange("p (q c) -> p q c", c=2 * D)
+            nc.sync.dma_start(out=dst, in_=rows.rearrange("(q p r) k -> p q (r k)", p=P, r=2))
 
         def copy_words(on_vector, dst, src):
             if on_vector:
@@ -110,9 +116,9 @@ def tile_distributedb_pa_t_kernel(tc, x_bytes, x_scale, h, Wv, W1, out):
         def every_second(tile, block, u):
             return tile[:].bitcast(F32)[:, 256 * block + u : 256 * (block + 1) : 2]
 
-        def in_a_row(tile, blocks, block, u):
+        def in_a_row(part, blocks, block, u):
             c = (u * blocks + block) * P
-            return tile[:].bitcast(F32)[:, c : c + P]
+            return part.bitcast(F32)[:, c : c + P]
 
         def turn(key, parts):
             bank = new_bank()
@@ -121,27 +127,24 @@ def tile_distributedb_pa_t_kernel(tc, x_bytes, x_scale, h, Wv, W1, out):
             banks[key] = bank
 
         def turn_wv(s, t):
-            w, j = wv_raw[s, t]
-            turn(("w", s, t), [every_second(w, 2 * j + g, u) for g in range(2) for u in range(2)])
+            turn(("w", s, t), [words_of("wv", s, 2 * t + g, u) for g in range(2) for u in range(2)])
 
         def copy_wv(s, t, on_vector=False):
-            if t % 2 == 0:
-                wv_stage[s, t // 2] = wpool.tile([P, 2 * D], BF16, name="wv_stage", align_bytes=256, bufs=3)
-            dst = wv_stage[s, t // 2][:, t % 2 * D : (t % 2 + 1) * D].bitcast(F32)
+            wv_stage[s, t] = wpool.tile([P, D], BF16, name="wv_stage", align_bytes=256, bufs=4)
             copy_words(
                 on_vector,
-                dst.rearrange("p (g m u) -> p g m u", g=2, u=2),
+                wv_stage[s, t][:].bitcast(F32).rearrange("p (g m u) -> p g m u", g=2, u=2),
                 banks["w", s, t][:].rearrange("p (g u m) -> p g m u", g=2, u=2),
             )
 
-        def quant_wv(s, half):
-            c = (2 * s + half) * 512
+        def quant_wv(s, t):
+            c = (4 * s + t) * 256
             nc.vector.quantize_mx(
-                out=wv_codes[:, c : c + 512].bitcast(X4), scales=wv_sc[:, c : c + 512], in_=wv_stage[s, half][:]
+                out=wv_codes[:, c : c + 256].bitcast(X4), scales=wv_sc[:, c : c + 256], in_=wv_stage[s, t][:]
             )
 
         def turn_w1(j):
-            turn(("1", j), [every_second(w1_raw[s], j, u) for s in range(NS) for u in range(2)])
+            turn(("1", j), [words_of("w1", s, j, u) for s in range(NS) for u in range(2)])
 
         def copy_w1(j, on_vector=False):
             dst = w1_stage[:, j * D : (j + 1) * D].bitcast(F32)
@@ -159,7 +162,7 @@ def tile_distributedb_pa_t_kernel(tc, x_bytes, x_scale, h, Wv, W1, out):
             )
 
         def widen_x(i):
-            blocks = 4 * PAIRS[i] - plain_blocks(i)
+            blocks = 4 * X_PAIRS[i] - plain_blocks(i)
             w = stage.tile([P, blocks * 512], BF16, name="x_wide", align_bytes=256)
             nc.vector.tensor_scalar(
                 out=w[:].rearrange("p (u n e) -> p n u e", u=2, e=2),
@@ -169,25 +172,30 @@ def tile_distributedb_pa_t_kernel(tc, x_bytes, x_scale, h, Wv, W1, out):
                 op0=MULT,
             )
             for b in range(blocks):
-                place["x", i, b] = w, blocks, b
+                place["x", i, b] = w[:], blocks, b
 
         def widen_x_plain(i):
-            first, c = 4 * PAIRS[i] - plain_blocks(i), h_blocks(i + 1)
+            lo = 4 * X_PAIRS[i] - plain_blocks(i)
+            tile, c = h_raw[i], h_blocks(i)
             nc.scalar.copy(
-                out=h_raw[i + 1][:, c * 512 : (c + plain_blocks(i)) * 512],
-                in_=x_raw[i][:, first * 512 : 4 * PAIRS[i] * 512].bitcast(F8),
+                out=tile[:, c * 512 : (c + plain_blocks(i)) * 512],
+                in_=x_raw[i][:, lo * 512 : 4 * X_PAIRS[i] * 512].bitcast(F8),
             )
             for b in range(plain_blocks(i)):
-                place["x", i, first + b] = h_raw[i + 1], None, c + b
+                place["x", i, lo + b] = tile, None, c + b
 
-        def sort_words(i, engine, dst, blocks):
-            keys = [key for key, (tile, order, n) in place.items() if tile is h_raw[i]][:blocks]
+        def sort_words(engine, src, blocks, dst, at=0):
+            keys = [key for key, (tile, order, n) in place.items() if tile is src][:blocks]
+            if not keys:
+                return
+            lo = place[keys[0]][2]
+            part = dst[:, at * 512 : (at + len(keys)) * 512]
             engine.tensor_copy(
-                out=dst[:, : len(keys) * 512].bitcast(F32).rearrange("p (u n) -> p u n", u=2),
-                in_=h_raw[i][:, : len(keys) * 512].bitcast(F32).rearrange("p (n u) -> p u n", u=2),
+                out=part.bitcast(F32).rearrange("p (u n) -> p u n", u=2),
+                in_=src[:, lo * 512 : (lo + len(keys)) * 512].bitcast(F32).rearrange("p (n u) -> p u n", u=2),
             )
             for n, key in enumerate(keys):
-                place[key] = dst, len(keys), n
+                place[key] = part, len(keys), n
 
         def words_of(kind, i, block, u):
             tile, blocks, n = place[kind, i, block]
@@ -220,11 +228,12 @@ def tile_distributedb_pa_t_kernel(tc, x_bytes, x_scale, h, Wv, W1, out):
 
         def quantise(kind, i, pieces=1, only=None):
             if (kind, i) not in quant:
-                codes = stage.tile([P, D], U32, name=kind + "_codes", align_bytes=256)
-                scales = stage.tile([P, D], U8, name=kind + "_scales", align_bytes=256)
+                bufs = 2
+                codes = stage.tile([P, D], U32, name=kind + "_codes", align_bytes=256, bufs=bufs)
+                scales = stage.tile([P, D], U8, name=kind + "_scales", align_bytes=256, bufs=bufs)
                 quant[kind, i] = codes, scales
             codes, scales = quant[kind, i]
-            n = PAIRS[i] * 512 // pieces
+            n = pairs[kind][i] * 512 // pieces
             for k in only or range(pieces):
                 nc.vector.quantize_mx(
                     out=codes[:, k * n : (k + 1) * n].bitcast(X4),
@@ -232,12 +241,14 @@ def tile_distributedb_pa_t_kernel(tc, x_bytes, x_scale, h, Wv, W1, out):
                     in_=stages[kind, i][:, 4 * k * n : 4 * (k + 1) * n],
                 )
 
-        def views(i, q, s):
+        def views(i, q, s, groups=range(4)):
             codes, scales = quant["h", i]
             stages["v", i] = shared[(i + 1) % 2]
             for a in range(2):
-                bank = new_bank()
-                for t in range(4):
+                if groups[0] == 0:
+                    banks["v", a] = new_bank()
+                bank = banks["v", a]
+                for t in groups:
                     for g in range(2):
                         w = ((4 * s + t) * 2 + g) * P
                         c = ((2 * q + g) * 2 + a) * P
@@ -250,11 +261,34 @@ def tile_distributedb_pa_t_kernel(tc, x_bytes, x_scale, h, Wv, W1, out):
                             start=(g == 0),
                             stop=(g == 1),
                         )
-                k = (2 * q + s) * 2 + a
-                nc.scalar.copy(
-                    out=stages["v", i][:, k * 512 : (k + 1) * 512].rearrange("p (r t) -> p r t", t=4),
-                    in_=bank[:].rearrange("p (t r) -> p r t", t=4),
-                )
+                if groups[-1] == 3:
+                    k = (2 * q + s) * 2 + a
+                    nc.scalar.copy(
+                        out=stages["v", i][:, k * 512 : (k + 1) * 512].rearrange("p (r t) -> p r t", t=4),
+                        in_=bank[:].rearrange("p (t r) -> p r t", t=4),
+                    )
+
+        def views_wide(i, q, s):
+            codes, scales = quant["h", i]
+            stages["v", i] = shared[(i + 1) % 2]
+            k = (2 * q + s) * 2
+            dst = stages["v", i][:, k * 512 : (k + 2) * 512].rearrange("p (n j e) -> p n j e", j=2, e=2)
+            for j in range(2):
+                bank = new_bank()
+                for e in range(2):
+                    for g in range(2):
+                        w = ((4 * s + 2 * j + e) * 2 + g) * P
+                        c = (2 * q + g) * 256
+                        nc.tensor.matmul_mx(
+                            out=bank[:, e * 256 : (e + 1) * 256],
+                            lhsT=wv_codes[:, w : w + P].bitcast(X4),
+                            lhsT_scale=wv_sc[:, w : w + P],
+                            rhs=codes[:, c : c + 256].bitcast(X4),
+                            rhs_scale=scales[:, c : c + 256],
+                            start=(g == 0),
+                            stop=(g == 1),
+                        )
+                nc.scalar.copy(out=dst[:, :, j, :], in_=bank[:].rearrange("p (e n) -> p n e", e=2))
 
         def second(dst, kind, i, c, w, n, start, stop):
             codes, scales = quant[kind, i]
@@ -268,14 +302,16 @@ def tile_distributedb_pa_t_kernel(tc, x_bytes, x_scale, h, Wv, W1, out):
                 stop=stop,
             )
 
-        def out_view(i):
-            return out_rows[:, row0[i] : row0[i + 1], :].rearrange("s (p r) f -> p s r f", p=P)
+        def out_view(i, q):
+            r = 256 * (first["h"][i] + q)
+            return out_rows[:, r : r + 256, :].rearrange("s (p a) f -> p s a f", p=P)
 
         def finish(i, q):
+            xi, xq = x_place[first["h"][i] + q]
             bank = new_bank()
             for a in range(2):
                 for g in range(2):
-                    second(bank[:, a * 256 : (a + 1) * 256], "x", i, ((2 * q + g) * 2 + a) * P, g * 256, 256, g == 0, False)
+                    second(bank[:, a * 256 : (a + 1) * 256], "x", xi, ((2 * xq + g) * 2 + a) * P, g * 256, 256, g == 0, False)
                 for s in range(NS):
                     k = 2 * a + s
                     second(bank[:, k * P : (k + 1) * P], "v", i, ((2 * q + s) * 2 + a) * P, (4 + s) * P, P, False, s == 1)
@@ -286,99 +322,116 @@ def tile_distributedb_pa_t_kernel(tc, x_bytes, x_scale, h, Wv, W1, out):
                 func=ACT.Silu,
             )
             nc.sync.dma_start(
-                out=out_view(i)[:, :, 2 * q : 2 * q + 2, :].rearrange("p s a f -> p s (a f)"),
+                out=out_view(i, q).rearrange("p s a f -> p s (a f)"),
                 in_=res[:].rearrange("p (s c) -> p s c", s=2),
             )
 
         def finish_apart(i, q):
+            xi, xq = x_place[first["h"][i] + q]
             for k in range(4):
                 s, a = divmod(k, 2)
                 bank = new_bank()
                 for g in range(2):
-                    second(bank[:, 0:P], "x", i, ((2 * q + g) * 2 + a) * P, (2 * g + s) * P, P, g == 0, False)
+                    second(bank[:, 0:P], "x", xi, ((2 * xq + g) * 2 + a) * P, (2 * g + s) * P, P, g == 0, False)
                 second(bank[:, 0:P], "v", i, (4 * q + k) * P, (4 + s) * P, P, False, True)
                 res = stage.tile([P, P], F32, name="res_apart", bufs=4)
                 nc.scalar.activation(out=res[:], in_=bank[:, 0:P], func=ACT.Silu)
-                nc.sync.dma_start(out=out_view(i)[:, s, 2 * q + a, :], in_=res[:])
+                nc.sync.dma_start(out=out_view(i, q)[:, s, a, :], in_=res[:])
 
-        def halves(i):
-            return [(q, g) for q in range(PAIRS[i]) for g in range(2)]
+        def halves(kind, i):
+            return [(q, g) for q in range(pairs[kind][i]) for g in range(2)]
 
         with tc.manual_schedule():
-            load_x(0)
-            for t, n in ((0, 1), (1, 1), (2, 2)):
-                load_wv(0, t, n)
+            load_x(1)
+            load_wv(0, 0, 1)
+            load_wv(0, 1, 1)
+            load_scale(nc.sync)
             load_h(0)
+            load_wv(0, 2, 2)
             for t in (0, 2):
                 load_wv(1, t, 2)
             load_h(1)
+            load_x(2)
             for s in range(NS):
                 load_w1(s)
-            load_x(1)
             load_h(2)
-            load_x(2)
-            load_h(3)
             load_x(3)
-            widen_x(0)
-            for t in range(4):
+            load_h(3)
+            load_x(4)
+            widen_x(1)
+            for t in range(2):
                 turn_wv(0, t)
                 copy_wv(0, t)
-                if t == 1:
-                    for g in range(2):
-                        turn_rows("x", 0, 0, g)
-                        scale_x(0, 0, g)
             for g in range(2):
-                quant_wv(0, g)
+                turn_rows("x", 1, 0, g)
+                scale_x(1, 0, g)
+            for g in range(2):
                 turn_rows("h", 0, 0, g)
                 copy_h(0, 0, g)
+            for t in range(2):
+                quant_wv(0, t)
             quantise("h", 0)
-            for t in range(4):
+            for t in range(2, 4):
+                turn_wv(0, t)
+                copy_wv(0, t)
+                quant_wv(0, t)
+            for t in range(2):
                 turn_wv(1, t)
                 copy_wv(1, t)
-            sort_words(1, nc.vector, shared[0], 4)
-            for g in range(2):
-                quant_wv(1, g)
             views(0, 0, 0)
-            widen_x(1)
+            sort_words(nc.vector, wv_raw[1, 2], 4, shared[0], 0)
+            sort_words(nc.vector, h_raw[1], 4, shared[0], 4)
+            for t in range(2):
+                quant_wv(1, t)
+            widen_x(2)
+            for t in range(2, 4):
+                turn_wv(1, t)
+                copy_wv(1, t)
             for g in range(2):
                 turn_rows("h", 1, 0, g)
                 copy_h(1, 0, g)
+            for t in range(2, 4):
+                quant_wv(1, t)
             for j in range(3):
                 turn_w1(j)
                 if j == 0:
-                    sort_words(2, nc.vector, shared[0], 4)
+                    sort_words(nc.vector, h_raw[2], 4, shared[0])
                 copy_w1(j, j == 0)
             quantise("h", 1)
             views(0, 0, 1)
-            quantise("x", 0)
+            quantise("x", 1)
             quant_w1(0, 2)
             quant_w1(2, 3)
-            widen_x_plain(2)
+            widen_x_plain(3)
             for i in range(1, STEPS):
                 more = i + 1 < STEPS
                 if i + 3 <= STEPS:
                     load_h(i + 3)
-                if i + 3 < STEPS:
-                    load_x(i + 3)
+                if i + 4 <= STEPS and X_PAIRS[i + 4]:
+                    load_x(i + 4)
                 quantise("v", i - 1)
+                if more and h_blocks(i + 2) + plain_blocks(i + 2):
+                    sort_words(nc.gpsimd, h_raw[i + 2], G_BLOCKS[i], shared[i % 2])
                 if more:
-                    sort_words(i + 2, nc.gpsimd, shared[i % 2], G_BLOCKS[PAIRS[i]])
-                    for q, g in halves(i + 1):
+                    for q, g in halves("h", i + 1):
                         turn_rows("h", i + 1, q, g)
                         copy_h(i + 1, q, g)
-                if i + 2 < STEPS:
-                    widen_x_plain(i + 2)
-                for q, g in halves(i):
-                    turn_rows("x", i, q, g)
-                    scale_x(i, q, g)
+                for q, g in halves("x", i + 1):
+                    turn_rows("x", i + 1, q, g)
+                    scale_x(i + 1, q, g)
                 if more:
-                    widen_x(i + 1)
+                    sort_words(nc.vector, h_raw[i + 2], V_BLOCKS[i], shared[i % 2], G_BLOCKS[i])
+                if more and X_PAIRS[i + 2] * 4 > plain_blocks(i + 2):
+                    widen_x(i + 2)
                 for q in range(PAIRS[i]):
                     for s in range(NS):
-                        views(i, q, s)
+                        (views_wide if 2 * q + s < WIDE[i] else views)(i, q, s)
+                if i + 3 <= STEPS and X_PAIRS[i + 3]:
+                    widen_x_plain(i + 3)
                 if more:
                     quantise("h", i + 1)
-                quantise("x", i)
+                if X_PAIRS[i + 1]:
+                    quantise("x", i + 1)
                 for q in range(PAIRS[i - 1]):
                     finish(i - 1, q)
             last = STEPS - 1

@@ -19,8 +19,9 @@ D = 1024
 NS = 2
 PAIRS = (1, 1, 1, 2, 2, 2, 2, 2, 2, 1)
 X_PAIRS = (0, 1, 1, 1, 2, 2, 2, 2, 2, 2, 1)
-WIDE = (0,0,0,0,0,0,0,0,2,1)
-V_BLOCKS = (0,)*10
+WIDE = (0,0,0,0,0,0,0,1,3,1)
+V_BLOCKS = (0,2,0,0,0,0,0,0,0,0)
+WARM = {0: (512,), 3: (64,), 5: (64,), 7: (64,)}
 STEPS = len(PAIRS)
 S_BLOCKS = (0,0,0,1,3,3,3,3,3,4,2)
 G_BLOCKS = (0,5,5,11,11,11,11,11,11)
@@ -122,6 +123,8 @@ def tile_distributedb_pa_t_kernel(tc, x_bytes, x_scale, h, Wv, W1, out):
 
         def turn(key, parts):
             bank = new_bank()
+            for n in WARM.get(len(banks), ()):
+                nc.tensor.matmul(out=bank[:, :n] if n <= P else bank[:, :n].rearrange("p (r c) -> p r c", c=P), lhsT=ident[:], rhs=ident[:, :n] if n <= P else ident[:].unsqueeze(1).to_broadcast([P, n // P, P]), start=True, stop=True)
             for c, words in enumerate(parts):
                 nc.tensor.transpose(bank[:, c * P : (c + 1) * P], words, ident[:])
             banks[key] = bank
@@ -344,9 +347,9 @@ def tile_distributedb_pa_t_kernel(tc, x_bytes, x_scale, h, Wv, W1, out):
         with tc.manual_schedule():
             load_x(1)
             load_wv(0, 0, 1)
-            load_wv(0, 1, 1)
             load_scale(nc.sync)
             load_h(0)
+            load_wv(0, 1, 1)
             load_wv(0, 2, 2)
             for t in (0, 2):
                 load_wv(1, t, 2)
@@ -359,19 +362,17 @@ def tile_distributedb_pa_t_kernel(tc, x_bytes, x_scale, h, Wv, W1, out):
             load_h(3)
             load_x(4)
             widen_x(1)
-            for t in range(2):
-                turn_wv(0, t)
-                copy_wv(0, t)
+            turn_wv(0, 0)
+            copy_wv(0, 0)
             for g in range(2):
                 turn_rows("x", 1, 0, g)
                 scale_x(1, 0, g)
             for g in range(2):
                 turn_rows("h", 0, 0, g)
                 copy_h(0, 0, g)
-            for t in range(2):
-                quant_wv(0, t)
+            quant_wv(0, 0)
             quantise("h", 0)
-            for t in range(2, 4):
+            for t in range(1, 4):
                 turn_wv(0, t)
                 copy_wv(0, t)
                 quant_wv(0, t)

@@ -20,10 +20,10 @@ NS = 2
 PAIRS = (1, 1, 1, 2, 2, 2, 2, 2, 2, 1)
 X_PAIRS = (0, 1, 1, 1, 2, 2, 2, 2, 2, 2, 1)
 WIDE = (0,0,0,0,0,0,0,1,3,1)
-V_BLOCKS = (0,2,0,0,0,0,0,0,0,0)
-WARM = {0: (512,), 3: (64,), 5: (64,), 7: (64,)}
+V_BLOCKS = (0,0,0,0,0,0,0,0,0,0)
+W1_BANKS = (((0, 0), (0, 1)), ((0, 2), (1, 2)), ((1, 0), (1, 1)))
 STEPS = len(PAIRS)
-S_BLOCKS = (0,0,0,1,3,3,3,3,3,4,2)
+S_BLOCKS = (0,2,0,1,3,3,3,3,3,4,2)
 G_BLOCKS = (0,5,5,11,11,11,11,11,11)
 
 
@@ -65,6 +65,8 @@ def tile_distributedb_pa_t_kernel(tc, x_bytes, x_scale, h, Wv, W1, out):
         wide = max(h_blocks(i) + plain_blocks(i) for i in range(STEPS + 1)) * 512
         shared = [keep.tile([P, wide], BF16, name="shared%d" % n, align_bytes=256) for n in range(2)]
 
+        early = keep.tile([P, 4096], BF16, name="early", align_bytes=256)
+        early2 = early
 
         wv_raw, w1_raw, h_raw, x_raw = {}, {}, {}, {}
         wv_stage, place, stages, quant, banks = {}, {}, {}, {}, {}
@@ -123,8 +125,6 @@ def tile_distributedb_pa_t_kernel(tc, x_bytes, x_scale, h, Wv, W1, out):
 
         def turn(key, parts):
             bank = new_bank()
-            for n in WARM.get(len(banks), ()):
-                nc.tensor.matmul(out=bank[:, :n] if n <= P else bank[:, :n].rearrange("p (r c) -> p r c", c=P), lhsT=ident[:], rhs=ident[:, :n] if n <= P else ident[:].unsqueeze(1).to_broadcast([P, n // P, P]), start=True, stop=True)
             for c, words in enumerate(parts):
                 nc.tensor.transpose(bank[:, c * P : (c + 1) * P], words, ident[:])
             banks[key] = bank
@@ -146,15 +146,17 @@ def tile_distributedb_pa_t_kernel(tc, x_bytes, x_scale, h, Wv, W1, out):
                 out=wv_codes[:, c : c + 256].bitcast(X4), scales=wv_sc[:, c : c + 256], in_=wv_stage[s, t][:]
             )
 
-        def turn_w1(j):
-            turn(("1", j), [words_of("w1", s, j, u) for s in range(NS) for u in range(2)])
+        def turn_w1(n):
+            turn(("1", n), [words_of("w1", s, j, u) for s, j in W1_BANKS[n] for u in range(2)])
 
-        def copy_w1(j, on_vector=False):
-            dst = w1_stage[:, j * D : (j + 1) * D].bitcast(F32)
+        def copy_w1(n, on_vector=False):
+            (s0, j0), (s1, j1) = W1_BANKS[n]
+            dst = w1_stage[:].bitcast(F32).rearrange("p (c f u) -> p c f u", f=P, u=2)
+            lo, hi = 2 * j0 + s0, 2 * j1 + s1
             copy_words(
                 on_vector,
-                dst.rearrange("p (s f u) -> p s f u", s=2, u=2),
-                banks["1", j][:].rearrange("p (s u f) -> p s f u", s=2, u=2),
+                dst[:, lo : hi + 1 : hi - lo],
+                banks["1", n][:].rearrange("p (c u f) -> p c f u", c=2, u=2),
             )
 
         def quant_w1(lo, hi):
@@ -164,22 +166,23 @@ def tile_distributedb_pa_t_kernel(tc, x_bytes, x_scale, h, Wv, W1, out):
                 in_=w1_stage[:, lo * D : hi * D],
             )
 
-        def widen_x(i):
-            blocks = 4 * X_PAIRS[i] - plain_blocks(i)
-            w = stage.tile([P, blocks * 512], BF16, name="x_wide", align_bytes=256)
+        def widen_x(i, lo=0, hi=None):
+            hi = hi or 4 * X_PAIRS[i] - plain_blocks(i)
+            blocks = hi - lo
+            w = stage.tile([P, blocks * 512], BF16, name="x_wide", align_bytes=256, bufs=3)
             nc.vector.tensor_scalar(
                 out=w[:].rearrange("p (u n e) -> p n u e", u=2, e=2),
-                in0=x_raw[i][:, : blocks * 512].bitcast(F8).rearrange("p (n u e) -> p n u e", u=2, e=2),
+                in0=x_raw[i][:, lo * 512 : hi * 512].bitcast(F8).rearrange("p (n u e) -> p n u e", u=2, e=2),
                 scalar1=ones[:, 0:1],
                 scalar2=None,
                 op0=MULT,
             )
             for b in range(blocks):
-                place["x", i, b] = w[:], blocks, b
+                place["x", i, lo + b] = w[:], blocks, b
 
         def widen_x_plain(i):
             lo = 4 * X_PAIRS[i] - plain_blocks(i)
-            tile, c = h_raw[i], h_blocks(i)
+            tile, c = (h_raw[i], h_blocks(i)) if i >= 3 else ((early, early2)[i - 1], 0)
             nc.scalar.copy(
                 out=tile[:, c * 512 : (c + plain_blocks(i)) * 512],
                 in_=x_raw[i][:, lo * 512 : 4 * X_PAIRS[i] * 512].bitcast(F8),
@@ -351,10 +354,10 @@ def tile_distributedb_pa_t_kernel(tc, x_bytes, x_scale, h, Wv, W1, out):
             load_h(0)
             load_wv(0, 1, 1)
             load_wv(0, 2, 2)
-            for t in (0, 2):
-                load_wv(1, t, 2)
-            load_h(1)
+            load_wv(1, 0, 2)
             load_x(2)
+            load_wv(1, 2, 2)
+            load_h(1)
             for s in range(NS):
                 load_w1(s)
             load_h(2)
@@ -362,6 +365,7 @@ def tile_distributedb_pa_t_kernel(tc, x_bytes, x_scale, h, Wv, W1, out):
             load_h(3)
             load_x(4)
             widen_x(1)
+            widen_x_plain(1)
             turn_wv(0, 0)
             copy_wv(0, 0)
             for g in range(2):
@@ -375,16 +379,20 @@ def tile_distributedb_pa_t_kernel(tc, x_bytes, x_scale, h, Wv, W1, out):
             for t in range(1, 4):
                 turn_wv(0, t)
                 copy_wv(0, t)
+                if t == 2:
+                    widen_x(2, 0, 2)
                 quant_wv(0, t)
             for t in range(2):
                 turn_wv(1, t)
                 copy_wv(1, t)
             views(0, 0, 0)
             sort_words(nc.vector, wv_raw[1, 2], 4, shared[0], 0)
+            widen_x(2, 2, 4)
             sort_words(nc.vector, h_raw[1], 4, shared[0], 4)
+            sort_words(nc.vector, w1_raw[0], 3, early, 2)
             for t in range(2):
                 quant_wv(1, t)
-            widen_x(2)
+            sort_words(nc.vector, w1_raw[1], 3, early, 5)
             for t in range(2, 4):
                 turn_wv(1, t)
                 copy_wv(1, t)
@@ -414,7 +422,7 @@ def tile_distributedb_pa_t_kernel(tc, x_bytes, x_scale, h, Wv, W1, out):
                 if more and h_blocks(i + 2) + plain_blocks(i + 2):
                     sort_words(nc.gpsimd, h_raw[i + 2], G_BLOCKS[i], shared[i % 2])
                 if more:
-                    for q, g in halves("h", i + 1):
+                    for q, g in halves("h", i + 1)[::-1]:
                         turn_rows("h", i + 1, q, g)
                         copy_h(i + 1, q, g)
                 for q, g in halves("x", i + 1):

@@ -17,14 +17,13 @@ ACT = mybir.ActivationFunctionType
 P = 128
 D = 1024
 NS = 2
-PAIRS = (1, 1, 1, 2, 2, 2, 2, 2, 2, 1)
-X_PAIRS = (0, 1, 1, 1, 2, 2, 2, 2, 2, 2, 1)
-WIDE = (0,0,0,0,0,0,0,1,3,1)
-V_BLOCKS = (0,0,0,0,0,0,0,0,0,0)
-W1_BANKS = (((0, 0), (0, 1)), ((0, 2), (1, 2)), ((1, 0), (1, 1)))
+PIECE = 512
+PAIRS = (1,) * 3 + (2,) * 6 + (1,)
 STEPS = len(PAIRS)
-S_BLOCKS = (0,2,0,1,3,3,3,3,3,4,2)
-G_BLOCKS = (0,5,5,11,11,11,11,11,11)
+LAST = STEPS - 1
+SCALAR_PIECES = {1: 1, 2: 3}
+GPSIMD_PIECES = {1: 5, 2: 11}
+W1_BANKS = (((0, 0), (0, 1)), ((0, 2), (1, 2)), ((1, 0), (1, 1)))
 
 
 def tile_distributedb_pa_t_kernel(tc, x_bytes, x_scale, h, Wv, W1, out):
@@ -32,15 +31,15 @@ def tile_distributedb_pa_t_kernel(tc, x_bytes, x_scale, h, Wv, W1, out):
     x_rows = x_bytes.rearrange("b r k -> (b r) k")
     h_rows = h.rearrange("b r k -> (b r) k")
     out_rows = out.rearrange("s b r f -> s (b r) f")
-    pairs = {"h": PAIRS, "v": PAIRS, "x": X_PAIRS}
-    first = {kind: [sum(n[:i]) for i in range(len(n) + 1)] for kind, n in pairs.items()}
-    x_place = [(i, q) for i in range(STEPS + 1) for q in range(X_PAIRS[i])]
+    row0 = [256 * sum(PAIRS[:i]) for i in range(STEPS + 1)]
 
-    def plain_blocks(i):
-        return S_BLOCKS[i]
-
-    def h_blocks(i):
+    def pieces(i):
         return 4 * PAIRS[i] if i < STEPS else 0
+
+    def scalar_pieces(i):
+        if i in (0, LAST - 1, LAST):
+            return pieces(i) // 2
+        return SCALAR_PIECES[PAIRS[i]] if i > 1 else 0
 
     with ExitStack() as ctx:
         keep = ctx.enter_context(tc.tile_pool(name="keep", bufs=1))
@@ -54,25 +53,24 @@ def tile_distributedb_pa_t_kernel(tc, x_bytes, x_scale, h, Wv, W1, out):
         make_identity(nc, ident[:])
         ones = keep.tile([P, 1], F32, name="ones")
         nc.vector.memset(ones[:], 1.0)
-        warm = keep.tile([P, 1], F32, name="warm")
-        nc.scalar.activation(out=warm[:], in_=ones[:], func=ACT.Silu)
+        table_load = keep.tile([P, 1], F32, name="table_load")
+        nc.scalar.activation(out=table_load[:], in_=ones[:], func=ACT.Silu)
 
         wv_codes = keep.tile([P, 4 * 512], U32, name="wv_codes", align_bytes=256)
-        wv_sc = keep.tile([P, 4 * 512], U8, name="wv_sc", align_bytes=256)
+        wv_scales = keep.tile([P, 4 * 512], U8, name="wv_scales", align_bytes=256)
         w1_codes = keep.tile([P, 6 * P], U32, name="w1_codes", align_bytes=256)
-        w1_sc = keep.tile([P, 6 * P], U8, name="w1_sc", align_bytes=256)
+        w1_scales = keep.tile([P, 6 * P], U8, name="w1_scales", align_bytes=256)
         w1_stage = keep.tile([P, 6 * P * 4], BF16, name="w1_stage", align_bytes=256)
-        wide = max(h_blocks(i) + plain_blocks(i) for i in range(STEPS + 1)) * 512
-        shared = [keep.tile([P, wide], BF16, name="shared%d" % n, align_bytes=256) for n in range(2)]
-
-        early = keep.tile([P, 4096], BF16, name="early", align_bytes=256)
-        early2 = early
+        width = max(pieces(i + 1) + scalar_pieces(i) for i in range(STEPS)) * PIECE
+        shared = [keep.tile([P, width], BF16, name="shared%d" % n, align_bytes=256) for n in range(2)]
+        early = keep.tile([P, 8 * PIECE], BF16, name="early", align_bytes=256)
 
         wv_raw, w1_raw, h_raw, x_raw = {}, {}, {}, {}
-        wv_stage, place, stages, quant, banks = {}, {}, {}, {}, {}
+        wv_stage, stages, quant, banks = {}, {}, {}, {}
+        place = {}
 
         def new_bank():
-            return psum.tile([P, 512], F32, name="bank")
+            return psum.tile([P, PIECE], F32, name="bank")
 
         def load_wv(s, t, n):
             w = keep.tile([P, n * D], BF16, name="wv_raw%d%d" % (s, t))
@@ -81,47 +79,50 @@ def tile_distributedb_pa_t_kernel(tc, x_bytes, x_scale, h, Wv, W1, out):
                 place["wv", s, 2 * t + b] = w, None, b
             wv_raw[s, t] = w
 
-        def load_scale(engine):
-            engine.dma_start(
+        def load_scale():
+            nc.sync.dma_start(
                 out=scale[:].rearrange("p (g t) -> p g t", g=2),
                 in_=x_scale.rearrange("o b (g p t) -> p (o b g) t", g=2, p=P, t=4),
             )
 
         def load_w1(s):
-            w = wpool.tile([P, 1536], BF16, name="w1_raw")
+            w = wpool.tile([P, 3 * PIECE], BF16, name="w1_raw")
             nc.sync.dma_start(out=w[:], in_=W1[s])
             for j in range(3):
                 place["w1", s, j] = w, None, j
             w1_raw[s] = w
 
+        def load_rows(tile, rows, i):
+            dst = tile[:, : pieces(i) * PIECE].rearrange("p (q c) -> p q c", c=2 * D)
+            nc.sync.dma_start(out=dst, in_=rows[row0[i] : row0[i + 1], :].rearrange("(q p a) k -> p q (a k)", p=P, a=2))
+
         def load_h(i):
-            h_raw[i] = raw.tile([P, wide], BF16, name="h_raw", align_bytes=256, bufs=4)
-            if i == STEPS:
-                return
-            rows = h_rows[256 * first["h"][i] : 256 * first["h"][i + 1], :]
-            dst = h_raw[i][:, : h_blocks(i) * 512].rearrange("p (q c) -> p q c", c=2 * D)
-            nc.sync.dma_start(out=dst, in_=rows.rearrange("(q p r) k -> p q (r k)", p=P, r=2))
-            for b in range(h_blocks(i)):
-                place["h", i, b] = h_raw[i], None, b
+            h_raw[i] = raw.tile([P, width], BF16, name="h_raw", align_bytes=256)
+            if i < STEPS:
+                load_rows(h_raw[i], h_rows, i)
+                for b in range(pieces(i)):
+                    place["h", i, b] = h_raw[i], None, b
 
         def load_x(i):
-            x_raw[i] = raw.tile([P, 4 * D], U8, name="x_raw", bufs=4)
-            rows = x_rows[256 * first["x"][i] : 256 * first["x"][i + 1], :]
-            dst = x_raw[i][:, : X_PAIRS[i] * 2 * D].rearrange("p (q c) -> p q c", c=2 * D)
-            nc.sync.dma_start(out=dst, in_=rows.rearrange("(q p r) k -> p q (r k)", p=P, r=2))
+            x_raw[i] = raw.tile([P, 4 * D], U8, name="x_raw")
+            load_rows(x_raw[i], x_rows, i)
 
-        def copy_words(on_vector, dst, src):
-            if on_vector:
-                nc.vector.tensor_copy(out=dst, in_=src)
-            else:
-                nc.scalar.copy(out=dst, in_=src)
+        def words_of(kind, i, piece, u):
+            where, count, n = place[kind, i, piece]
+            if count is None:
+                return where[:].bitcast(F32)[:, 256 * n + u : 256 * (n + 1) : 2]
+            c = (u * count + n) * P
+            return where.bitcast(F32)[:, c : c + P]
 
-        def every_second(tile, block, u):
-            return tile[:].bitcast(F32)[:, 256 * block + u : 256 * (block + 1) : 2]
-
-        def in_a_row(part, blocks, block, u):
-            c = (u * blocks + block) * P
-            return part.bitcast(F32)[:, c : c + P]
+        def sort_words(engine, src, most, dst, at=0):
+            keys = [key for key, (where, count, n) in place.items() if where is src][:most]
+            part = dst[:, at * PIECE : (at + len(keys)) * PIECE]
+            engine.tensor_copy(
+                out=part.bitcast(F32).rearrange("p (u n) -> p u n", u=2),
+                in_=src[:, : len(keys) * PIECE].bitcast(F32).rearrange("p (n u) -> p u n", u=2),
+            )
+            for n, key in enumerate(keys):
+                place[key] = part, len(keys), n
 
         def turn(key, parts):
             bank = new_bank()
@@ -130,197 +131,161 @@ def tile_distributedb_pa_t_kernel(tc, x_bytes, x_scale, h, Wv, W1, out):
             banks[key] = bank
 
         def turn_wv(s, t):
-            turn(("w", s, t), [words_of("wv", s, 2 * t + g, u) for g in range(2) for u in range(2)])
-
-        def copy_wv(s, t, on_vector=False):
+            turn(("wv", s, t), [words_of("wv", s, 2 * t + g, u) for g in range(2) for u in range(2)])
             wv_stage[s, t] = wpool.tile([P, D], BF16, name="wv_stage", align_bytes=256, bufs=4)
-            copy_words(
-                on_vector,
-                wv_stage[s, t][:].bitcast(F32).rearrange("p (g m u) -> p g m u", g=2, u=2),
-                banks["w", s, t][:].rearrange("p (g u m) -> p g m u", g=2, u=2),
+            nc.scalar.copy(
+                out=wv_stage[s, t][:].bitcast(F32).rearrange("p (g m u) -> p g m u", g=2, u=2),
+                in_=banks["wv", s, t][:].rearrange("p (g u m) -> p g m u", g=2, u=2),
             )
 
         def quant_wv(s, t):
             c = (4 * s + t) * 256
             nc.vector.quantize_mx(
-                out=wv_codes[:, c : c + 256].bitcast(X4), scales=wv_sc[:, c : c + 256], in_=wv_stage[s, t][:]
+                out=wv_codes[:, c : c + 256].bitcast(X4), scales=wv_scales[:, c : c + 256], in_=wv_stage[s, t][:]
             )
 
         def turn_w1(n):
-            turn(("1", n), [words_of("w1", s, j, u) for s, j in W1_BANKS[n] for u in range(2)])
+            turn(("w1", n), [words_of("w1", s, j, u) for s, j in W1_BANKS[n] for u in range(2)])
 
-        def copy_w1(n, on_vector=False):
-            (s0, j0), (s1, j1) = W1_BANKS[n]
+        def copy_w1(n, copy):
+            lo, hi = [2 * j + s for s, j in W1_BANKS[n]]
             dst = w1_stage[:].bitcast(F32).rearrange("p (c f u) -> p c f u", f=P, u=2)
-            lo, hi = 2 * j0 + s0, 2 * j1 + s1
-            copy_words(
-                on_vector,
-                dst[:, lo : hi + 1 : hi - lo],
-                banks["1", n][:].rearrange("p (c u f) -> p c f u", c=2, u=2),
-            )
+            copy(out=dst[:, lo : hi + 1 : hi - lo], in_=banks["w1", n][:].rearrange("p (c u f) -> p c f u", c=2, u=2))
 
         def quant_w1(lo, hi):
             nc.vector.quantize_mx(
                 out=w1_codes[:, lo * 256 : hi * 256].bitcast(X4),
-                scales=w1_sc[:, lo * 256 : hi * 256],
+                scales=w1_scales[:, lo * 256 : hi * 256],
                 in_=w1_stage[:, lo * D : hi * D],
             )
 
-        def widen_x(i, lo=0, hi=None):
-            hi = hi or 4 * X_PAIRS[i] - plain_blocks(i)
-            blocks = hi - lo
-            w = stage.tile([P, blocks * 512], BF16, name="x_wide", align_bytes=256, bufs=3)
+        def widen_sorted(i, lo, hi):
+            w = stage.tile([P, (hi - lo) * PIECE], BF16, name="x_wide", align_bytes=256, bufs=3)
             nc.vector.tensor_scalar(
                 out=w[:].rearrange("p (u n e) -> p n u e", u=2, e=2),
-                in0=x_raw[i][:, lo * 512 : hi * 512].bitcast(F8).rearrange("p (n u e) -> p n u e", u=2, e=2),
+                in0=x_raw[i][:, lo * PIECE : hi * PIECE].bitcast(F8).rearrange("p (n u e) -> p n u e", u=2, e=2),
                 scalar1=ones[:, 0:1],
                 scalar2=None,
                 op0=MULT,
             )
-            for b in range(blocks):
-                place["x", i, lo + b] = w[:], blocks, b
+            for b in range(lo, hi):
+                place["x", i, b] = w[:], hi - lo, b - lo
 
-        def widen_x_plain(i):
-            lo = 4 * X_PAIRS[i] - plain_blocks(i)
-            tile, c = (h_raw[i], h_blocks(i)) if i >= 3 else ((early, early2)[i - 1], 0)
+        def widen_on_vector(i):
+            widen_sorted(i, 0, pieces(i) - scalar_pieces(i))
+
+        def widen_on_scalar(i):
+            lo = pieces(i) - scalar_pieces(i)
+            tile, c = (h_raw[i + 1], pieces(i + 1)) if i else (early, 0)
             nc.scalar.copy(
-                out=tile[:, c * 512 : (c + plain_blocks(i)) * 512],
-                in_=x_raw[i][:, lo * 512 : 4 * X_PAIRS[i] * 512].bitcast(F8),
+                out=tile[:, c * PIECE : (c + scalar_pieces(i)) * PIECE],
+                in_=x_raw[i][:, lo * PIECE : pieces(i) * PIECE].bitcast(F8),
             )
-            for b in range(plain_blocks(i)):
+            for b in range(scalar_pieces(i)):
                 place["x", i, lo + b] = tile, None, c + b
 
-        def sort_words(engine, src, blocks, dst, at=0):
-            keys = [key for key, (tile, order, n) in place.items() if tile is src][:blocks]
-            if not keys:
-                return
-            lo = place[keys[0]][2]
-            part = dst[:, at * 512 : (at + len(keys)) * 512]
-            engine.tensor_copy(
-                out=part.bitcast(F32).rearrange("p (u n) -> p u n", u=2),
-                in_=src[:, lo * 512 : (lo + len(keys)) * 512].bitcast(F32).rearrange("p (n u) -> p u n", u=2),
-            )
-            for n, key in enumerate(keys):
-                place[key] = part, len(keys), n
-
-        def words_of(kind, i, block, u):
-            tile, blocks, n = place[kind, i, block]
-            return every_second(tile, n, u) if blocks is None else in_a_row(tile, blocks, n, u)
-
         def turn_rows(kind, i, q, g):
-            turn((kind, i, q, g), [words_of(kind, i, 2 * (2 * q + a) + g, u) for u in range(2) for a in range(2)])
-
-        def stage_part(kind, i, q, g):
+            turn((kind, i, q, g), [words_of(kind, i, 4 * q + 2 * a + g, u) for u in range(2) for a in range(2)])
             if (kind, i) not in stages:
                 stages[kind, i] = stage.tile([P, 4 * D], BF16, name=kind + "_stage", align_bytes=256)
             c = (2 * q + g) * D
-            return stages[kind, i][:, c : c + D]
+            return banks[kind, i, q, g], stages[kind, i][:, c : c + D]
 
-        def copy_h(i, q, g, on_vector=False):
-            copy_words(
-                on_vector,
-                stage_part("h", i, q, g).bitcast(F32).rearrange("p (n u) -> p n u", u=2),
-                banks["h", i, q, g][:].rearrange("p (u n) -> p n u", u=2),
+        def turn_h(i, q, g):
+            bank, dst = turn_rows("h", i, q, g)
+            nc.scalar.copy(
+                out=dst.bitcast(F32).rearrange("p (n u) -> p n u", u=2), in_=bank[:].rearrange("p (u n) -> p n u", u=2)
             )
 
-        def scale_x(i, q, g):
+        def turn_x(i, q, g):
+            bank, dst = turn_rows("x", i, q, g)
             sc = scale[:, 4 * g : 4 * g + 4].rearrange("p (u e) -> p u e", u=2)
             nc.vector.tensor_tensor(
-                out=stage_part("x", i, q, g).rearrange("p (n u e) -> p n u e", u=2, e=2),
-                in0=banks["x", i, q, g][:].bitcast(BF16).rearrange("p (u n e) -> p n u e", u=2, e=2),
+                out=dst.rearrange("p (n u e) -> p n u e", u=2, e=2),
+                in0=bank[:].bitcast(BF16).rearrange("p (u n e) -> p n u e", u=2, e=2),
                 in1=sc.unsqueeze(1).to_broadcast([P, 256, 2, 2]),
                 op=MULT,
             )
 
-        def quantise(kind, i, pieces=1, only=None):
+        def quantise(kind, i, parts=1, only=None):
             if (kind, i) not in quant:
-                bufs = 2
-                codes = stage.tile([P, D], U32, name=kind + "_codes", align_bytes=256, bufs=bufs)
-                scales = stage.tile([P, D], U8, name=kind + "_scales", align_bytes=256, bufs=bufs)
+                codes = stage.tile([P, D], U32, name=kind + "_codes", align_bytes=256)
+                scales = stage.tile([P, D], U8, name=kind + "_scales", align_bytes=256)
                 quant[kind, i] = codes, scales
             codes, scales = quant[kind, i]
-            n = pairs[kind][i] * 512 // pieces
-            for k in only or range(pieces):
+            n = PAIRS[i] * 512 // parts
+            for k in only or range(parts):
                 nc.vector.quantize_mx(
                     out=codes[:, k * n : (k + 1) * n].bitcast(X4),
                     scales=scales[:, k * n : (k + 1) * n],
                     in_=stages[kind, i][:, 4 * k * n : 4 * (k + 1) * n],
                 )
 
-        def views(i, q, s, groups=range(4)):
+        def first_product(dst, i, s, t, q, c, n):
             codes, scales = quant["h", i]
+            for g in range(2):
+                w = ((4 * s + t) * 2 + g) * P
+                r = (2 * q + g) * 256 + c
+                nc.tensor.matmul_mx(
+                    out=dst,
+                    lhsT=wv_codes[:, w : w + P].bitcast(X4),
+                    lhsT_scale=wv_scales[:, w : w + P],
+                    rhs=codes[:, r : r + n].bitcast(X4),
+                    rhs_scale=scales[:, r : r + n],
+                    start=(g == 0),
+                    stop=(g == 1),
+                )
+
+        def views_stage(i, q, s):
             stages["v", i] = shared[(i + 1) % 2]
+            k = (2 * q + s) * D
+            return stages["v", i][:, k : k + D]
+
+        def views(i, q, s):
+            dst = views_stage(i, q, s)
             for a in range(2):
-                if groups[0] == 0:
-                    banks["v", a] = new_bank()
-                bank = banks["v", a]
-                for t in groups:
-                    for g in range(2):
-                        w = ((4 * s + t) * 2 + g) * P
-                        c = ((2 * q + g) * 2 + a) * P
-                        nc.tensor.matmul_mx(
-                            out=bank[:, t * P : (t + 1) * P],
-                            lhsT=wv_codes[:, w : w + P].bitcast(X4),
-                            lhsT_scale=wv_sc[:, w : w + P],
-                            rhs=codes[:, c : c + P].bitcast(X4),
-                            rhs_scale=scales[:, c : c + P],
-                            start=(g == 0),
-                            stop=(g == 1),
-                        )
-                if groups[-1] == 3:
-                    k = (2 * q + s) * 2 + a
-                    nc.scalar.copy(
-                        out=stages["v", i][:, k * 512 : (k + 1) * 512].rearrange("p (r t) -> p r t", t=4),
-                        in_=bank[:].rearrange("p (t r) -> p r t", t=4),
-                    )
+                bank = new_bank()
+                for t in range(4):
+                    first_product(bank[:, t * P : (t + 1) * P], i, s, t, q, a * P, P)
+                nc.scalar.copy(
+                    out=dst[:, a * 512 : (a + 1) * 512].rearrange("p (r t) -> p r t", t=4),
+                    in_=bank[:].rearrange("p (t r) -> p r t", t=4),
+                )
 
         def views_wide(i, q, s):
-            codes, scales = quant["h", i]
-            stages["v", i] = shared[(i + 1) % 2]
-            k = (2 * q + s) * 2
-            dst = stages["v", i][:, k * 512 : (k + 2) * 512].rearrange("p (n j e) -> p n j e", j=2, e=2)
-            for j in range(2):
+            dst = views_stage(i, q, s).rearrange("p (n u e) -> p n u e", u=2, e=2)
+            for u in range(2):
                 bank = new_bank()
                 for e in range(2):
-                    for g in range(2):
-                        w = ((4 * s + 2 * j + e) * 2 + g) * P
-                        c = (2 * q + g) * 256
-                        nc.tensor.matmul_mx(
-                            out=bank[:, e * 256 : (e + 1) * 256],
-                            lhsT=wv_codes[:, w : w + P].bitcast(X4),
-                            lhsT_scale=wv_sc[:, w : w + P],
-                            rhs=codes[:, c : c + 256].bitcast(X4),
-                            rhs_scale=scales[:, c : c + 256],
-                            start=(g == 0),
-                            stop=(g == 1),
-                        )
-                nc.scalar.copy(out=dst[:, :, j, :], in_=bank[:].rearrange("p (e n) -> p n e", e=2))
+                    first_product(bank[:, e * 256 : (e + 1) * 256], i, s, 2 * u + e, q, 0, 256)
+                nc.scalar.copy(out=dst[:, :, u, :], in_=bank[:].rearrange("p (e n) -> p n e", e=2))
 
-        def second(dst, kind, i, c, w, n, start, stop):
-            codes, scales = quant[kind, i]
-            nc.tensor.matmul_mx(
-                out=dst,
-                lhsT=codes[:, c : c + P].bitcast(X4),
-                lhsT_scale=scales[:, c : c + P],
-                rhs=w1_codes[:, w : w + n].bitcast(X4),
-                rhs_scale=w1_sc[:, w : w + n],
-                start=start,
-                stop=stop,
-            )
+        def second_product(dst, i, q, a, subnets):
+            n = len(subnets) * P
+            passes = [("x", (2 * q + g) * 2 + a, 2 * g + subnets[0], dst) for g in range(2)]
+            for c, s in enumerate(subnets):
+                passes.append(("v", (2 * q + s) * 2 + a, 4 + s, dst[:, c * P : (c + 1) * P]))
+            for k, (kind, c, w, part) in enumerate(passes):
+                codes, scales = quant[kind, i]
+                cols = slice(w * P, w * P + (n if kind == "x" else P))
+                nc.tensor.matmul_mx(
+                    out=part,
+                    lhsT=codes[:, c * P : (c + 1) * P].bitcast(X4),
+                    lhsT_scale=scales[:, c * P : (c + 1) * P],
+                    rhs=w1_codes[:, cols].bitcast(X4),
+                    rhs_scale=w1_scales[:, cols],
+                    start=(k == 0),
+                    stop=(k == len(passes) - 1),
+                )
 
         def out_view(i, q):
-            r = 256 * (first["h"][i] + q)
+            r = row0[i] + 256 * q
             return out_rows[:, r : r + 256, :].rearrange("s (p a) f -> p s a f", p=P)
 
         def finish(i, q):
-            xi, xq = x_place[first["h"][i] + q]
             bank = new_bank()
             for a in range(2):
-                for g in range(2):
-                    second(bank[:, a * 256 : (a + 1) * 256], "x", xi, ((2 * xq + g) * 2 + a) * P, g * 256, 256, g == 0, False)
-                for s in range(NS):
-                    k = 2 * a + s
-                    second(bank[:, k * P : (k + 1) * P], "v", i, ((2 * q + s) * 2 + a) * P, (4 + s) * P, P, False, s == 1)
+                second_product(bank[:, a * 256 : (a + 1) * 256], i, q, a, range(NS))
             res = stage.tile([P, 512], F32, name="res", bufs=4)
             nc.scalar.activation(
                 out=res[:].rearrange("p (s a f) -> p s a f", s=2, a=2),
@@ -332,62 +297,62 @@ def tile_distributedb_pa_t_kernel(tc, x_bytes, x_scale, h, Wv, W1, out):
                 in_=res[:].rearrange("p (s c) -> p s c", s=2),
             )
 
-        def finish_apart(i, q):
-            xi, xq = x_place[first["h"][i] + q]
-            for k in range(4):
-                s, a = divmod(k, 2)
+        def finish_by_row_tile(i, q):
+            for a in range(2):
                 bank = new_bank()
-                for g in range(2):
-                    second(bank[:, 0:P], "x", xi, ((2 * xq + g) * 2 + a) * P, (2 * g + s) * P, P, g == 0, False)
-                second(bank[:, 0:P], "v", i, (4 * q + k) * P, (4 + s) * P, P, False, True)
-                res = stage.tile([P, P], F32, name="res_apart", bufs=4)
-                nc.scalar.activation(out=res[:], in_=bank[:, 0:P], func=ACT.Silu)
-                nc.sync.dma_start(out=out_view(i, q)[:, s, a, :], in_=res[:])
+                second_product(bank[:, :256], i, q, a, range(NS))
+                res = stage.tile([P, 256], F32, name="res_rows")
+                nc.scalar.activation(out=res[:], in_=bank[:, :256], func=ACT.Silu)
+                nc.sync.dma_start(out=out_view(i, q)[:, :, a, :], in_=res[:].rearrange("p (s f) -> p s f", s=2))
 
-        def halves(kind, i):
-            return [(q, g) for q in range(pairs[kind][i]) for g in range(2)]
+        def finish_by_subnet(i, q):
+            for s in range(NS):
+                bank = new_bank()
+                for a in range(2):
+                    second_product(bank[:, a * P : (a + 1) * P], i, q, a, (s,))
+                res = stage.tile([P, 256], F32, name="res_subnet")
+                nc.scalar.activation(out=res[:], in_=bank[:, :256], func=ACT.Silu)
+                nc.sync.dma_start(out=out_view(i, q)[:, s].rearrange("p a f -> p (a f)"), in_=res[:])
+
+        def passes_of(i):
+            return [(q, g) for q in range(PAIRS[i]) for g in range(2)]
 
         with tc.manual_schedule():
-            load_x(1)
+            load_x(0)
             load_wv(0, 0, 1)
-            load_scale(nc.sync)
+            load_scale()
             load_h(0)
             load_wv(0, 1, 1)
             load_wv(0, 2, 2)
             load_wv(1, 0, 2)
-            load_x(2)
+            load_x(1)
             load_wv(1, 2, 2)
             load_h(1)
             for s in range(NS):
                 load_w1(s)
-            load_h(2)
-            load_x(3)
-            load_h(3)
-            load_x(4)
-            widen_x(1)
-            widen_x_plain(1)
+            for i in (2, 3):
+                load_h(i)
+                load_x(i)
+
+            widen_on_vector(0)
+            widen_on_scalar(0)
             turn_wv(0, 0)
-            copy_wv(0, 0)
-            for g in range(2):
-                turn_rows("x", 1, 0, g)
-                scale_x(1, 0, g)
-            for g in range(2):
-                turn_rows("h", 0, 0, g)
-                copy_h(0, 0, g)
+            for q, g in passes_of(0):
+                turn_x(0, q, g)
+            for q, g in passes_of(0):
+                turn_h(0, q, g)
             quant_wv(0, 0)
             quantise("h", 0)
             for t in range(1, 4):
                 turn_wv(0, t)
-                copy_wv(0, t)
                 if t == 2:
-                    widen_x(2, 0, 2)
+                    widen_sorted(1, 0, 2)
                 quant_wv(0, t)
             for t in range(2):
                 turn_wv(1, t)
-                copy_wv(1, t)
             views(0, 0, 0)
-            sort_words(nc.vector, wv_raw[1, 2], 4, shared[0], 0)
-            widen_x(2, 2, 4)
+            sort_words(nc.vector, wv_raw[1, 2], 4, shared[0])
+            widen_sorted(1, 2, 4)
             sort_words(nc.vector, h_raw[1], 4, shared[0], 4)
             sort_words(nc.vector, w1_raw[0], 3, early, 2)
             for t in range(2):
@@ -395,57 +360,53 @@ def tile_distributedb_pa_t_kernel(tc, x_bytes, x_scale, h, Wv, W1, out):
             sort_words(nc.vector, w1_raw[1], 3, early, 5)
             for t in range(2, 4):
                 turn_wv(1, t)
-                copy_wv(1, t)
-            for g in range(2):
-                turn_rows("h", 1, 0, g)
-                copy_h(1, 0, g)
+            for q, g in passes_of(1):
+                turn_h(1, q, g)
             for t in range(2, 4):
                 quant_wv(1, t)
-            for j in range(3):
-                turn_w1(j)
-                if j == 0:
-                    sort_words(nc.vector, h_raw[2], 4, shared[0])
-                copy_w1(j, j == 0)
+            turn_w1(0)
+            sort_words(nc.vector, h_raw[2], 4, shared[0])
+            copy_w1(0, nc.vector.tensor_copy)
+            for n in (1, 2):
+                turn_w1(n)
+                copy_w1(n, nc.scalar.copy)
             quantise("h", 1)
             views(0, 0, 1)
-            quantise("x", 1)
+            quantise("x", 0)
             quant_w1(0, 2)
             quant_w1(2, 3)
-            widen_x_plain(3)
-            for i in range(1, STEPS):
-                more = i + 1 < STEPS
+            widen_on_scalar(2)
+
+            for i in range(1, LAST):
                 if i + 3 <= STEPS:
                     load_h(i + 3)
-                if i + 4 <= STEPS and X_PAIRS[i + 4]:
-                    load_x(i + 4)
+                if i + 3 < STEPS:
+                    load_x(i + 3)
                 quantise("v", i - 1)
-                if more and h_blocks(i + 2) + plain_blocks(i + 2):
-                    sort_words(nc.gpsimd, h_raw[i + 2], G_BLOCKS[i], shared[i % 2])
-                if more:
-                    for q, g in halves("h", i + 1)[::-1]:
-                        turn_rows("h", i + 1, q, g)
-                        copy_h(i + 1, q, g)
-                for q, g in halves("x", i + 1):
-                    turn_rows("x", i + 1, q, g)
-                    scale_x(i + 1, q, g)
-                if more:
-                    sort_words(nc.vector, h_raw[i + 2], V_BLOCKS[i], shared[i % 2], G_BLOCKS[i])
-                if more and X_PAIRS[i + 2] * 4 > plain_blocks(i + 2):
-                    widen_x(i + 2)
-                for q in range(PAIRS[i]):
-                    for s in range(NS):
-                        (views_wide if 2 * q + s < WIDE[i] else views)(i, q, s)
-                if i + 3 <= STEPS and X_PAIRS[i + 3]:
-                    widen_x_plain(i + 3)
-                if more:
-                    quantise("h", i + 1)
-                if X_PAIRS[i + 1]:
-                    quantise("x", i + 1)
+                sort_words(nc.gpsimd, h_raw[i + 2], GPSIMD_PIECES[PAIRS[i]], shared[i % 2])
+                for q, g in reversed(passes_of(i + 1)):
+                    turn_h(i + 1, q, g)
+                for q, g in passes_of(i):
+                    turn_x(i, q, g)
+                widen_on_vector(i + 1)
+                for n in range(NS * PAIRS[i]):
+                    wide = i == LAST - 1 and n < NS * PAIRS[i] - 1
+                    (views_wide if wide else views)(i, *divmod(n, NS))
+                if i + 2 < STEPS:
+                    widen_on_scalar(i + 2)
+                quantise("h", i + 1)
+                quantise("x", i)
                 for q in range(PAIRS[i - 1]):
                     finish(i - 1, q)
-            last = STEPS - 1
-            for q in range(PAIRS[last] - 1):
-                quantise("v", last, PAIRS[last], (q,))
-                finish(last, q)
-            quantise("v", last, 4 * PAIRS[last], range(4 * PAIRS[last] - 4, 4 * PAIRS[last]))
-            finish_apart(last, PAIRS[last] - 1)
+
+            quantise("v", LAST - 1, 2, (0,))
+            for q, g in passes_of(LAST):
+                turn_x(LAST, q, g)
+            quantise("v", LAST - 1, 2, (1,))
+            views_wide(LAST, 0, 0)
+            finish(LAST - 1, 0)
+            views(LAST, 0, 1)
+            quantise("x", LAST)
+            finish_by_row_tile(LAST - 1, 1)
+            quantise("v", LAST, 4)
+            finish_by_subnet(LAST, 0)

@@ -23,6 +23,7 @@ STEPS = len(PAIRS)
 LAST = STEPS - 1
 SCALAR_PIECES = {1: 1, 2: 3}
 GPSIMD_PIECES = {1: 5, 2: 11}
+W_SCALE_ROW = 4
 W1_BANKS = (((0, 0), (0, 1)), ((0, 2), (1, 2)), ((1, 0), (1, 1)))
 
 
@@ -37,8 +38,12 @@ def tile_distributedb_pa_t_kernel(tc, x_bytes, x_scale, h, Wv, W1, out):
         return 4 * PAIRS[i] if i < STEPS else 0
 
     def scalar_pieces(i):
-        if i in (0, LAST - 1, LAST):
+        if i == 0:
             return pieces(i) // 2
+        if i == LAST - 1:
+            return SCALAR_PIECES[PAIRS[i]] + 2
+        if i == LAST:
+            return pieces(i)
         return SCALAR_PIECES[PAIRS[i]] if i > 1 else 0
 
     with ExitStack() as ctx:
@@ -46,7 +51,7 @@ def tile_distributedb_pa_t_kernel(tc, x_bytes, x_scale, h, Wv, W1, out):
         raw = ctx.enter_context(tc.tile_pool(name="raw", bufs=4))
         wpool = ctx.enter_context(tc.tile_pool(name="wpool", bufs=2))
         stage = ctx.enter_context(tc.tile_pool(name="stage", bufs=2))
-        psum = ctx.enter_context(tc.psum_pool(name="psum", bufs=8))
+        psum = ctx.enter_context(tc.psum_pool(name="psum", bufs=1))
 
         scale = keep.tile([P, 8], F32, name="scale")
         ident = keep.tile([P, P], F32, name="ident", align_bytes=64)
@@ -69,8 +74,14 @@ def tile_distributedb_pa_t_kernel(tc, x_bytes, x_scale, h, Wv, W1, out):
         wv_stage, stages, quant, banks = {}, {}, {}, {}
         place = {}
 
-        def new_bank():
-            return psum.tile([P, PIECE], F32, name="bank")
+        by_age = list(range(8))
+        x_banks = []
+
+        def new_bank(avoid=()):
+            n = [b for b in by_age if b not in avoid][0]
+            by_age.remove(n)
+            by_age.append(n)
+            return psum.tile([P, PIECE], F32, name="bank%d" % n)
 
         def load_wv(s, t, n):
             w = keep.tile([P, n * D], BF16, name="wv_raw%d%d" % (s, t))
@@ -141,7 +152,7 @@ def tile_distributedb_pa_t_kernel(tc, x_bytes, x_scale, h, Wv, W1, out):
         def quant_wv(s, t):
             c = (4 * s + t) * 256
             nc.vector.quantize_mx(
-                out=wv_codes[:, c : c + 256].bitcast(X4), scales=wv_scales[:, c : c + 256], in_=wv_stage[s, t][:]
+                out=wv_codes[:, c : c + 256].bitcast(X4), scales=wv_scales[W_SCALE_ROW:, c : c + 256], in_=wv_stage[s, t][:]
             )
 
         def turn_w1(n):
@@ -155,7 +166,7 @@ def tile_distributedb_pa_t_kernel(tc, x_bytes, x_scale, h, Wv, W1, out):
         def quant_w1(lo, hi):
             nc.vector.quantize_mx(
                 out=w1_codes[:, lo * 256 : hi * 256].bitcast(X4),
-                scales=w1_scales[:, lo * 256 : hi * 256],
+                scales=w1_scales[W_SCALE_ROW:, lo * 256 : hi * 256],
                 in_=w1_stage[:, lo * D : hi * D],
             )
 
@@ -172,16 +183,17 @@ def tile_distributedb_pa_t_kernel(tc, x_bytes, x_scale, h, Wv, W1, out):
                 place["x", i, b] = w[:], hi - lo, b - lo
 
         def widen_on_vector(i):
-            widen_sorted(i, 0, pieces(i) - scalar_pieces(i))
+            if scalar_pieces(i) < pieces(i):
+                widen_sorted(i, 0, pieces(i) - scalar_pieces(i))
 
-        def widen_on_scalar(i):
+        def widen_on_scalar(i, share):
             lo = pieces(i) - scalar_pieces(i)
             tile, c = (h_raw[i + 1], pieces(i + 1)) if i else (early, 0)
             nc.scalar.copy(
-                out=tile[:, c * PIECE : (c + scalar_pieces(i)) * PIECE],
-                in_=x_raw[i][:, lo * PIECE : pieces(i) * PIECE].bitcast(F8),
+                out=tile[:, (c + share.start) * PIECE : (c + share.stop) * PIECE],
+                in_=x_raw[i][:, (lo + share.start) * PIECE : (lo + share.stop) * PIECE].bitcast(F8),
             )
-            for b in range(scalar_pieces(i)):
+            for b in share:
                 place["x", i, lo + b] = tile, None, c + b
 
         def turn_rows(kind, i, q, g):
@@ -229,7 +241,7 @@ def tile_distributedb_pa_t_kernel(tc, x_bytes, x_scale, h, Wv, W1, out):
                 nc.tensor.matmul_mx(
                     out=dst,
                     lhsT=wv_codes[:, w : w + P].bitcast(X4),
-                    lhsT_scale=wv_scales[:, w : w + P],
+                    lhsT_scale=wv_scales[W_SCALE_ROW:, w : w + P],
                     rhs=codes[:, r : r + n].bitcast(X4),
                     rhs_scale=scales[:, r : r + n],
                     start=(g == 0),
@@ -244,7 +256,7 @@ def tile_distributedb_pa_t_kernel(tc, x_bytes, x_scale, h, Wv, W1, out):
         def views(i, q, s):
             dst = views_stage(i, q, s)
             for a in range(2):
-                bank = new_bank()
+                bank = new_bank(x_banks)
                 for t in range(4):
                     first_product(bank[:, t * P : (t + 1) * P], i, s, t, q, a * P, P)
                 nc.scalar.copy(
@@ -255,7 +267,7 @@ def tile_distributedb_pa_t_kernel(tc, x_bytes, x_scale, h, Wv, W1, out):
         def views_wide(i, q, s):
             dst = views_stage(i, q, s).rearrange("p (n u e) -> p n u e", u=2, e=2)
             for u in range(2):
-                bank = new_bank()
+                bank = new_bank(x_banks)
                 for e in range(2):
                     first_product(bank[:, e * 256 : (e + 1) * 256], i, s, 2 * u + e, q, 0, 256)
                 nc.scalar.copy(out=dst[:, :, u, :], in_=bank[:].rearrange("p (e n) -> p n e", e=2))
@@ -273,7 +285,7 @@ def tile_distributedb_pa_t_kernel(tc, x_bytes, x_scale, h, Wv, W1, out):
                     lhsT=codes[:, c * P : (c + 1) * P].bitcast(X4),
                     lhsT_scale=scales[:, c * P : (c + 1) * P],
                     rhs=w1_codes[:, cols].bitcast(X4),
-                    rhs_scale=w1_scales[:, cols],
+                    rhs_scale=w1_scales[W_SCALE_ROW:, cols],
                     start=(k == 0),
                     stop=(k == len(passes) - 1),
                 )
@@ -335,7 +347,7 @@ def tile_distributedb_pa_t_kernel(tc, x_bytes, x_scale, h, Wv, W1, out):
                 load_x(i)
 
             widen_on_vector(0)
-            widen_on_scalar(0)
+            widen_on_scalar(0, range(scalar_pieces(0)))
             turn_wv(0, 0)
             for q, g in passes_of(0):
                 turn_x(0, q, g)
@@ -375,7 +387,7 @@ def tile_distributedb_pa_t_kernel(tc, x_bytes, x_scale, h, Wv, W1, out):
             quantise("x", 0)
             quant_w1(0, 2)
             quant_w1(2, 3)
-            widen_on_scalar(2)
+            widen_on_scalar(2, range(scalar_pieces(2)))
 
             for i in range(1, LAST):
                 if i + 3 <= STEPS:
@@ -386,19 +398,25 @@ def tile_distributedb_pa_t_kernel(tc, x_bytes, x_scale, h, Wv, W1, out):
                 sort_words(nc.gpsimd, h_raw[i + 2], GPSIMD_PIECES[PAIRS[i]], shared[i % 2])
                 for q, g in reversed(passes_of(i + 1)):
                     turn_h(i + 1, q, g)
+                ahead = PAIRS[i] - 1
+                if ahead and i + 2 < STEPS:
+                    widen_on_scalar(i + 2, range(ahead))
                 for q, g in passes_of(i):
                     turn_x(i, q, g)
+                x_banks.clear()
+                x_banks.extend(by_age[-PAIRS[i] :])
                 widen_on_vector(i + 1)
                 for n in range(NS * PAIRS[i]):
                     wide = i == LAST - 1 and n < NS * PAIRS[i] - 1
                     (views_wide if wide else views)(i, *divmod(n, NS))
                 if i + 2 < STEPS:
-                    widen_on_scalar(i + 2)
+                    widen_on_scalar(i + 2, range(ahead, scalar_pieces(i + 2)))
                 quantise("h", i + 1)
                 quantise("x", i)
                 for q in range(PAIRS[i - 1]):
                     finish(i - 1, q)
 
+            x_banks.clear()
             quantise("v", LAST - 1, 2, (0,))
             for q, g in passes_of(LAST):
                 turn_x(LAST, q, g)

@@ -23,6 +23,8 @@ STEPS = len(PAIRS)
 LAST = STEPS - 1
 SCALAR_PIECES = {1: 1, 2: 3}
 GPSIMD_PIECES = {1: 5, 2: 11}
+LAST_SHORT = 2
+VECTOR_PIECES = 3
 W_SCALE_ROW = 4
 W1_BANKS = (((0, 0), (0, 1)), ((0, 2), (1, 2)), ((1, 0), (1, 1)))
 
@@ -127,10 +129,11 @@ def tile_distributedb_pa_t_kernel(tc, x_bytes, x_scale, h, Wv, W1, out):
 
         def sort_words(engine, src, most, dst, at=0):
             keys = [key for key, (where, count, n) in place.items() if where is src][:most]
+            first = place[keys[0]][2]
             part = dst[:, at * PIECE : (at + len(keys)) * PIECE]
             engine.tensor_copy(
                 out=part.bitcast(F32).rearrange("p (u n) -> p u n", u=2),
-                in_=src[:, : len(keys) * PIECE].bitcast(F32).rearrange("p (n u) -> p u n", u=2),
+                in_=src[:, first * PIECE : (first + len(keys)) * PIECE].bitcast(F32).rearrange("p (n u) -> p u n", u=2),
             )
             for n, key in enumerate(keys):
                 place[key] = part, len(keys), n
@@ -394,6 +397,8 @@ def tile_distributedb_pa_t_kernel(tc, x_bytes, x_scale, h, Wv, W1, out):
                     load_h(i + 3)
                 if i + 3 < STEPS:
                     load_x(i + 3)
+                if i == LAST_SHORT:
+                    sort_words(nc.vector, h_raw[i + 2], VECTOR_PIECES, early, 2)
                 quantise("v", i - 1)
                 sort_words(nc.gpsimd, h_raw[i + 2], GPSIMD_PIECES[PAIRS[i]], shared[i % 2])
                 for q, g in reversed(passes_of(i + 1)):
@@ -404,7 +409,7 @@ def tile_distributedb_pa_t_kernel(tc, x_bytes, x_scale, h, Wv, W1, out):
                 for q, g in passes_of(i):
                     turn_x(i, q, g)
                 x_banks.clear()
-                x_banks.extend(by_age[-PAIRS[i] :])
+                x_banks.extend(by_age[-(PAIRS[i] + 1) :])
                 widen_on_vector(i + 1)
                 for n in range(NS * PAIRS[i]):
                     wide = i == LAST - 1 and n < NS * PAIRS[i] - 1

@@ -46,6 +46,8 @@ def tile_distributedb_pa_t_kernel(tc, x_bytes, x_scale, h, Wv, W1, out):
             return SCALAR_PIECES[PAIRS[i]] + 2
         if i == LAST:
             return pieces(i)
+        if i > LAST_SHORT + 1:
+            return SCALAR_PIECES[PAIRS[i]] + 2
         return SCALAR_PIECES[PAIRS[i]] if i > 1 else 0
 
     with ExitStack() as ctx:
@@ -69,7 +71,7 @@ def tile_distributedb_pa_t_kernel(tc, x_bytes, x_scale, h, Wv, W1, out):
         w1_scales = keep.tile([P, 6 * P], U8, name="w1_scales", align_bytes=256)
         w1_stage = keep.tile([P, 6 * P * 4], BF16, name="w1_stage", align_bytes=256)
         width = max(pieces(i + 1) + scalar_pieces(i) for i in range(STEPS)) * PIECE
-        shared = [keep.tile([P, width], BF16, name="shared%d" % n, align_bytes=256) for n in range(2)]
+        shared = [keep.tile([P, GPSIMD_PIECES[2] * PIECE], BF16, name="shared%d" % n, align_bytes=256) for n in range(2)]
         early = keep.tile([P, 8 * PIECE], BF16, name="early", align_bytes=256)
 
         wv_raw, w1_raw, h_raw, x_raw = {}, {}, {}, {}
@@ -127,8 +129,8 @@ def tile_distributedb_pa_t_kernel(tc, x_bytes, x_scale, h, Wv, W1, out):
             c = (u * count + n) * P
             return where.bitcast(F32)[:, c : c + P]
 
-        def sort_words(engine, src, most, dst, at=0):
-            keys = [key for key, (where, count, n) in place.items() if where is src][:most]
+        def sort_words(engine, src, most, dst, at=0, skip=0):
+            keys = [key for key, (where, count, n) in place.items() if where is src][skip : skip + most]
             first = place[keys[0]][2]
             part = dst[:, at * PIECE : (at + len(keys)) * PIECE]
             engine.tensor_copy(
@@ -316,7 +318,7 @@ def tile_distributedb_pa_t_kernel(tc, x_bytes, x_scale, h, Wv, W1, out):
             for a in range(2):
                 bank = new_bank()
                 second_product(bank[:, :256], i, q, a, range(NS))
-                res = stage.tile([P, 256], F32, name="res_rows")
+                res = stage.tile([P, 256], F32, name="res", bufs=4)
                 nc.scalar.activation(out=res[:], in_=bank[:, :256], func=ACT.Silu)
                 nc.sync.dma_start(out=out_view(i, q)[:, :, a, :], in_=res[:].rearrange("p (s f) -> p s f", s=2))
 
@@ -325,7 +327,7 @@ def tile_distributedb_pa_t_kernel(tc, x_bytes, x_scale, h, Wv, W1, out):
                 bank = new_bank()
                 for a in range(2):
                     second_product(bank[:, a * P : (a + 1) * P], i, q, a, (s,))
-                res = stage.tile([P, 256], F32, name="res_subnet")
+                res = stage.tile([P, 256], F32, name="res", bufs=4)
                 nc.scalar.activation(out=res[:], in_=bank[:, :256], func=ACT.Silu)
                 nc.sync.dma_start(out=out_view(i, q)[:, s].rearrange("p a f -> p (a f)"), in_=res[:])
 
@@ -400,10 +402,11 @@ def tile_distributedb_pa_t_kernel(tc, x_bytes, x_scale, h, Wv, W1, out):
                 if i == LAST_SHORT:
                     sort_words(nc.vector, h_raw[i + 2], VECTOR_PIECES, early, 2)
                 quantise("v", i - 1)
-                sort_words(nc.gpsimd, h_raw[i + 2], GPSIMD_PIECES[PAIRS[i]], shared[i % 2])
+                left = pieces(i + 2) + scalar_pieces(i + 1) - GPSIMD_PIECES[2] if i > LAST_SHORT else 0
+                sort_words(nc.gpsimd, h_raw[i + 2], GPSIMD_PIECES[PAIRS[i]], shared[i % 2], skip=max(left, 0))
                 for q, g in reversed(passes_of(i + 1)):
                     turn_h(i + 1, q, g)
-                ahead = PAIRS[i] - 1
+                ahead = 2 * (PAIRS[i] - 1)
                 if ahead and i + 2 < STEPS:
                     widen_on_scalar(i + 2, range(ahead))
                 for q, g in passes_of(i):
@@ -411,6 +414,8 @@ def tile_distributedb_pa_t_kernel(tc, x_bytes, x_scale, h, Wv, W1, out):
                 x_banks.clear()
                 x_banks.extend(by_age[-(PAIRS[i] + 1) :])
                 widen_on_vector(i + 1)
+                if left > 0:
+                    sort_words(nc.vector, h_raw[i + 2], left, early, 0 if i % 2 else 5)
                 for n in range(NS * PAIRS[i]):
                     wide = i == LAST - 1 and n < NS * PAIRS[i] - 1
                     (views_wide if wide else views)(i, *divmod(n, NS))

@@ -60,6 +60,8 @@ def tile_distributedb_pa_t_kernel(tc, x_bytes, x_scale, h, Wv, W1, out):
         scale = keep.tile([P, 8], F32, name="scale")
         ident = keep.tile([P, P], F32, name="ident", align_bytes=64)
         make_identity(nc, ident[:])
+        ident16 = keep.tile([P, P], BF16, name="ident16", align_bytes=64)
+        make_identity(nc, ident16[:])
         ones = keep.tile([P, 1], F32, name="ones")
         nc.vector.memset(ones[:], 1.0)
         table_load = keep.tile([P, 1], F32, name="table_load")
@@ -79,6 +81,7 @@ def tile_distributedb_pa_t_kernel(tc, x_bytes, x_scale, h, Wv, W1, out):
         place = {}
 
         by_age = list(range(8))
+        edge = []
         x_banks = []
 
         def new_bank(avoid=()):
@@ -221,6 +224,44 @@ def tile_distributedb_pa_t_kernel(tc, x_bytes, x_scale, h, Wv, W1, out):
                 out=dst.rearrange("p (n u e) -> p n u e", u=2, e=2),
                 in0=bank[:].bitcast(BF16).rearrange("p (u n e) -> p n u e", u=2, e=2),
                 in1=sc.unsqueeze(1).to_broadcast([P, 256, 2, 2]),
+                op=MULT,
+            )
+
+        def turn_values(bank, i, u):
+            pairs = words_of("x", i, 0, u).bitcast(BF16)
+            for e in range(2):
+                t = 2 * u + e
+                nc.tensor.matmul(
+                    out=bank[:].bitcast(BF16)[:, t * P : (t + 1) * P],
+                    lhsT=pairs[:, e : 2 * P : 2],
+                    rhs=ident16[:],
+                    start=True,
+                    stop=True,
+                )
+
+        def open_run(i):
+            banks["x", i, 0, 0] = new_bank()
+            edge.append(by_age[-1])
+            turn_values(banks["x", i, 0, 0], i, 0)
+
+        def close_run(i):
+            bank = banks["x", i, 0, 0]
+            for u in range(2):
+                nc.tensor.transpose(bank[:, (2 + u) * P : (3 + u) * P], words_of("x", i, 2, u), ident[:])
+            turn_values(bank, i, 1)
+            by_age.remove(edge[-1])
+            by_age.append(edge[-1])
+            dst = stages["x", i][:, :D]
+            nc.vector.tensor_tensor(
+                out=dst[:, :PIECE].rearrange("p (n t) -> p n t", t=4),
+                in0=bank[:].bitcast(BF16)[:, :PIECE].rearrange("p (t n) -> p n t", t=4),
+                in1=scale[:, 0:4].unsqueeze(1).to_broadcast([P, P, 4]),
+                op=MULT,
+            )
+            nc.vector.tensor_tensor(
+                out=dst[:, PIECE:].rearrange("p (n u e) -> p n u e", u=2, e=2),
+                in0=bank[:].bitcast(BF16)[:, PIECE:].rearrange("p (u n e) -> p n u e", u=2, e=2),
+                in1=scale[:, 0:4].rearrange("p (u e) -> p u e", u=2).unsqueeze(1).to_broadcast([P, P, 2, 2]),
                 op=MULT,
             )
 
@@ -404,13 +445,18 @@ def tile_distributedb_pa_t_kernel(tc, x_bytes, x_scale, h, Wv, W1, out):
                 quantise("v", i - 1)
                 left = pieces(i + 2) + scalar_pieces(i + 1) - GPSIMD_PIECES[2] if i > LAST_SHORT else 0
                 sort_words(nc.gpsimd, h_raw[i + 2], GPSIMD_PIECES[PAIRS[i]], shared[i % 2], skip=max(left, 0))
+                edged = i > LAST_SHORT + 1
+                if edged:
+                    open_run(i)
                 for q, g in reversed(passes_of(i + 1)):
                     turn_h(i + 1, q, g)
                 ahead = 2 * (PAIRS[i] - 1)
                 if ahead and i + 2 < STEPS:
                     widen_on_scalar(i + 2, range(ahead))
-                for q, g in passes_of(i):
+                for q, g in passes_of(i)[edged:]:
                     turn_x(i, q, g)
+                if edged:
+                    close_run(i)
                 x_banks.clear()
                 x_banks.extend(by_age[-(PAIRS[i] + 1) :])
                 widen_on_vector(i + 1)

@@ -21,10 +21,10 @@ PIECE = 512
 PAIRS = (1,) * 3 + (2,) * 6 + (1,)
 STEPS = len(PAIRS)
 LAST = STEPS - 1
-SCALAR_PIECES = {1: 1, 2: 3}
-GPSIMD_PIECES = {1: 5, 2: 11}
 LAST_SHORT = 2
-VECTOR_PIECES = 3
+FIRST_LONG_PIECES = 3
+SHORT_SORT = 5
+AHEAD = 2
 W_SCALE_ROW = 4
 W1_BANKS = (((0, 0), (0, 1)), ((0, 2), (1, 2)), ((1, 0), (1, 1)))
 
@@ -40,15 +40,16 @@ def tile_distributedb_pa_t_kernel(tc, x_bytes, x_scale, h, Wv, W1, out):
         return 4 * PAIRS[i] if i < STEPS else 0
 
     def scalar_pieces(i):
-        if i == 0:
-            return pieces(i) // 2
-        if i == LAST - 1:
-            return SCALAR_PIECES[PAIRS[i]] + 2
+        if 0 < i <= LAST_SHORT:
+            return i - 1
+        if i == LAST_SHORT + 1:
+            return FIRST_LONG_PIECES
         if i == LAST:
             return pieces(i)
-        if i > LAST_SHORT + 1:
-            return SCALAR_PIECES[PAIRS[i]] + 2
-        return SCALAR_PIECES[PAIRS[i]] if i > 1 else 0
+        return pieces(i) // 2 + (i == LAST - 1)
+
+    def unsorted(i):
+        return pieces(i) + scalar_pieces(i - 1) - 1
 
     with ExitStack() as ctx:
         keep = ctx.enter_context(tc.tile_pool(name="keep", bufs=1))
@@ -73,7 +74,8 @@ def tile_distributedb_pa_t_kernel(tc, x_bytes, x_scale, h, Wv, W1, out):
         w1_scales = keep.tile([P, 6 * P], U8, name="w1_scales", align_bytes=256)
         w1_stage = keep.tile([P, 6 * P * 4], BF16, name="w1_stage", align_bytes=256)
         width = max(pieces(i + 1) + scalar_pieces(i) for i in range(STEPS)) * PIECE
-        shared = [keep.tile([P, GPSIMD_PIECES[2] * PIECE], BF16, name="shared%d" % n, align_bytes=256) for n in range(2)]
+        room = max(2 * PAIRS[i - 1] + unsorted(i + 2) for i in range(1, LAST)) * PIECE
+        shared = [keep.tile([P, room], BF16, name="shared%d" % n, align_bytes=256) for n in range(2)]
         early = keep.tile([P, 8 * PIECE], BF16, name="early", align_bytes=256)
 
         wv_raw, w1_raw, h_raw, x_raw = {}, {}, {}, {}
@@ -81,7 +83,7 @@ def tile_distributedb_pa_t_kernel(tc, x_bytes, x_scale, h, Wv, W1, out):
         place = {}
 
         by_age = list(range(8))
-        edge = []
+        edge = {}
         x_banks = []
 
         def new_bank(avoid=()):
@@ -115,7 +117,7 @@ def tile_distributedb_pa_t_kernel(tc, x_bytes, x_scale, h, Wv, W1, out):
             nc.sync.dma_start(out=dst, in_=rows[row0[i] : row0[i + 1], :].rearrange("(q p a) k -> p q (a k)", p=P, a=2))
 
         def load_h(i):
-            h_raw[i] = raw.tile([P, width], BF16, name="h_raw", align_bytes=256)
+            h_raw[i] = raw.tile([P, width], BF16, name="h_raw", align_bytes=256, bufs=3)
             if i < STEPS:
                 load_rows(h_raw[i], h_rows, i)
                 for b in range(pieces(i)):
@@ -132,8 +134,8 @@ def tile_distributedb_pa_t_kernel(tc, x_bytes, x_scale, h, Wv, W1, out):
             c = (u * count + n) * P
             return where.bitcast(F32)[:, c : c + P]
 
-        def sort_words(engine, src, most, dst, at=0, skip=0):
-            keys = [key for key, (where, count, n) in place.items() if where is src][skip : skip + most]
+        def sort_words(engine, src, most, dst, at=0):
+            keys = [key for key, (where, count, n) in place.items() if where is src][:most]
             first = place[keys[0]][2]
             part = dst[:, at * PIECE : (at + len(keys)) * PIECE]
             engine.tensor_copy(
@@ -227,43 +229,52 @@ def tile_distributedb_pa_t_kernel(tc, x_bytes, x_scale, h, Wv, W1, out):
                 op=MULT,
             )
 
-        def turn_values(bank, i, u):
-            pairs = words_of("x", i, 0, u).bitcast(BF16)
-            for e in range(2):
-                t = 2 * u + e
-                nc.tensor.matmul(
-                    out=bank[:].bitcast(BF16)[:, t * P : (t + 1) * P],
-                    lhsT=pairs[:, e : 2 * P : 2],
-                    rhs=ident16[:],
-                    start=True,
-                    stop=True,
-                )
+        def turn_values(dst, i, piece, t):
+            where, count, n = place["x", i, piece]
+            if count is None:
+                values = where[:, n * PIECE + t : (n + 1) * PIECE : 4]
+            else:
+                values = words_of("x", i, piece, t // 2).bitcast(BF16)[:, t % 2 : 2 * P : 2]
+            nc.tensor.matmul(out=dst, lhsT=values, rhs=ident16[:], start=True, stop=True)
 
         def open_run(i):
-            banks["x", i, 0, 0] = new_bank()
-            edge.append(by_age[-1])
-            turn_values(banks["x", i, 0, 0], i, 0)
+            edge[i] = new_bank(), by_age[-1]
+            for t in range(2):
+                turn_values(edge[i][0][:].bitcast(BF16)[:, PIECE + t * P : PIECE + (t + 1) * P], i, pieces(i) - 1, t)
 
         def close_run(i):
-            bank = banks["x", i, 0, 0]
+            bank, n = edge[i]
             for u in range(2):
-                nc.tensor.transpose(bank[:, (2 + u) * P : (3 + u) * P], words_of("x", i, 2, u), ident[:])
-            turn_values(bank, i, 1)
-            by_age.remove(edge[-1])
-            by_age.append(edge[-1])
-            dst = stages["x", i][:, :D]
+                nc.tensor.transpose(bank[:, u * P : (u + 1) * P], words_of("x", i, pieces(i) - 3, u), ident[:])
+            for t in range(2, 4):
+                turn_values(bank[:].bitcast(BF16)[:, PIECE + t * P : PIECE + (t + 1) * P], i, pieces(i) - 1, t)
+            by_age.remove(n)
+            by_age.append(n)
+            c = (2 * PAIRS[i] - 1) * D
+            dst = stages["x", i][:, c : c + D]
             nc.vector.tensor_tensor(
-                out=dst[:, :PIECE].rearrange("p (n t) -> p n t", t=4),
-                in0=bank[:].bitcast(BF16)[:, :PIECE].rearrange("p (t n) -> p n t", t=4),
-                in1=scale[:, 0:4].unsqueeze(1).to_broadcast([P, P, 4]),
+                out=dst[:, :PIECE].rearrange("p (n u e) -> p n u e", u=2, e=2),
+                in0=bank[:].bitcast(BF16)[:, :PIECE].rearrange("p (u n e) -> p n u e", u=2, e=2),
+                in1=scale[:, 4:8].rearrange("p (u e) -> p u e", u=2).unsqueeze(1).to_broadcast([P, P, 2, 2]),
                 op=MULT,
             )
             nc.vector.tensor_tensor(
-                out=dst[:, PIECE:].rearrange("p (n u e) -> p n u e", u=2, e=2),
-                in0=bank[:].bitcast(BF16)[:, PIECE:].rearrange("p (u n e) -> p n u e", u=2, e=2),
-                in1=scale[:, 0:4].rearrange("p (u e) -> p u e", u=2).unsqueeze(1).to_broadcast([P, P, 2, 2]),
+                out=dst[:, PIECE:].rearrange("p (n t) -> p n t", t=4),
+                in0=bank[:].bitcast(BF16)[:, PIECE:].rearrange("p (t n) -> p n t", t=4),
+                in1=scale[:, 4:8].unsqueeze(1).to_broadcast([P, P, 4]),
                 op=MULT,
             )
+
+        def turn_run(i):
+            open_run(i)
+            if i < LAST:
+                for q, g in reversed(passes_of(i + 1)):
+                    turn_h(i + 1, q, g)
+                if PAIRS[i] > 1 and i + 2 < STEPS:
+                    widen_on_scalar(i + 2, range(AHEAD))
+            for q, g in passes_of(i)[:-1]:
+                turn_x(i, q, g)
+            close_run(i)
 
         def quantise(kind, i, parts=1, only=None):
             if (kind, i) not in quant:
@@ -359,7 +370,7 @@ def tile_distributedb_pa_t_kernel(tc, x_bytes, x_scale, h, Wv, W1, out):
             for a in range(2):
                 bank = new_bank()
                 second_product(bank[:, :256], i, q, a, range(NS))
-                res = stage.tile([P, 256], F32, name="res", bufs=4)
+                res = stage.tile([P, 256], F32, name="res_rows", bufs=4)
                 nc.scalar.activation(out=res[:], in_=bank[:, :256], func=ACT.Silu)
                 nc.sync.dma_start(out=out_view(i, q)[:, :, a, :], in_=res[:].rearrange("p (s f) -> p s f", s=2))
 
@@ -368,7 +379,7 @@ def tile_distributedb_pa_t_kernel(tc, x_bytes, x_scale, h, Wv, W1, out):
                 bank = new_bank()
                 for a in range(2):
                     second_product(bank[:, a * P : (a + 1) * P], i, q, a, (s,))
-                res = stage.tile([P, 256], F32, name="res", bufs=4)
+                res = stage.tile([P, 256], F32, name="res_rows", bufs=4)
                 nc.scalar.activation(out=res[:], in_=bank[:, :256], func=ACT.Silu)
                 nc.sync.dma_start(out=out_view(i, q)[:, s].rearrange("p a f -> p (a f)"), in_=res[:])
 
@@ -378,39 +389,38 @@ def tile_distributedb_pa_t_kernel(tc, x_bytes, x_scale, h, Wv, W1, out):
         with tc.manual_schedule():
             load_x(0)
             load_wv(0, 0, 1)
+            load_x(1)
             load_scale()
             load_h(0)
             load_wv(0, 1, 1)
             load_wv(0, 2, 2)
             load_wv(1, 0, 2)
-            load_x(1)
             load_wv(1, 2, 2)
             load_h(1)
             for s in range(NS):
                 load_w1(s)
-            for i in (2, 3):
-                load_h(i)
-                load_x(i)
+            load_x(2)
+            load_h(2)
 
             widen_on_vector(0)
             widen_on_scalar(0, range(scalar_pieces(0)))
+            widen_on_vector(1)
             turn_wv(0, 0)
             for q, g in passes_of(0):
                 turn_x(0, q, g)
             for q, g in passes_of(0):
                 turn_h(0, q, g)
+            load_h(3)
+            load_x(3)
             quant_wv(0, 0)
             quantise("h", 0)
             for t in range(1, 4):
                 turn_wv(0, t)
-                if t == 2:
-                    widen_sorted(1, 0, 2)
                 quant_wv(0, t)
             for t in range(2):
                 turn_wv(1, t)
             views(0, 0, 0)
             sort_words(nc.vector, wv_raw[1, 2], 4, shared[0])
-            widen_sorted(1, 2, 4)
             sort_words(nc.vector, h_raw[1], 4, shared[0], 4)
             sort_words(nc.vector, w1_raw[0], 3, early, 2)
             for t in range(2):
@@ -420,6 +430,7 @@ def tile_distributedb_pa_t_kernel(tc, x_bytes, x_scale, h, Wv, W1, out):
                 turn_wv(1, t)
             for q, g in passes_of(1):
                 turn_h(1, q, g)
+            widen_on_vector(2)
             for t in range(2, 4):
                 quant_wv(1, t)
             turn_w1(0)
@@ -441,41 +452,29 @@ def tile_distributedb_pa_t_kernel(tc, x_bytes, x_scale, h, Wv, W1, out):
                 if i + 3 < STEPS:
                     load_x(i + 3)
                 if i == LAST_SHORT:
-                    sort_words(nc.vector, h_raw[i + 2], VECTOR_PIECES, early, 2)
-                quantise("v", i - 1)
-                left = pieces(i + 2) + scalar_pieces(i + 1) - GPSIMD_PIECES[2] if i > LAST_SHORT else 0
-                sort_words(nc.gpsimd, h_raw[i + 2], GPSIMD_PIECES[PAIRS[i]], shared[i % 2], skip=max(left, 0))
-                edged = i > LAST_SHORT + 1
-                if edged:
-                    open_run(i)
-                for q, g in reversed(passes_of(i + 1)):
-                    turn_h(i + 1, q, g)
-                ahead = 2 * (PAIRS[i] - 1)
-                if ahead and i + 2 < STEPS:
-                    widen_on_scalar(i + 2, range(ahead))
-                for q, g in passes_of(i)[edged:]:
-                    turn_x(i, q, g)
-                if edged:
-                    close_run(i)
+                    left = unsorted(i + 2) - SHORT_SORT
+                    sort_words(nc.vector, h_raw[i + 2], left, early, 8 - left)
+                quantise("v", i - 1, 2, (1, 0))
+                most = SHORT_SORT if PAIRS[i] == 1 else unsorted(i + 2)
+                sort_words(nc.gpsimd, h_raw[i + 2], most, shared[i % 2], 2 * PAIRS[i - 1])
+                turn_run(i)
                 x_banks.clear()
                 x_banks.extend(by_age[-(PAIRS[i] + 1) :])
-                widen_on_vector(i + 1)
-                if left > 0:
-                    sort_words(nc.vector, h_raw[i + 2], left, early, 0 if i % 2 else 5)
+                if i > 1:
+                    widen_on_vector(i + 1)
                 for n in range(NS * PAIRS[i]):
                     wide = i == LAST - 1 and n < NS * PAIRS[i] - 1
                     (views_wide if wide else views)(i, *divmod(n, NS))
-                if i + 2 < STEPS:
-                    widen_on_scalar(i + 2, range(ahead, scalar_pieces(i + 2)))
                 quantise("h", i + 1)
                 quantise("x", i)
                 for q in range(PAIRS[i - 1]):
                     finish(i - 1, q)
+                if i + 2 < STEPS:
+                    widen_on_scalar(i + 2, range(AHEAD * (PAIRS[i] - 1), scalar_pieces(i + 2)))
 
             x_banks.clear()
             quantise("v", LAST - 1, 2, (0,))
-            for q, g in passes_of(LAST):
-                turn_x(LAST, q, g)
+            turn_run(LAST)
             quantise("v", LAST - 1, 2, (1,))
             views_wide(LAST, 0, 0)
             finish(LAST - 1, 0)

@@ -59,12 +59,14 @@ def tile_distributedb_pa_t_kernel(tc, x_bytes, x_scale, h, Wv, W1, out):
         psum = ctx.enter_context(tc.psum_pool(name="psum", bufs=1))
 
         scale = keep.tile([P, 8], F32, name="scale")
+        scale_rows = keep.tile([P, 256], F32, name="scale_rows")
         ident = keep.tile([P, P], F32, name="ident", align_bytes=64)
         make_identity(nc, ident[:])
         ident16 = keep.tile([P, P], BF16, name="ident16", align_bytes=64)
         make_identity(nc, ident16[:])
         ones = keep.tile([P, 1], F32, name="ones")
         nc.vector.memset(ones[:], 1.0)
+        nc.vector.memset(scale_rows[:], 0.0)
         table_load = keep.tile([P, 1], F32, name="table_load")
         nc.scalar.activation(out=table_load[:], in_=ones[:], func=ACT.Silu)
 
@@ -101,9 +103,19 @@ def tile_distributedb_pa_t_kernel(tc, x_bytes, x_scale, h, Wv, W1, out):
 
         def load_scale():
             nc.sync.dma_start(
-                out=scale[:].rearrange("p (g t) -> p g t", g=2),
-                in_=x_scale.rearrange("o b (g p t) -> p (o b g) t", g=2, p=P, t=4),
+                out=scale_rows[0:P:32, :].rearrange("c (g n) -> c g n", g=2),
+                in_=x_scale.rearrange("o b (g c n) -> c (o b g) n", g=2, c=4),
             )
+
+        def spread_scale():
+            by_t = keep.tile([P, 256], F32, name="scale_by_t", align_bytes=64)
+            nc.scalar.copy(
+                out=by_t[:].rearrange("p (g t j) -> p g t j", g=2, t=4),
+                in_=scale_rows[:].rearrange("p (g j t) -> p g t j", g=2, t=4),
+            )
+            turned = keep.tile([P, 256], F32, name="scale_turned", align_bytes=64)
+            nc.vector.transpose(out=turned[:], in_=by_t[:])
+            nc.scalar.copy(out=scale[:], in_=turned[:, 0:256:32])
 
         def load_w1(s):
             w = wpool.tile([P, 3 * PIECE], BF16, name="w1_raw")
@@ -113,8 +125,8 @@ def tile_distributedb_pa_t_kernel(tc, x_bytes, x_scale, h, Wv, W1, out):
             w1_raw[s] = w
 
         def load_rows(tile, rows, i):
-            dst = tile[:, : pieces(i) * PIECE].rearrange("p (q c) -> p q c", c=2 * D)
-            nc.sync.dma_start(out=dst, in_=rows[row0[i] : row0[i + 1], :].rearrange("(q p a) k -> p q (a k)", p=P, a=2))
+            src = rows[row0[i] : row0[i + 1], :].rearrange("(p n) k -> p (n k)", p=P)
+            nc.sync.dma_start(out=tile[:, : pieces(i) * PIECE], in_=src)
 
         def load_h(i):
             h_raw[i] = raw.tile([P, width], BF16, name="h_raw", align_bytes=256, bufs=3)
@@ -167,11 +179,11 @@ def tile_distributedb_pa_t_kernel(tc, x_bytes, x_scale, h, Wv, W1, out):
 
         def turn_w1(n):
             turn(("w1", n), [words_of("w1", s, j, u) for s, j in W1_BANKS[n] for u in range(2)])
-
-        def copy_w1(n, copy):
             lo, hi = [2 * j + s for s, j in W1_BANKS[n]]
             dst = w1_stage[:].bitcast(F32).rearrange("p (c f u) -> p c f u", f=P, u=2)
-            copy(out=dst[:, lo : hi + 1 : hi - lo], in_=banks["w1", n][:].rearrange("p (c u f) -> p c f u", c=2, u=2))
+            nc.scalar.copy(
+                out=dst[:, lo : hi + 1 : hi - lo], in_=banks["w1", n][:].rearrange("p (c u f) -> p c f u", c=2, u=2)
+            )
 
         def quant_w1(lo, hi):
             nc.vector.quantize_mx(
@@ -348,8 +360,8 @@ def tile_distributedb_pa_t_kernel(tc, x_bytes, x_scale, h, Wv, W1, out):
                 )
 
         def out_view(i, q):
-            r = row0[i] + 256 * q
-            return out_rows[:, r : r + 256, :].rearrange("s (p a) f -> p s a f", p=P)
+            rows = out_rows[:, row0[i] : row0[i + 1], :].rearrange("s (p n) f -> p s n f", p=P)
+            return rows[:, :, 2 * q : 2 * q + 2, :]
 
         def finish(i, q):
             bank = new_bank()
@@ -388,57 +400,56 @@ def tile_distributedb_pa_t_kernel(tc, x_bytes, x_scale, h, Wv, W1, out):
 
         with tc.manual_schedule():
             load_x(0)
-            load_wv(0, 0, 1)
-            load_x(1)
             load_scale()
+            load_wv(0, 0, 2)
+            load_x(1)
             load_h(0)
-            load_wv(0, 1, 1)
             load_wv(0, 2, 2)
-            load_wv(1, 0, 2)
-            load_wv(1, 2, 2)
+            for t in (0, 2):
+                load_wv(1, t, 2)
             load_h(1)
             for s in range(NS):
                 load_w1(s)
-            load_x(2)
             load_h(2)
+            load_x(2)
 
             widen_on_vector(0)
             widen_on_scalar(0, range(scalar_pieces(0)))
+            spread_scale()
             widen_on_vector(1)
-            turn_wv(0, 0)
             for q, g in passes_of(0):
                 turn_x(0, q, g)
+            for t in range(2):
+                turn_wv(0, t)
             for q, g in passes_of(0):
                 turn_h(0, q, g)
             load_h(3)
             load_x(3)
             quant_wv(0, 0)
             quantise("h", 0)
-            for t in range(1, 4):
+            quant_wv(0, 1)
+            for t in range(2, 4):
                 turn_wv(0, t)
                 quant_wv(0, t)
             for t in range(2):
                 turn_wv(1, t)
             views(0, 0, 0)
             sort_words(nc.vector, wv_raw[1, 2], 4, shared[0])
-            sort_words(nc.vector, h_raw[1], 4, shared[0], 4)
-            sort_words(nc.vector, w1_raw[0], 3, early, 2)
             for t in range(2):
                 quant_wv(1, t)
-            sort_words(nc.vector, w1_raw[1], 3, early, 5)
+            sort_words(nc.vector, h_raw[1], 4, shared[0], 4)
+            for s in range(NS):
+                sort_words(nc.vector, w1_raw[s], 3, early, 2 + 3 * s)
             for t in range(2, 4):
                 turn_wv(1, t)
             for q, g in passes_of(1):
                 turn_h(1, q, g)
-            widen_on_vector(2)
             for t in range(2, 4):
                 quant_wv(1, t)
-            turn_w1(0)
-            sort_words(nc.vector, h_raw[2], 4, shared[0])
-            copy_w1(0, nc.vector.tensor_copy)
-            for n in (1, 2):
+            for n in range(len(W1_BANKS)):
                 turn_w1(n)
-                copy_w1(n, nc.scalar.copy)
+            sort_words(nc.vector, h_raw[2], 4, shared[0])
+            widen_on_vector(2)
             quantise("h", 1)
             views(0, 0, 1)
             quantise("x", 0)

from contextlib import ExitStack

import concourse.mybir as mybir
from concourse.masks import make_identity

FLOPS = 2 * 4096 * 1024 * 1024 + 2 * 4096 * 256 * 1536

F32 = mybir.dt.float32
BF16 = mybir.dt.bfloat16
U32 = mybir.dt.uint32
U8 = mybir.dt.uint8
F8 = mybir.dt.float8_e4m3fn
X4 = mybir.dt.float8_e4m3fn_x4
MULT = mybir.AluOpType.mult
ACT = mybir.ActivationFunctionType

P = 128
D = 1024
NS = 2
PIECE = 512
PAIRS = (1,) * 3 + (2,) * 6 + (1,)
STEPS = len(PAIRS)
LAST = STEPS - 1
LAST_SHORT = 2
FIRST_LONG_PIECES = 3
SHORT_SORT = 5
AHEAD = 2
W_SCALE_ROW = 4
W1_BANKS = (((0, 0), (0, 1)), ((0, 2), (1, 2)), ((1, 0), (1, 1)))


def tile_distributedb_pa_t_kernel(tc, x_bytes, x_scale, h, Wv, W1, out):
    nc = tc.nc
    x_rows = x_bytes.rearrange("b r k -> (b r) k")
    h_rows = h.rearrange("b r k -> (b r) k")
    out_rows = out.rearrange("s b r f -> s (b r) f")
    row0 = [256 * sum(PAIRS[:i]) for i in range(STEPS + 1)]

    def pieces(i):
        return 4 * PAIRS[i] if i < STEPS else 0

    def scalar_pieces(i):
        if 0 < i <= LAST_SHORT:
            return i - 1
        if i == LAST_SHORT + 1:
            return FIRST_LONG_PIECES
        if i == LAST:
            return pieces(i)
        return pieces(i) // 2 + (i == LAST - 1)

    def unsorted(i):
        return pieces(i) + scalar_pieces(i - 1) - 1

    with ExitStack() as ctx:
        keep = ctx.enter_context(tc.tile_pool(name="keep", bufs=1))
        raw = ctx.enter_context(tc.tile_pool(name="raw", bufs=4))
        wpool = ctx.enter_context(tc.tile_pool(name="wpool", bufs=2))
        stage = ctx.enter_context(tc.tile_pool(name="stage", bufs=2))
        psum = ctx.enter_context(tc.psum_pool(name="psum", bufs=1))

        scale = keep.tile([P, 8], F32, name="scale")
        scale_rows = keep.tile([P, 256], F32, name="scale_rows")
        ident = keep.tile([P, P], F32, name="ident", align_bytes=64)
        make_identity(nc, ident[:])
        ident16 = keep.tile([P, P], BF16, name="ident16", align_bytes=64)
        make_identity(nc, ident16[:])
        ones = keep.tile([P, 1], F32, name="ones")
        nc.vector.memset(ones[:], 1.0)
        nc.vector.memset(scale_rows[:], 0.0)
        table_load = keep.tile([P, 1], F32, name="table_load")
        nc.scalar.activation(out=table_load[:], in_=ones[:], func=ACT.Silu)

        wv_codes = keep.tile([P, 4 * 512], U32, name="wv_codes", align_bytes=256)
        wv_scales = keep.tile([P, 4 * 512], U8, name="wv_scales", align_bytes=256)
        w1_codes = keep.tile([P, 6 * P], U32, name="w1_codes", align_bytes=256)
        w1_scales = keep.tile([P, 6 * P], U8, name="w1_scales", align_bytes=256)
        w1_stage = keep.tile([P, 6 * P * 4], BF16, name="w1_stage", align_bytes=256)
        width = max(pieces(i + 1) + scalar_pieces(i) for i in range(STEPS)) * PIECE
        room = max(2 * PAIRS[i - 1] + unsorted(i + 2) for i in range(1, LAST)) * PIECE
        shared = [keep.tile([P, room], BF16, name="shared%d" % n, align_bytes=256) for n in range(2)]
        early = keep.tile([P, 8 * PIECE], BF16, name="early", align_bytes=256)

        wv_raw, w1_raw, h_raw, x_raw = {}, {}, {}, {}
        wv_stage, stages, quant, banks = {}, {}, {}, {}
        place = {}

        by_age = list(range(8))
        edge = {}
        x_banks = []

        def new_bank(avoid=()):
            n = [b for b in by_age if b not in avoid][0]
            by_age.remove(n)
            by_age.append(n)
            return psum.tile([P, PIECE], F32, name="bank%d" % n)

        def load_wv(s, t, n):
            w = keep.tile([P, n * D], BF16, name="wv_raw%d%d" % (s, t))
            nc.sync.dma_start(out=w[:], in_=Wv[s].rearrange("(m t) k -> m (t k)", t=4)[:, t * D : (t + n) * D])
            for b in range(2 * n):
                place["wv", s, 2 * t + b] = w, None, b
            wv_raw[s, t] = w

        def load_scale():
            nc.sync.dma_start(
                out=scale_rows[0:P:32, :].rearrange("c (g n) -> c g n", g=2),
                in_=x_scale.rearrange("o b (g c n) -> c (o b g) n", g=2, c=4),
            )

        def spread_scale():
            by_t = keep.tile([P, 256], F32, name="scale_by_t", align_bytes=64)
            nc.scalar.copy(
                out=by_t[:].rearrange("p (g t j) -> p g t j", g=2, t=4),
                in_=scale_rows[:].rearrange("p (g j t) -> p g t j", g=2, t=4),
            )
            turned = keep.tile([P, 256], F32, name="scale_turned", align_bytes=64)
            nc.vector.transpose(out=turned[:], in_=by_t[:])
            nc.scalar.copy(out=scale[:], in_=turned[:, 0:256:32])

        def load_w1(s):
            w = wpool.tile([P, 3 * PIECE], BF16, name="w1_raw")
            nc.sync.dma_start(out=w[:], in_=W1[s])
            for j in range(3):
                place["w1", s, j] = w, None, j
            w1_raw[s] = w

        def load_rows(tile, rows, i):
            src = rows[row0[i] : row0[i + 1], :].rearrange("(p n) k -> p (n k)", p=P)
            nc.sync.dma_start(out=tile[:, : pieces(i) * PIECE], in_=src)

        def load_h(i):
            h_raw[i] = raw.tile([P, width], BF16, name="h_raw", align_bytes=256, bufs=3)
            if i < STEPS:
                load_rows(h_raw[i], h_rows, i)
                for b in range(pieces(i)):
                    place["h", i, b] = h_raw[i], None, b

        def load_x(i):
            x_raw[i] = raw.tile([P, 4 * D], U8, name="x_raw")
            load_rows(x_raw[i], x_rows, i)

        def words_of(kind, i, piece, u):
            where, count, n = place[kind, i, piece]
            if count is None:
                return where[:].bitcast(F32)[:, 256 * n + u : 256 * (n + 1) : 2]
            c = (u * count + n) * P
            return where.bitcast(F32)[:, c : c + P]

        def sort_words(engine, src, most, dst, at=0):
            keys = [key for key, (where, count, n) in place.items() if where is src][:most]
            first = place[keys[0]][2]
            part = dst[:, at * PIECE : (at + len(keys)) * PIECE]
            engine.tensor_copy(
                out=part.bitcast(F32).rearrange("p (u n) -> p u n", u=2),
                in_=src[:, first * PIECE : (first + len(keys)) * PIECE].bitcast(F32).rearrange("p (n u) -> p u n", u=2),
            )
            for n, key in enumerate(keys):
                place[key] = part, len(keys), n

        def turn(key, parts):
            bank = new_bank()
            for c, words in enumerate(parts):
                nc.tensor.transpose(bank[:, c * P : (c + 1) * P], words, ident[:])
            banks[key] = bank

        def turn_wv(s, t):
            turn(("wv", s, t), [words_of("wv", s, 2 * t + g, u) for g in range(2) for u in range(2)])
            wv_stage[s, t] = wpool.tile([P, D], BF16, name="wv_stage", align_bytes=256, bufs=4)
            nc.scalar.copy(
                out=wv_stage[s, t][:].bitcast(F32).rearrange("p (g m u) -> p g m u", g=2, u=2),
                in_=banks["wv", s, t][:].rearrange("p (g u m) -> p g m u", g=2, u=2),
            )

        def quant_wv(s, t):
            c = (4 * s + t) * 256
            nc.vector.quantize_mx(
                out=wv_codes[:, c : c + 256].bitcast(X4), scales=wv_scales[W_SCALE_ROW:, c : c + 256], in_=wv_stage[s, t][:]
            )

        def turn_w1(n):
            turn(("w1", n), [words_of("w1", s, j, u) for s, j in W1_BANKS[n] for u in range(2)])
            lo, hi = [2 * j + s for s, j in W1_BANKS[n]]
            dst = w1_stage[:].bitcast(F32).rearrange("p (c f u) -> p c f u", f=P, u=2)
            nc.scalar.copy(
                out=dst[:, lo : hi + 1 : hi - lo], in_=banks["w1", n][:].rearrange("p (c u f) -> p c f u", c=2, u=2)
            )

        def quant_w1(lo, hi):
            nc.vector.quantize_mx(
                out=w1_codes[:, lo * 256 : hi * 256].bitcast(X4),
                scales=w1_scales[W_SCALE_ROW:, lo * 256 : hi * 256],
                in_=w1_stage[:, lo * D : hi * D],
            )

        def widen_sorted(i, lo, hi):
            w = stage.tile([P, (hi - lo) * PIECE], BF16, name="x_wide", align_bytes=256, bufs=3)
            nc.vector.tensor_scalar(
                out=w[:].rearrange("p (u n e) -> p n u e", u=2, e=2),
                in0=x_raw[i][:, lo * PIECE : hi * PIECE].bitcast(F8).rearrange("p (n u e) -> p n u e", u=2, e=2),
                scalar1=ones[:, 0:1],
                scalar2=None,
                op0=MULT,
            )
            for b in range(lo, hi):
                place["x", i, b] = w[:], hi - lo, b - lo

        def widen_on_vector(i):
            if scalar_pieces(i) < pieces(i):
                widen_sorted(i, 0, pieces(i) - scalar_pieces(i))

        def widen_on_scalar(i, share):
            lo = pieces(i) - scalar_pieces(i)
            tile, c = (h_raw[i + 1], pieces(i + 1)) if i else (early, 0)
            nc.scalar.copy(
                out=tile[:, (c + share.start) * PIECE : (c + share.stop) * PIECE],
                in_=x_raw[i][:, (lo + share.start) * PIECE : (lo + share.stop) * PIECE].bitcast(F8),
            )
            for b in share:
                place["x", i, lo + b] = tile, None, c + b

        def turn_rows(kind, i, q, g):
            turn((kind, i, q, g), [words_of(kind, i, 4 * q + 2 * a + g, u) for u in range(2) for a in range(2)])
            if (kind, i) not in stages:
                stages[kind, i] = stage.tile([P, 4 * D], BF16, name=kind + "_stage", align_bytes=256)
            c = (2 * q + g) * D
            return banks[kind, i, q, g], stages[kind, i][:, c : c + D]

        def turn_h(i, q, g):
            bank, dst = turn_rows("h", i, q, g)
            nc.scalar.copy(
                out=dst.bitcast(F32).rearrange("p (n u) -> p n u", u=2), in_=bank[:].rearrange("p (u n) -> p n u", u=2)
            )

        def turn_x(i, q, g):
            bank, dst = turn_rows("x", i, q, g)
            sc = scale[:, 4 * g : 4 * g + 4].rearrange("p (u e) -> p u e", u=2)
            nc.vector.tensor_tensor(
                out=dst.rearrange("p (n u e) -> p n u e", u=2, e=2),
                in0=bank[:].bitcast(BF16).rearrange("p (u n e) -> p n u e", u=2, e=2),
                in1=sc.unsqueeze(1).to_broadcast([P, 256, 2, 2]),
                op=MULT,
            )

        def turn_values(dst, i, piece, t):
            where, count, n = place["x", i, piece]
            if count is None:
                values = where[:, n * PIECE + t : (n + 1) * PIECE : 4]
            else:
                values = words_of("x", i, piece, t // 2).bitcast(BF16)[:, t % 2 : 2 * P : 2]
            nc.tensor.matmul(out=dst, lhsT=values, rhs=ident16[:], start=True, stop=True)

        def open_run(i):
            edge[i] = new_bank(), by_age[-1]
            for t in range(2):
                turn_values(edge[i][0][:].bitcast(BF16)[:, PIECE + t * P : PIECE + (t + 1) * P], i, pieces(i) - 1, t)

        def close_run(i):
            bank, n = edge[i]
            for u in range(2):
                nc.tensor.transpose(bank[:, u * P : (u + 1) * P], words_of("x", i, pieces(i) - 3, u), ident[:])
            for t in range(2, 4):
                turn_values(bank[:].bitcast(BF16)[:, PIECE + t * P : PIECE + (t + 1) * P], i, pieces(i) - 1, t)
            by_age.remove(n)
            by_age.append(n)
            c = (2 * PAIRS[i] - 1) * D
            dst = stages["x", i][:, c : c + D]
            nc.vector.tensor_tensor(
                out=dst[:, :PIECE].rearrange("p (n u e) -> p n u e", u=2, e=2),
                in0=bank[:].bitcast(BF16)[:, :PIECE].rearrange("p (u n e) -> p n u e", u=2, e=2),
                in1=scale[:, 4:8].rearrange("p (u e) -> p u e", u=2).unsqueeze(1).to_broadcast([P, P, 2, 2]),
                op=MULT,
            )
            nc.vector.tensor_tensor(
                out=dst[:, PIECE:].rearrange("p (n t) -> p n t", t=4),
                in0=bank[:].bitcast(BF16)[:, PIECE:].rearrange("p (t n) -> p n t", t=4),
                in1=scale[:, 4:8].unsqueeze(1).to_broadcast([P, P, 4]),
                op=MULT,
            )

        def turn_run(i):
            open_run(i)
            if i < LAST:
                for q, g in reversed(passes_of(i + 1)):
                    turn_h(i + 1, q, g)
                if PAIRS[i] > 1 and i + 2 < STEPS:
                    widen_on_scalar(i + 2, range(AHEAD))
            for q, g in passes_of(i)[:-1]:
                turn_x(i, q, g)
            close_run(i)

        def quantise(kind, i, parts=1, only=None):
            if (kind, i) not in quant:
                codes = stage.tile([P, D], U32, name=kind + "_codes", align_bytes=256)
                scales = stage.tile([P, D], U8, name=kind + "_scales", align_bytes=256)
                quant[kind, i] = codes, scales
            codes, scales = quant[kind, i]
            n = PAIRS[i] * 512 // parts
            for k in only or range(parts):
                nc.vector.quantize_mx(
                    out=codes[:, k * n : (k + 1) * n].bitcast(X4),
                    scales=scales[:, k * n : (k + 1) * n],
                    in_=stages[kind, i][:, 4 * k * n : 4 * (k + 1) * n],
                )

        def first_product(dst, i, s, t, q, c, n):
            codes, scales = quant["h", i]
            for g in range(2):
                w = ((4 * s + t) * 2 + g) * P
                r = (2 * q + g) * 256 + c
                nc.tensor.matmul_mx(
                    out=dst,
                    lhsT=wv_codes[:, w : w + P].bitcast(X4),
                    lhsT_scale=wv_scales[W_SCALE_ROW:, w : w + P],
                    rhs=codes[:, r : r + n].bitcast(X4),
                    rhs_scale=scales[:, r : r + n],
                    start=(g == 0),
                    stop=(g == 1),
                )

        def views_stage(i, q, s):
            stages["v", i] = shared[(i + 1) % 2]
            k = (2 * q + s) * D
            return stages["v", i][:, k : k + D]

        def views(i, q, s):
            dst = views_stage(i, q, s)
            for a in range(2):
                bank = new_bank(x_banks)
                for t in range(4):
                    first_product(bank[:, t * P : (t + 1) * P], i, s, t, q, a * P, P)
                nc.scalar.copy(
                    out=dst[:, a * 512 : (a + 1) * 512].rearrange("p (r t) -> p r t", t=4),
                    in_=bank[:].rearrange("p (t r) -> p r t", t=4),
                )

        def views_wide(i, q, s):
            dst = views_stage(i, q, s).rearrange("p (n u e) -> p n u e", u=2, e=2)
            for u in range(2):
                bank = new_bank(x_banks)
                for e in range(2):
                    first_product(bank[:, e * 256 : (e + 1) * 256], i, s, 2 * u + e, q, 0, 256)
                nc.scalar.copy(out=dst[:, :, u, :], in_=bank[:].rearrange("p (e n) -> p n e", e=2))

        def second_product(dst, i, q, a, subnets):
            n = len(subnets) * P
            passes = [("x", (2 * q + g) * 2 + a, 2 * g + subnets[0], dst) for g in range(2)]
            for c, s in enumerate(subnets):
                passes.append(("v", (2 * q + s) * 2 + a, 4 + s, dst[:, c * P : (c + 1) * P]))
            for k, (kind, c, w, part) in enumerate(passes):
                codes, scales = quant[kind, i]
                cols = slice(w * P, w * P + (n if kind == "x" else P))
                nc.tensor.matmul_mx(
                    out=part,
                    lhsT=codes[:, c * P : (c + 1) * P].bitcast(X4),
                    lhsT_scale=scales[:, c * P : (c + 1) * P],
                    rhs=w1_codes[:, cols].bitcast(X4),
                    rhs_scale=w1_scales[W_SCALE_ROW:, cols],
                    start=(k == 0),
                    stop=(k == len(passes) - 1),
                )

        def out_view(i, q):
            rows = out_rows[:, row0[i] : row0[i + 1], :].rearrange("s (p n) f -> p s n f", p=P)
            return rows[:, :, 2 * q : 2 * q + 2, :]

        def finish(i, q):
            bank = new_bank()
            for a in range(2):
                second_product(bank[:, a * 256 : (a + 1) * 256], i, q, a, range(NS))
            res = stage.tile([P, 512], F32, name="res", bufs=4)
            nc.scalar.activation(
                out=res[:].rearrange("p (s a f) -> p s a f", s=2, a=2),
                in_=bank[:].rearrange("p (a s f) -> p s a f", s=2, a=2),
                func=ACT.Silu,
            )
            nc.sync.dma_start(
                out=out_view(i, q).rearrange("p s a f -> p s (a f)"),
                in_=res[:].rearrange("p (s c) -> p s c", s=2),
            )

        def finish_by_row_tile(i, q):
            for a in range(2):
                bank = new_bank()
                second_product(bank[:, :256], i, q, a, range(NS))
                res = stage.tile([P, 256], F32, name="res_rows", bufs=4)
                nc.scalar.activation(out=res[:], in_=bank[:, :256], func=ACT.Silu)
                nc.sync.dma_start(out=out_view(i, q)[:, :, a, :], in_=res[:].rearrange("p (s f) -> p s f", s=2))

        def finish_by_subnet(i, q):
            for s in range(NS):
                bank = new_bank()
                for a in range(2):
                    second_product(bank[:, a * P : (a + 1) * P], i, q, a, (s,))
                res = stage.tile([P, 256], F32, name="res_rows", bufs=4)
                nc.scalar.activation(out=res[:], in_=bank[:, :256], func=ACT.Silu)
                nc.sync.dma_start(out=out_view(i, q)[:, s].rearrange("p a f -> p (a f)"), in_=res[:])

        def passes_of(i):
            return [(q, g) for q in range(PAIRS[i]) for g in range(2)]

        with tc.manual_schedule():
            load_x(0)
            load_scale()
            load_wv(0, 0, 2)
            load_x(1)
            load_h(0)
            load_wv(0, 2, 2)
            for t in (0, 2):
                load_wv(1, t, 2)
            load_h(1)
            for s in range(NS):
                load_w1(s)
            load_h(2)
            load_x(2)

            widen_on_vector(0)
            widen_on_scalar(0, range(scalar_pieces(0)))
            spread_scale()
            widen_on_vector(1)
            for q, g in passes_of(0):
                turn_x(0, q, g)
            for t in range(2):
                turn_wv(0, t)
            for q, g in passes_of(0):
                turn_h(0, q, g)
            load_h(3)
            load_x(3)
            quant_wv(0, 0)
            quantise("h", 0)
            quant_wv(0, 1)
            for t in range(2, 4):
                turn_wv(0, t)
                quant_wv(0, t)
            for t in range(2):
                turn_wv(1, t)
            views(0, 0, 0)
            sort_words(nc.vector, wv_raw[1, 2], 4, shared[0])
            for t in range(2):
                quant_wv(1, t)
            sort_words(nc.vector, h_raw[1], 4, shared[0], 4)
            for s in range(NS):
                sort_words(nc.vector, w1_raw[s], 3, early, 2 + 3 * s)
            for t in range(2, 4):
                turn_wv(1, t)
            for q, g in passes_of(1):
                turn_h(1, q, g)
            for t in range(2, 4):
                quant_wv(1, t)
            for n in range(len(W1_BANKS)):
                turn_w1(n)
            sort_words(nc.vector, h_raw[2], 4, shared[0])
            widen_on_vector(2)
            quantise("h", 1)
            views(0, 0, 1)
            quantise("x", 0)
            quant_w1(0, 2)
            quant_w1(2, 3)
            widen_on_scalar(2, range(scalar_pieces(2)))

            for i in range(1, LAST):
                if i + 3 <= STEPS:
                    load_h(i + 3)
                if i + 3 < STEPS:
                    load_x(i + 3)
                if i == LAST_SHORT:
                    left = unsorted(i + 2) - SHORT_SORT
                    sort_words(nc.vector, h_raw[i + 2], left, early, 8 - left)
                quantise("v", i - 1, 2, (1, 0))
                most = SHORT_SORT if PAIRS[i] == 1 else unsorted(i + 2)
                sort_words(nc.gpsimd, h_raw[i + 2], most, shared[i % 2], 2 * PAIRS[i - 1])
                turn_run(i)
                x_banks.clear()
                x_banks.extend(by_age[-(PAIRS[i] + 1) :])
                if i > 1:
                    widen_on_vector(i + 1)
                for n in range(NS * PAIRS[i]):
                    wide = i == LAST - 1 and n < NS * PAIRS[i] - 1
                    (views_wide if wide else views)(i, *divmod(n, NS))
                quantise("h", i + 1)
                quantise("x", i)
                for q in range(PAIRS[i - 1]):
                    finish(i - 1, q)
                if i + 2 < STEPS:
                    widen_on_scalar(i + 2, range(AHEAD * (PAIRS[i] - 1), scalar_pieces(i + 2)))

            x_banks.clear()
            quantise("v", LAST - 1, 2, (0,))
            turn_run(LAST)
            quantise("v", LAST - 1, 2, (1,))
            views_wide(LAST, 0, 0)
            finish(LAST - 1, 0)
            views(LAST, 0, 1)
            quantise("x", LAST)
            finish_by_row_tile(LAST - 1, 1)
            quantise("v", LAST, 4)
            finish_by_subnet(LAST, 0)
